import numpy as np
import ml_dtypes


def mxq(x, axis, fmt="e4m3"):
    dtype, down = {"e4m3": (ml_dtypes.float8_e4m3fn, 7), "e5m2": (ml_dtypes.float8_e5m2, 14)}[fmt]
    v = np.moveaxis(np.asarray(x, np.float32).astype(ml_dtypes.bfloat16).astype(np.float64), axis, -1)
    blocks = v.reshape(v.shape[:-1] + (-1, 32))
    amax = np.abs(blocks).max(-1, keepdims=True)
    byte = np.maximum(np.where(amax > 0, np.frexp(amax)[1] - 1 + 127, 0) - down, 1)
    scale = np.exp2(byte - 127.0)
    codes = (blocks / scale).astype(np.float32).astype(dtype).astype(np.float64)
    return np.moveaxis((codes * scale).reshape(v.shape), -1, axis)


WIDE = False


def mx_kscale(k):
    if not WIDE:
        return np.ones(k)
    levels = np.array([10, -10, 5, -5, 0])
    if k % 512:
        return np.exp2(np.random.permutation(np.resize(levels, k // 32))).repeat(32)
    a = np.empty((k // 512, 16))
    for p in range(k // 512):
        a[p, :8] = np.random.permutation(np.resize(levels, 8))
        for g in range(8):
            far = levels[np.abs(levels - a[p, g]) >= 10]
            a[p, g + 8] = far[np.random.randint(len(far))]
    return np.exp2(a.ravel()).repeat(32)


BF16 = ml_dtypes.bfloat16


def bf(x):
    return np.asarray(x, np.float32).astype(BF16)


def f64(x):
    return np.asarray(x).astype(np.float64)


E2M1 = np.array([0.0, 0.5, 1.0, 1.5, 2.0, 3.0, 4.0, 6.0, -0.0, -0.5, -1.0, -1.5, -2.0, -3.0, -4.0, -6.0])


def pack_weight(w, fmt):
    k, n = w.shape
    w = f64(bf(w)).reshape(k // 32, 32, n)
    amax = np.abs(w).max(1)
    if fmt == "e4m3":
        byte = np.frexp(amax)[1] - 1 + 127 - 7
    else:
        mant, ex = np.frexp(amax / 6.0)
        byte = np.where(mant > 0.5, ex, ex - 1) + 127
    byte = np.clip(np.where(amax > 0, byte, 1), 1, 254)
    scaled = (w * np.exp2(127.0 - byte)[:, None, :]).reshape(k, n).astype(np.float32)
    by_word = np.ascontiguousarray(scaled.reshape(k // 512, 128, 4, n).transpose(0, 1, 3, 2))
    if fmt == "e4m3":
        words = by_word.astype(ml_dtypes.float8_e4m3fn).view(np.uint8)
    else:
        c = by_word.astype(ml_dtypes.float4_e2m1fn).view(np.uint8) & 0xF
        words = c[..., 0::2] | (c[..., 1::2] << 4)
    return np.ascontiguousarray(words), np.ascontiguousarray(byte.astype(np.uint8).reshape(k // 512, 16, n))


def unpack_weight(words, scales, fmt):
    g, p, n, _ = words.shape
    if fmt == "e4m3":
        vals = np.ascontiguousarray(words).view(ml_dtypes.float8_e4m3fn).astype(np.float64)
    else:
        nib = np.empty((g, p, n, 4), np.uint8)
        nib[..., 0::2] = words & 0xF
        nib[..., 1::2] = words >> 4
        vals = E2M1[nib]
    vals = vals * np.repeat(np.exp2(scales.astype(np.float64) - 127.0), 8, axis=1)[..., None]
    return vals.transpose(0, 1, 3, 2).reshape(g * 512, n)
def pack4(w):
    words, scales = pack_weight(w, "e2m1")
    return words.reshape(words.shape[0], 128, -1), scales


def unpack4(words, scales):
    return unpack_weight(words.reshape(words.shape[0], 128, -1, 2), scales, "e2m1")


N, E, HD, H1, H3, DM = 1024, 8192, 256, 1024, 128, 1024
C = 2 * HD


def draw0():
    s = mx_kscale(N)
    t = mx_kscale(C)
    r = np.concatenate([np.full(HD, 2.0 / np.sqrt(HD)), np.full(HD, 8.0 / np.sqrt(N * HD))])
    H_A = bf(np.random.standard_normal((N, E)) * 0.25 * s[:, None])
    H_mean_A = bf(np.random.standard_normal((N, HD)) * 0.35 / s[:, None] * t[HD:])
    H_mean_M = bf(np.random.standard_normal((E, HD)) * 0.35 * t[:HD])
    words, scales = pack4(np.random.standard_normal((C, H3)) * (r / t)[:, None])
    return {
        "H_A": H_A,
        "H_mean_A": H_mean_A,
        "H_mean_M": H_mean_M,
        "wEA1_words": words,
        "wEA1_scales": scales,
        "bEA1": bf(np.random.standard_normal(H3) * 0.1),
    }


def core(H_A, H_mean_A, H_mean_M, wEA1_words, wEA1_scales, bEA1):
    sum_A = mxq(f64(H_A), 0, "e4m3").T @ mxq(f64(H_mean_A), 0, "e4m3")
    EventA = np.concatenate([f64(H_mean_M), sum_A], axis=1)
    return np.maximum((mxq(EventA, 1, "e4m3") @ unpack4(wEA1_words, wEA1_scales)) + f64(bEA1), 0.0)


def e4m3fn_bytes(y):
    return np.clip(np.asarray(y, np.float64), -448.0, 448.0).astype(np.float32).astype(ml_dtypes.float8_e4m3fn).view(np.uint8)


def e4m3fn_values(b):
    return np.asarray(b, np.uint8).view(ml_dtypes.float8_e4m3fn).astype(np.float64)


def setup_inputs():
    d = draw0()
    x0 = np.asarray(d['H_A']).astype(np.float64)
    s = (np.max(np.abs(x0), axis=(1,), keepdims=True) / 448.0).astype(np.float32)
    out = {}
    for k, v in d.items():
        if k == 'H_A':
            out['H_A_bytes'] = e4m3fn_bytes(x0 / s.astype(np.float64))
            out['H_A_scale'] = s
        else:
            out[k] = v
    return out


def reference(H_A_bytes, H_A_scale, H_mean_A, H_mean_M, wEA1_words, wEA1_scales, bEA1):
    return core(e4m3fn_values(H_A_bytes) * H_A_scale.astype(np.float64), H_mean_A, H_mean_M, wEA1_words, wEA1_scales, bEA1)

@@ -1,0 +1,334 @@
+from contextlib import ExitStack
+
+import concourse.mybir as mybir
+from concourse.masks import make_identity
+
+F32 = mybir.dt.float32
+BF16 = mybir.dt.bfloat16
+U32 = mybir.dt.uint32
+I32 = mybir.dt.int32
+U8 = mybir.dt.uint8
+FP8 = mybir.dt.float8_e4m3fn
+FP8X4 = mybir.dt.float8_e4m3fn_x4
+FP4X4 = mybir.dt.float4_e2m1fn_x4
+ALU = mybir.AluOpType
+COPY = mybir.ActivationFunctionType.Copy
+RELU = mybir.ActivationFunctionType.Relu
+
+NODES, EVENTS, HIDDEN, OUT = 1024, 8192, 256, 128
+
+P = 128
+PACK = 4
+PASS = P * PACK
+GROUPS = NODES // PASS
+PAIR = 2 * P
+QUADS = HIDDEN // PACK
+BANK = 512
+PLANES = GROUPS * PACK
+
+CHUNKS = (256, 512, 1024, 1024, 1024, 1024, 1024, 1024, 512, 512, 256)
+VECTOR_PLANES = (5, 2, 3, 3, 4, 4, 4, 3, 1, 4, 0)
+FIRST_DIRECT = 7
+AHEAD = 4
+
+FLOPS = 2 * NODES * EVENTS * HIDDEN + 2 * EVENTS * 2 * HIDDEN * OUT
+
+
+def tile_mymodel_icdm_pa_t_w4_kernel(
+    tc, H_A_bytes, H_A_scale, H_mean_A, H_mean_M, wEA1_words, wEA1_scales, bEA1, out
+):
+    nc = tc.nc
+    n_chunks = len(CHUNKS)
+    first_event = [sum(CHUNKS[:c]) for c in range(n_chunks)]
+
+    with ExitStack() as ctx:
+        keep = ctx.enter_context(tc.tile_pool(name="keep", bufs=1))
+        work = ctx.enter_context(tc.tile_pool(name="work", bufs=2))
+        psum = ctx.enter_context(tc.psum_pool(name="psum", bufs=2))
+        ctx.enter_context(tc.manual_schedule(engines={mybir.EngineType.SP}))
+
+        warm = keep.tile([P, 1], F32, name="warm")
+        nc.vector.memset(warm[:], 0.0)
+        nc.scalar.activation(out=warm[:], in_=warm[:], func=COPY)
+
+
+        n_blocks = 2 * PLANES + 1
+        node_codes = keep.tile([P, n_blocks * QUADS], U32, name="node_codes", align_bytes=64)
+        node_scales = keep.tile([P, n_blocks * QUADS], U8, name="node_scales", align_bytes=64)
+        nc.vector.memset(node_codes[:], 0)
+        nc.vector.memset(node_scales[:].bitcast(I32), 0)
+
+        weight = keep.tile([P, 4, 2 * OUT], U8, name="weight", align_bytes=64)
+        weight_scales = keep.tile([P, 4, OUT], U8, name="weight_scales", align_bytes=64)
+        nc.vector.memset(weight[:].rearrange("p v b -> p (v b)").bitcast(I32), 0)
+        nc.vector.memset(weight_scales[:].rearrange("p v n -> p (v n)").bitcast(I32), 0)
+
+        bias_in = keep.tile([P, 1], BF16, name="bias_in")
+        bias_column = keep.tile([P, 1], F32, name="bias_column")
+        bias_row = keep.tile([P, OUT], BF16, name="bias_row")
+        bias_spread = keep.tile([P, BANK // OUT, OUT], F32, name="bias_spread")
+        ones = keep.tile([P, P], BF16, name="ones")
+        nc.vector.memset(bias_row[:], 0.0)
+        nc.vector.memset(ones[:], 1.0)
+        identity = keep.tile([P, P], F32, name="identity")
+        make_identity(nc, identity[:])
+
+
+        plane_scales = keep.tile([P, GROUPS, PACK], F32, name="plane_scales")
+        nc.sync.dma_start(out=plane_scales[:], in_=H_A_scale.rearrange("(g p t) o -> p g (t o)", p=P, t=PACK))
+
+        event_bytes = {}
+        event_rows = {}
+
+        def load_bytes(c):
+            events = slice(first_event[c], first_event[c] + CHUNKS[c])
+            for g in range(GROUPS):
+                raw = keep.tile([P, PACK, CHUNKS[c]], U8, name="bytes_%d_%d" % (c, g), align_bytes=64)
+                event_bytes[c, g] = raw
+                nodes = slice(PASS * g, PASS * (g + 1))
+                nc.sync.dma_start(out=raw[:], in_=H_A_bytes[nodes, events].rearrange("(p t) e -> p t e", t=PACK))
+
+        def load_rows(c):
+            events = slice(first_event[c], first_event[c] + CHUNKS[c])
+            rows = keep.tile([P, CHUNKS[c] // P, HIDDEN], BF16, name="rows_%d" % c, align_bytes=64)
+            event_rows[c] = rows
+            nc.sync.dma_start(out=rows[:], in_=H_mean_M[events, :].rearrange("(r i) k -> i r k", i=P))
+
+        load_bytes(0)
+        load_bytes(1)
+        nc.sync.dma_start(out=bias_in[:], in_=bEA1.rearrange("(c o) -> c o", o=1))
+        nc.sync.dma_start(out=bias_row[0:1, :], in_=bEA1.rearrange("(o c) -> o c", o=1))
+        node_rows = keep.tile([P, GROUPS, PACK, HIDDEN], BF16, name="node_rows", align_bytes=64)
+        for g in range(GROUPS):
+            nodes = slice(PASS * g, PASS * (g + 1))
+            nc.sync.dma_start(out=node_rows[:, g], in_=H_mean_A[nodes, :].rearrange("(p j) c -> p j c", j=PACK))
+        load_rows(0)
+        load_bytes(2)
+        load_rows(1)
+        load_bytes(3)
+        load_rows(2)
+        word_halves = wEA1_words[0].rearrange("(h p) b -> p h b", h=2).bitcast(I32)
+        scale_quadrants = wEA1_scales[0].rearrange("(h r b) n -> r b h n", h=2, r=2)
+        for side in range(2):
+            forms = slice(2 * side, 2 * side + 2)
+            nc.sync.dma_start(out=weight[QUADS * side : QUADS * (side + 1), forms, :].bitcast(I32), in_=word_halves)
+        for quadrant in range(4):
+            side, r = divmod(quadrant, 2)
+            forms = slice(2 * side, 2 * side + 2)
+            nc.sync.dma_start(
+                out=weight_scales[32 * quadrant : 32 * quadrant + 4, forms, :].bitcast(I32),
+                in_=scale_quadrants[r].bitcast(I32),
+            )
+        load_rows(3)
+
+
+        def spread_bias():
+            po = psum.tile([P, BANK // OUT, OUT], F32, name="po", bufs=2)
+            for i in range(BANK // OUT):
+                nc.tensor.matmul(out=po[:, i, :], lhsT=ones[:], rhs=bias_row[:], start=True, stop=True)
+            nc.scalar.copy(out=bias_spread[:], in_=po[:])
+            nc.scalar.copy(out=bias_column[:], in_=bias_in[:])
+
+        def quantize_nodes():
+            grouped = keep.tile([P, GROUPS, PACK, QUADS, PACK], BF16, name="node_grouped", align_bytes=64)
+            for g in range(GROUPS):
+                nc.vector.tensor_copy(out=grouped[:, g], in_=node_rows[:, g].rearrange("p j (q t) -> p t q j", t=PACK))
+            for g in range(GROUPS):
+                for t in range(PACK):
+                    c0 = (2 * (PACK * g + t) + 1) * QUADS
+                    nc.vector.quantize_mx(
+                        out=node_codes[:, c0 : c0 + QUADS].bitcast(FP8X4),
+                        scales=node_scales[:, c0 : c0 + QUADS],
+                        in_=grouped[:, g, t].rearrange("p q j -> p (q j)"),
+                    )
+
+
+        wide, h_grouped, h_codes, h_scales = {}, {}, {}, {}
+        m_grouped, m_codes, m_scales = {}, {}, {}
+        a_grouped, a_codes, a_scales = {}, {}, {}
+        results = {}
+
+        def widen(c, plane):
+            g, t = divmod(plane, PACK)
+            if t == 0:
+                planes = work.tile([P, PACK, CHUNKS[c]], BF16, name="wide", bufs=4, align_bytes=64)
+                wide[c, g] = planes
+            values = event_bytes[c, g][:, t, :].bitcast(FP8)
+            scale = plane_scales[:, g, t : t + 1]
+            if plane < PLANES - VECTOR_PLANES[c]:
+                nc.scalar.activation(out=wide[c, g][:, t, :], in_=values, func=COPY, scale=scale)
+            else:
+                nc.vector.tensor_scalar(
+                    out=wide[c, g][:, t, :], in0=values, scalar1=scale, scalar2=None, op0=ALU.mult
+                )
+
+        def interleave(c, g):
+            grouped = work.tile([P, PACK * CHUNKS[c]], BF16, name="h_grouped", bufs=3, align_bytes=64)
+            h_grouped[c, g] = grouped
+            nc.vector.tensor_copy(
+                out=grouped[:].rearrange("p (e i t) -> p e t i", i=4, t=PACK),
+                in_=wide[c, g][:].rearrange("p t (e i) -> p e t i", i=4),
+            )
+
+        def quantize_events(c, g):
+            if g == 0:
+                codes = work.tile([P, GROUPS, CHUNKS[c]], U32, name="h_codes", bufs=2, align_bytes=64)
+                scales = work.tile([P, GROUPS, CHUNKS[c]], U8, name="h_scales", bufs=2, align_bytes=64)
+                h_codes[c], h_scales[c] = codes, scales
+            nc.vector.quantize_mx(
+                out=h_codes[c][:, g, :].bitcast(FP8X4), scales=h_scales[c][:, g, :], in_=h_grouped[c, g][:]
+            )
+
+        def pool_nodes(c, j):
+            ps = psum.tile([P, PACK, P], F32, name="ps", bufs=2)
+            for t in range(PACK):
+                for side in range(2):
+                    cols = slice(PAIR * j + P * side, PAIR * j + P * (side + 1))
+                    for g in range(GROUPS):
+                        c0 = (2 * (PACK * g + t) + 1 - side) * QUADS
+                        nc.tensor.matmul_mx(
+                            out=ps[:, t, :],
+                            lhsT=node_codes[:, c0 : c0 + P].bitcast(FP8X4),
+                            lhsT_scale=node_scales[:, c0 : c0 + P],
+                            rhs=h_codes[c][:, g, cols].bitcast(FP8X4),
+                            rhs_scale=h_scales[c][:, g, cols],
+                            start=(side == 0 and g == 0),
+                            stop=(side == 1 and g == GROUPS - 1),
+                        )
+            return ps
+
+        def empty_sums(c, j, ps):
+            if j == 0:
+                grouped = work.tile([P, PACK * CHUNKS[c] // 2], BF16, name="a_grouped", bufs=2, align_bytes=64)
+                a_grouped[c] = grouped
+            nc.scalar.copy(
+                out=a_grouped[c][:, BANK * j : BANK * (j + 1)].rearrange("p (n t) -> p n t", t=PACK),
+                in_=ps[:].rearrange("p t n -> p n t"),
+            )
+
+        def turn_rows(c, b):
+            n_pairs = min(2, CHUNKS[c] // PAIR - 2 * b)
+            if b == 0:
+                grouped = work.tile([P, PACK * CHUNKS[c] // 2], BF16, name="m_grouped", bufs=2, align_bytes=64)
+                m_grouped[c] = grouped
+            words = event_rows[c][:].rearrange("p r k -> p (r k)").bitcast(F32)
+            pt = psum.tile([P, n_pairs, 2, P], F32, name="pt", bufs=2)
+            for j in range(n_pairs):
+                w0 = HIDDEN * (2 * b + j)
+                for u in range(2):
+                    nc.tensor.transpose(pt[:, j, u, :], words[:, w0 + u : w0 + HIDDEN : 2], identity[:])
+            nc.scalar.copy(
+                out=m_grouped[c][:]
+                .bitcast(F32)[:, BANK * b : BANK * b + HIDDEN * n_pairs]
+                .rearrange("p (j n u) -> p j n u", n=P, u=2),
+                in_=pt[:].rearrange("p j u n -> p j n u"),
+            )
+
+        def quantize_rows(c):
+            codes = work.tile([P, CHUNKS[c] // 2], U32, name="m_codes", bufs=3, align_bytes=64)
+            scales = work.tile([P, CHUNKS[c] // 2], U8, name="m_scales", bufs=3, align_bytes=64)
+            m_codes[c], m_scales[c] = codes, scales
+            nc.vector.quantize_mx(out=codes[:].bitcast(FP8X4), scales=scales[:], in_=m_grouped[c][:])
+
+        def quantize_sums(c):
+            codes = work.tile([P, CHUNKS[c] // 2], U32, name="a_codes", bufs=2, align_bytes=64)
+            scales = work.tile([P, CHUNKS[c] // 2], U8, name="a_scales", bufs=2, align_bytes=64)
+            a_codes[c], a_scales[c] = codes, scales
+            nc.vector.quantize_mx(out=codes[:].bitcast(FP8X4), scales=scales[:], in_=a_grouped[c][:])
+
+        def halves(c):
+            return ((0, m_codes[c], m_scales[c]), (1, a_codes[c], a_scales[c]))
+
+        def new_result(c):
+            result = work.tile([P, CHUNKS[c] // P, OUT], F32, name="result", bufs=3)
+            results[c] = result
+
+        def finish_direct(c):
+            new_result(c)
+            n_sets = CHUNKS[c] // P
+            for r0 in range(0, n_sets, BANK // OUT):
+                n = min(BANK // OUT, n_sets - r0)
+                po = psum.tile([P, n, OUT], F32, name="po", bufs=2)
+                for i in range(n):
+                    pair, side = divmod(r0 + i, 2)
+                    cols = slice(P * pair, P * (pair + 1))
+                    for half, codes, scales in halves(c):
+                        nc.tensor.matmul_mx(
+                            out=po[:, i, :],
+                            lhsT=codes[:, cols].bitcast(FP8X4),
+                            lhsT_scale=scales[:, cols],
+                            rhs=weight[:, 2 * side + half, :].bitcast(FP4X4),
+                            rhs_scale=weight_scales[:, 2 * side + half, :],
+                            start=(half == 0),
+                            stop=(half == 1),
+                        )
+                nc.vector.tensor_tensor(
+                    out=results[c][:, r0 : r0 + n, :], in0=po[:], in1=bias_spread[:, 0:n, :], op=ALU.add
+                )
+            nc.vector.tensor_scalar(out=results[c][:], in0=results[c][:], scalar1=0.0, scalar2=None, op0=ALU.max)
+
+        def finish_turned(c):
+            n = CHUNKS[c] // 2
+            width = BANK if n == BANK else P
+            turned = []
+            for side in range(2):
+                po = psum.tile([P, n], F32, name="po", bufs=2)
+                for c0 in range(0, n, width):
+                    cols = slice(c0, c0 + width)
+                    for half, codes, scales in halves(c):
+                        nc.tensor.matmul_mx(
+                            out=po[:, cols],
+                            lhsT=weight[:, 2 * side + half, :].bitcast(FP4X4),
+                            lhsT_scale=weight_scales[:, 2 * side + half, :],
+                            rhs=codes[:, cols].bitcast(FP8X4),
+                            rhs_scale=scales[:, cols],
+                            start=(half == 0),
+                            stop=(half == 1),
+                        )
+                channels = work.tile([P, n], F32, name="channels", bufs=2)
+                nc.scalar.activation(out=channels[:], in_=po[:], func=RELU, bias=bias_column[:])
+                turned.append(channels)
+            new_result(c)
+            for side in range(2):
+                pz = psum.tile([P, n // P, OUT], F32, name="pz", bufs=2)
+                for j in range(n // P):
+                    nc.tensor.transpose(pz[:, j, :], turned[side][:, P * j : P * (j + 1)], identity[:])
+                nc.scalar.copy(out=results[c][:, side::2, :], in_=pz[:])
+
+        def store(c):
+            events = slice(first_event[c], first_event[c] + CHUNKS[c])
+            nc.sync.dma_start(out=out[events, :].rearrange("(r i) k -> i r k", i=P), in_=results[c][:])
+
+
+        for step in range(-1, n_chunks + 2):
+            to_widen, to_quantize, to_pool, to_finish = step + 1, step, step - 1, step - 2
+            if 0 <= step < n_chunks - AHEAD:
+                load_bytes(step + AHEAD)
+                load_rows(step + AHEAD)
+            if step == 0:
+                quantize_nodes()
+            if step == 1:
+                spread_bias()
+            if 0 <= to_finish < n_chunks:
+                quantize_rows(to_finish)
+                quantize_sums(to_finish)
+            if 0 <= to_quantize < n_chunks:
+                for g in range(GROUPS):
+                    interleave(to_quantize, g)
+                for g in range(GROUPS):
+                    quantize_events(to_quantize, g)
+            if 0 <= to_pool < n_chunks:
+                for j in range(CHUNKS[to_pool] // PAIR):
+                    empty_sums(to_pool, j, pool_nodes(to_pool, j))
+            if 0 <= to_finish < n_chunks:
+                if to_finish < FIRST_DIRECT:
+                    finish_turned(to_finish)
+                else:
+                    finish_direct(to_finish)
+                store(to_finish)
+            if to_widen < n_chunks:
+                for plane in range(PLANES):
+                    widen(to_widen, plane)
+            if 0 <= to_quantize < n_chunks:
+                for b in range((CHUNKS[to_quantize] + 2 * PAIR - 1) // (2 * PAIR)):
+                    turn_rows(to_quantize, b)

@@ -26,12 +26,25 @@ QUADS = HIDDEN // PACK
 BANK = 512
 PLANES = GROUPS * PACK
 
-CHUNKS = (256, 512, 1024, 1024, 1024, 1024, 1024, 1024, 512, 512, 256)
-VECTOR_PLANES = (5, 2, 3, 3, 4, 4, 4, 3, 1, 4, 0)
-FIRST_DIRECT = 7
-AHEAD = 4
+CHUNKS = (2 * PAIR,) * 15 + (PAIR,) * 2
+LOADS = (512, 512, 1024, 1024, 1024, 2048, 2048)
+DIRECT = 3
 
 FLOPS = 2 * NODES * EVENTS * HIDDEN + 2 * EVENTS * 2 * HIDDEN * OUT
+
+
+def scalar_planes(c):
+    if c == 0:
+        return (0, PACK)
+    if c == 1:
+        return range(PLANES)
+    if c == 2:
+        return range(6)
+    if c == 3:
+        return range(5)
+    if c >= len(CHUNKS) - 2:
+        return range(5)
+    return range(PACK)
 
 
 def tile_mymodel_icdm_pa_t_w4_kernel(
@@ -40,16 +53,13 @@ def tile_mymodel_icdm_pa_t_w4_kernel(
     nc = tc.nc
     n_chunks = len(CHUNKS)
     first_event = [sum(CHUNKS[:c]) for c in range(n_chunks)]
+    load_start = [sum(LOADS[:i]) for i in range(len(LOADS))]
 
     with ExitStack() as ctx:
         keep = ctx.enter_context(tc.tile_pool(name="keep", bufs=1))
         work = ctx.enter_context(tc.tile_pool(name="work", bufs=2))
         psum = ctx.enter_context(tc.psum_pool(name="psum", bufs=2))
-        ctx.enter_context(tc.manual_schedule(engines={mybir.EngineType.SP}))
-
-        warm = keep.tile([P, 1], F32, name="warm")
-        nc.vector.memset(warm[:], 0.0)
-        nc.scalar.activation(out=warm[:], in_=warm[:], func=COPY)
+        ctx.enter_context(tc.manual_schedule())
 
 
         n_blocks = 2 * PLANES + 1
@@ -63,13 +73,8 @@ def tile_mymodel_icdm_pa_t_w4_kernel(
         nc.vector.memset(weight[:].rearrange("p v b -> p (v b)").bitcast(I32), 0)
         nc.vector.memset(weight_scales[:].rearrange("p v n -> p (v n)").bitcast(I32), 0)
 
-        bias_in = keep.tile([P, 1], BF16, name="bias_in")
-        bias_column = keep.tile([P, 1], F32, name="bias_column")
-        bias_row = keep.tile([P, OUT], BF16, name="bias_row")
-        bias_spread = keep.tile([P, BANK // OUT, OUT], F32, name="bias_spread")
-        ones = keep.tile([P, P], BF16, name="ones")
-        nc.vector.memset(bias_row[:], 0.0)
-        nc.vector.memset(ones[:], 1.0)
+        bias_column = keep.tile([P, 1], BF16, name="bias_column")
+        bias_rows = keep.tile([P, 1, OUT], BF16, name="bias_rows")
         identity = keep.tile([P, P], F32, name="identity")
         make_identity(nc, identity[:])
 
@@ -80,33 +85,32 @@ def tile_mymodel_icdm_pa_t_w4_kernel(
         event_bytes = {}
         event_rows = {}
 
-        def load_bytes(c):
-            events = slice(first_event[c], first_event[c] + CHUNKS[c])
+        def load_bytes(i):
+            events = slice(load_start[i], load_start[i] + LOADS[i])
             for g in range(GROUPS):
-                raw = keep.tile([P, PACK, CHUNKS[c]], U8, name="bytes_%d_%d" % (c, g), align_bytes=64)
-                event_bytes[c, g] = raw
+                raw = keep.tile([P, PACK, LOADS[i]], U8, name="bytes_%d_%d" % (i, g), align_bytes=64)
+                event_bytes[i, g] = raw
                 nodes = slice(PASS * g, PASS * (g + 1))
                 nc.sync.dma_start(out=raw[:], in_=H_A_bytes[nodes, events].rearrange("(p t) e -> p t e", t=PACK))
 
-        def load_rows(c):
-            events = slice(first_event[c], first_event[c] + CHUNKS[c])
-            rows = keep.tile([P, CHUNKS[c] // P, HIDDEN], BF16, name="rows_%d" % c, align_bytes=64)
-            event_rows[c] = rows
+        def load_rows(i):
+            events = slice(load_start[i], load_start[i] + LOADS[i])
+            rows = keep.tile([P, LOADS[i] // P, HIDDEN], BF16, name="rows_%d" % i, align_bytes=64)
+            event_rows[i] = rows
             nc.sync.dma_start(out=rows[:], in_=H_mean_M[events, :].rearrange("(r i) k -> i r k", i=P))
+
+        def place(c):
+            i = max(i for i in range(len(LOADS)) if load_start[i] <= first_event[c])
+            return i, first_event[c] - load_start[i]
 
         load_bytes(0)
         load_bytes(1)
-        nc.sync.dma_start(out=bias_in[:], in_=bEA1.rearrange("(c o) -> c o", o=1))
-        nc.sync.dma_start(out=bias_row[0:1, :], in_=bEA1.rearrange("(o c) -> o c", o=1))
         node_rows = keep.tile([P, GROUPS, PACK, HIDDEN], BF16, name="node_rows", align_bytes=64)
-        for g in range(GROUPS):
-            nodes = slice(PASS * g, PASS * (g + 1))
-            nc.sync.dma_start(out=node_rows[:, g], in_=H_mean_A[nodes, :].rearrange("(p j) c -> p j c", j=PACK))
+        nc.sync.dma_start(out=node_rows[:], in_=H_mean_A.rearrange("(g p j) c -> p g j c", p=P, j=PACK))
         load_rows(0)
         load_bytes(2)
         load_rows(1)
         load_bytes(3)
-        load_rows(2)
         word_halves = wEA1_words[0].rearrange("(h p) b -> p h b", h=2).bitcast(I32)
         scale_quadrants = wEA1_scales[0].rearrange("(h r b) n -> r b h n", h=2, r=2)
         for side in range(2):
@@ -119,15 +123,13 @@ def tile_mymodel_icdm_pa_t_w4_kernel(
                 out=weight_scales[32 * quadrant : 32 * quadrant + 4, forms, :].bitcast(I32),
                 in_=scale_quadrants[r].bitcast(I32),
             )
+        nc.sync.dma_start(out=bias_column[:], in_=bEA1.rearrange("(c o) -> c o", o=1))
+        load_rows(2)
         load_rows(3)
-
-
-        def spread_bias():
-            po = psum.tile([P, BANK // OUT, OUT], F32, name="po", bufs=2)
-            for i in range(BANK // OUT):
-                nc.tensor.matmul(out=po[:, i, :], lhsT=ones[:], rhs=bias_row[:], start=True, stop=True)
-            nc.scalar.copy(out=bias_spread[:], in_=po[:])
-            nc.scalar.copy(out=bias_column[:], in_=bias_in[:])
+        for i in range(4, len(LOADS)):
+            load_bytes(i)
+            load_rows(i)
+        nc.sync.dma_start(out=bias_rows[:, 0, :], in_=bEA1.partition_broadcast(P))
 
         def quantize_nodes():
             grouped = keep.tile([P, GROUPS, PACK, QUADS, PACK], BF16, name="node_grouped", align_bytes=64)
@@ -144,191 +146,244 @@ def tile_mymodel_icdm_pa_t_w4_kernel(
 
 
         wide, h_grouped, h_codes, h_scales = {}, {}, {}, {}
-        m_grouped, m_codes, m_scales = {}, {}, {}
-        a_grouped, a_codes, a_scales = {}, {}, {}
-        results = {}
+        sums, turned_rows, e_grouped, e_codes, e_scales = {}, {}, {}, {}, {}
+        products, channels, turned_channels, results = {}, {}, {}, {}
+
+        def exists(c, j=0):
+            return 0 <= c < n_chunks and PAIR * j < CHUNKS[c]
 
         def widen(c, plane):
             g, t = divmod(plane, PACK)
-            if t == 0:
-                planes = work.tile([P, PACK, CHUNKS[c]], BF16, name="wide", bufs=4, align_bytes=64)
+            if (c, g) not in wide:
+                planes = work.tile([P, PACK, CHUNKS[c]], BF16, name="wide", bufs=6, align_bytes=64)
                 wide[c, g] = planes
-            values = event_bytes[c, g][:, t, :].bitcast(FP8)
+            i, e0 = place(c)
+            values = event_bytes[i, g][:, t, e0 : e0 + CHUNKS[c]].bitcast(FP8)
             scale = plane_scales[:, g, t : t + 1]
-            if plane < PLANES - VECTOR_PLANES[c]:
+            if plane in scalar_planes(c):
                 nc.scalar.activation(out=wide[c, g][:, t, :], in_=values, func=COPY, scale=scale)
             else:
                 nc.vector.tensor_scalar(
                     out=wide[c, g][:, t, :], in0=values, scalar1=scale, scalar2=None, op0=ALU.mult
                 )
 
+        def widen_scalar(c, quarter):
+            if exists(c):
+                planes = scalar_planes(c)
+                for plane in planes[len(planes) * quarter // 4 : len(planes) * (quarter + 1) // 4]:
+                    widen(c, plane)
+
+        def widen_vector(c, quarter):
+            if exists(c):
+                planes = [plane for plane in range(PLANES) if plane not in scalar_planes(c)]
+                for plane in planes[len(planes) * quarter // 4 : len(planes) * (quarter + 1) // 4]:
+                    widen(c, plane)
+
         def interleave(c, g):
-            grouped = work.tile([P, PACK * CHUNKS[c]], BF16, name="h_grouped", bufs=3, align_bytes=64)
-            h_grouped[c, g] = grouped
-            nc.vector.tensor_copy(
-                out=grouped[:].rearrange("p (e i t) -> p e t i", i=4, t=PACK),
-                in_=wide[c, g][:].rearrange("p t (e i) -> p e t i", i=4),
-            )
+            if exists(c):
+                grouped = work.tile([P, PACK * CHUNKS[c]], BF16, name="h_grouped", bufs=3, align_bytes=64)
+                h_grouped[c, g] = grouped
+                nc.vector.tensor_copy(
+                    out=grouped[:].rearrange("p (e i t) -> p e t i", i=4, t=PACK),
+                    in_=wide[c, g][:].rearrange("p t (e i) -> p e t i", i=4),
+                )
 
         def quantize_events(c, g):
-            if g == 0:
-                codes = work.tile([P, GROUPS, CHUNKS[c]], U32, name="h_codes", bufs=2, align_bytes=64)
-                scales = work.tile([P, GROUPS, CHUNKS[c]], U8, name="h_scales", bufs=2, align_bytes=64)
-                h_codes[c], h_scales[c] = codes, scales
-            nc.vector.quantize_mx(
-                out=h_codes[c][:, g, :].bitcast(FP8X4), scales=h_scales[c][:, g, :], in_=h_grouped[c, g][:]
-            )
+            if exists(c):
+                codes = work.tile([P, CHUNKS[c]], U32, name="h_codes", bufs=6, align_bytes=64)
+                scales = work.tile([P, CHUNKS[c]], U8, name="h_scales", bufs=6, align_bytes=64)
+                h_codes[c, g], h_scales[c, g] = codes, scales
+                nc.vector.quantize_mx(out=codes[:].bitcast(FP8X4), scales=scales[:], in_=h_grouped[c, g][:])
 
         def pool_nodes(c, j):
-            ps = psum.tile([P, PACK, P], F32, name="ps", bufs=2)
-            for t in range(PACK):
-                for side in range(2):
-                    cols = slice(PAIR * j + P * side, PAIR * j + P * (side + 1))
-                    for g in range(GROUPS):
-                        c0 = (2 * (PACK * g + t) + 1 - side) * QUADS
+            if exists(c, j):
+                ps = psum.tile([P, PACK, P], F32, name="ps", bufs=3)
+                sums[c, j] = ps
+                for g in (1, 0):
+                    for t in range(PACK):
+                        for side in range(2):
+                            cols = slice(PAIR * j + P * side, PAIR * j + P * (side + 1))
+                            c0 = (2 * (PACK * g + t) + 1 - side) * QUADS
+                            nc.tensor.matmul_mx(
+                                out=ps[:, t, :],
+                                lhsT=node_codes[:, c0 : c0 + P].bitcast(FP8X4),
+                                lhsT_scale=node_scales[:, c0 : c0 + P],
+                                rhs=h_codes[c, g][:, cols].bitcast(FP8X4),
+                                rhs_scale=h_scales[c, g][:, cols],
+                                start=(g == 1 and t == 0 and side == 0),
+                                stop=(g == 0 and t == PACK - 1 and side == 1),
+                            )
+
+        def event_features(c):
+            if c not in e_grouped:
+                grouped = work.tile([P, 2, PACK * CHUNKS[c] // 2], BF16, name="e_grouped", bufs=3, align_bytes=64)
+                e_grouped[c] = grouped
+            return e_grouped[c]
+
+        def empty_sums(c, j):
+            if exists(c, j):
+                nc.scalar.copy(
+                    out=event_features(c)[:, 1, BANK * j : BANK * (j + 1)].rearrange("p (n t) -> p n t", t=PACK),
+                    in_=sums[c, j][:].rearrange("p t n -> p n t"),
+                )
+
+        def turn_rows(c):
+            if exists(c):
+                i, e0 = place(c)
+                words = event_rows[i][:].rearrange("p r k -> p (r k)").bitcast(F32)
+                pt = psum.tile([P, CHUNKS[c] // PAIR, 2, P], F32, name="pt", bufs=2)
+                turned_rows[c] = pt
+                for j in range(CHUNKS[c] // PAIR):
+                    w0 = e0 + HIDDEN * j
+                    for u in range(2):
+                        nc.tensor.transpose(pt[:, j, u, :], words[:, w0 + u : w0 + HIDDEN : 2], identity[:])
+
+        def empty_rows(c):
+            if exists(c):
+                nc.scalar.copy(
+                    out=event_features(c)[:, 0, :].bitcast(F32).rearrange("p (j n u) -> p j n u", n=P, u=2),
+                    in_=turned_rows[c][:].rearrange("p j u n -> p j n u"),
+                )
+
+        def quantize_features(c):
+            if exists(c):
+                codes = work.tile([P, CHUNKS[c]], U32, name="e_codes", bufs=3, align_bytes=64)
+                scales = work.tile([P, CHUNKS[c]], U8, name="e_scales", bufs=3, align_bytes=64)
+                e_codes[c], e_scales[c] = codes, scales
+                nc.vector.quantize_mx(
+                    out=codes[:].bitcast(FP8X4), scales=scales[:], in_=e_grouped[c][:].rearrange("p h n -> p (h n)")
+                )
+
+        def project(c):
+            if exists(c):
+                po = psum.tile([P, CHUNKS[c] // P, OUT], F32, name="po", bufs=2)
+                products[c] = po
+                for r in range(CHUNKS[c] // P):
+                    j, side = divmod(r, 2)
+                    for half in range(2):
+                        c0 = half * CHUNKS[c] // 2 + P * j
+                        events = e_codes[c][:, c0 : c0 + P].bitcast(FP8X4), e_scales[c][:, c0 : c0 + P]
+                        form = weight[:, 2 * side + half, :].bitcast(FP4X4), weight_scales[:, 2 * side + half, :]
+                        still, moving = (events, form) if c >= n_chunks - DIRECT else (form, events)
                         nc.tensor.matmul_mx(
-                            out=ps[:, t, :],
-                            lhsT=node_codes[:, c0 : c0 + P].bitcast(FP8X4),
-                            lhsT_scale=node_scales[:, c0 : c0 + P],
-                            rhs=h_codes[c][:, g, cols].bitcast(FP8X4),
-                            rhs_scale=h_scales[c][:, g, cols],
-                            start=(side == 0 and g == 0),
-                            stop=(side == 1 and g == GROUPS - 1),
+                            out=po[:, r, :],
+                            lhsT=still[0],
+                            lhsT_scale=still[1],
+                            rhs=moving[0],
+                            rhs_scale=moving[1],
+                            start=(half == 0),
+                            stop=(half == 1),
                         )
-            return ps
-
-        def empty_sums(c, j, ps):
-            if j == 0:
-                grouped = work.tile([P, PACK * CHUNKS[c] // 2], BF16, name="a_grouped", bufs=2, align_bytes=64)
-                a_grouped[c] = grouped
-            nc.scalar.copy(
-                out=a_grouped[c][:, BANK * j : BANK * (j + 1)].rearrange("p (n t) -> p n t", t=PACK),
-                in_=ps[:].rearrange("p t n -> p n t"),
-            )
-
-        def turn_rows(c, b):
-            n_pairs = min(2, CHUNKS[c] // PAIR - 2 * b)
-            if b == 0:
-                grouped = work.tile([P, PACK * CHUNKS[c] // 2], BF16, name="m_grouped", bufs=2, align_bytes=64)
-                m_grouped[c] = grouped
-            words = event_rows[c][:].rearrange("p r k -> p (r k)").bitcast(F32)
-            pt = psum.tile([P, n_pairs, 2, P], F32, name="pt", bufs=2)
-            for j in range(n_pairs):
-                w0 = HIDDEN * (2 * b + j)
-                for u in range(2):
-                    nc.tensor.transpose(pt[:, j, u, :], words[:, w0 + u : w0 + HIDDEN : 2], identity[:])
-            nc.scalar.copy(
-                out=m_grouped[c][:]
-                .bitcast(F32)[:, BANK * b : BANK * b + HIDDEN * n_pairs]
-                .rearrange("p (j n u) -> p j n u", n=P, u=2),
-                in_=pt[:].rearrange("p j u n -> p j n u"),
-            )
-
-        def quantize_rows(c):
-            codes = work.tile([P, CHUNKS[c] // 2], U32, name="m_codes", bufs=3, align_bytes=64)
-            scales = work.tile([P, CHUNKS[c] // 2], U8, name="m_scales", bufs=3, align_bytes=64)
-            m_codes[c], m_scales[c] = codes, scales
-            nc.vector.quantize_mx(out=codes[:].bitcast(FP8X4), scales=scales[:], in_=m_grouped[c][:])
-
-        def quantize_sums(c):
-            codes = work.tile([P, CHUNKS[c] // 2], U32, name="a_codes", bufs=2, align_bytes=64)
-            scales = work.tile([P, CHUNKS[c] // 2], U8, name="a_scales", bufs=2, align_bytes=64)
-            a_codes[c], a_scales[c] = codes, scales
-            nc.vector.quantize_mx(out=codes[:].bitcast(FP8X4), scales=scales[:], in_=a_grouped[c][:])
-
-        def halves(c):
-            return ((0, m_codes[c], m_scales[c]), (1, a_codes[c], a_scales[c]))
 
         def new_result(c):
-            result = work.tile([P, CHUNKS[c] // P, OUT], F32, name="result", bufs=3)
+            result = keep.tile([P, CHUNKS[c] // P, OUT], F32, name="result_%d" % c)
             results[c] = result
-
-        def finish_direct(c):
-            new_result(c)
-            n_sets = CHUNKS[c] // P
-            for r0 in range(0, n_sets, BANK // OUT):
-                n = min(BANK // OUT, n_sets - r0)
-                po = psum.tile([P, n, OUT], F32, name="po", bufs=2)
-                for i in range(n):
-                    pair, side = divmod(r0 + i, 2)
-                    cols = slice(P * pair, P * (pair + 1))
-                    for half, codes, scales in halves(c):
-                        nc.tensor.matmul_mx(
-                            out=po[:, i, :],
-                            lhsT=codes[:, cols].bitcast(FP8X4),
-                            lhsT_scale=scales[:, cols],
-                            rhs=weight[:, 2 * side + half, :].bitcast(FP4X4),
-                            rhs_scale=weight_scales[:, 2 * side + half, :],
-                            start=(half == 0),
-                            stop=(half == 1),
-                        )
-                nc.vector.tensor_tensor(
-                    out=results[c][:, r0 : r0 + n, :], in0=po[:], in1=bias_spread[:, 0:n, :], op=ALU.add
-                )
-            nc.vector.tensor_scalar(out=results[c][:], in0=results[c][:], scalar1=0.0, scalar2=None, op0=ALU.max)
-
-        def finish_turned(c):
-            n = CHUNKS[c] // 2
-            width = BANK if n == BANK else P
-            turned = []
-            for side in range(2):
-                po = psum.tile([P, n], F32, name="po", bufs=2)
-                for c0 in range(0, n, width):
-                    cols = slice(c0, c0 + width)
-                    for half, codes, scales in halves(c):
-                        nc.tensor.matmul_mx(
-                            out=po[:, cols],
-                            lhsT=weight[:, 2 * side + half, :].bitcast(FP4X4),
-                            lhsT_scale=weight_scales[:, 2 * side + half, :],
-                            rhs=codes[:, cols].bitcast(FP8X4),
-                            rhs_scale=scales[:, cols],
-                            start=(half == 0),
-                            stop=(half == 1),
-                        )
-                channels = work.tile([P, n], F32, name="channels", bufs=2)
-                nc.scalar.activation(out=channels[:], in_=po[:], func=RELU, bias=bias_column[:])
-                turned.append(channels)
-            new_result(c)
-            for side in range(2):
-                pz = psum.tile([P, n // P, OUT], F32, name="pz", bufs=2)
-                for j in range(n // P):
-                    nc.tensor.transpose(pz[:, j, :], turned[side][:, P * j : P * (j + 1)], identity[:])
-                nc.scalar.copy(out=results[c][:, side::2, :], in_=pz[:])
+            return result
 
         def store(c):
             events = slice(first_event[c], first_event[c] + CHUNKS[c])
-            nc.sync.dma_start(out=out[events, :].rearrange("(r i) k -> i r k", i=P), in_=results[c][:])
+            order = "(r i) k -> i r k" if c >= n_chunks - DIRECT else "(i r) k -> i r k"
+            nc.sync.dma_start(out=out[events, :].rearrange(order, i=P), in_=results[c][:])
+
+        def empty_products(c):
+            if exists(c) and c >= n_chunks - DIRECT:
+                result = new_result(c)
+                bias = bias_rows[:].broadcast_to([P, CHUNKS[c] // P, OUT])
+                nc.vector.tensor_tensor(out=result[:], in0=products[c][:], in1=bias, op=ALU.add)
+            elif exists(c):
+                finished = work.tile([P, CHUNKS[c] // P, P], F32, name="channels", bufs=2)
+                channels[c] = finished
+                by_event = products[c][:].rearrange("p r i -> p (r i)").rearrange("p (i r) -> p r i", i=P)
+                nc.scalar.activation(out=finished[:], in_=by_event, func=RELU, bias=bias_column[:])
+
+        def rectify(c):
+            nc.vector.tensor_scalar(out=results[c][:], in0=results[c][:], scalar1=0.0, scalar2=None, op0=ALU.max)
+            store(c)
+
+        def turn_channels(c):
+            if c in channels:
+                pz = psum.tile([P, CHUNKS[c] // P, OUT], F32, name="pz", bufs=1)
+                turned_channels[c] = pz
+                for r in range(CHUNKS[c] // P):
+                    nc.tensor.transpose(pz[:, r, :], channels[c][:, r, :], identity[:])
+
+        def empty_channels(c):
+            if c in turned_channels:
+                nc.scalar.copy(out=new_result(c)[:], in_=turned_channels[c][:])
+                store(c)
 
 
-        for step in range(-1, n_chunks + 2):
-            to_widen, to_quantize, to_pool, to_finish = step + 1, step, step - 1, step - 2
-            if 0 <= step < n_chunks - AHEAD:
-                load_bytes(step + AHEAD)
-                load_rows(step + AHEAD)
-            if step == 0:
+        last = n_chunks - 1
+
+        def widen_next(widen_quarter, c, quarter):
+            widen_quarter(c + 1, quarter)
+            if c + 2 == last:
+                widen_quarter(last, quarter)
+
+        for c in range(-1, last - 1):
+            interleave(c, 1)
+            widen_next(widen_scalar, c, 0)
+            pool_nodes(c - 1, 1)
+            empty_rows(c - 1)
+            interleave(c, 0)
+            widen_next(widen_scalar, c, 1)
+            project(c - 2)
+            empty_sums(c - 1, 0)
+            widen_next(widen_vector, c, 0)
+            quantize_events(c, 1)
+            widen_next(widen_vector, c, 1)
+            quantize_events(c, 0)
+            if c == 0:
                 quantize_nodes()
-            if step == 1:
-                spread_bias()
-            if 0 <= to_finish < n_chunks:
-                quantize_rows(to_finish)
-                quantize_sums(to_finish)
-            if 0 <= to_quantize < n_chunks:
-                for g in range(GROUPS):
-                    interleave(to_quantize, g)
-                for g in range(GROUPS):
-                    quantize_events(to_quantize, g)
-            if 0 <= to_pool < n_chunks:
-                for j in range(CHUNKS[to_pool] // PAIR):
-                    empty_sums(to_pool, j, pool_nodes(to_pool, j))
-            if 0 <= to_finish < n_chunks:
-                if to_finish < FIRST_DIRECT:
-                    finish_turned(to_finish)
-                else:
-                    finish_direct(to_finish)
-                store(to_finish)
-            if to_widen < n_chunks:
-                for plane in range(PLANES):
-                    widen(to_widen, plane)
-            if 0 <= to_quantize < n_chunks:
-                for b in range((CHUNKS[to_quantize] + 2 * PAIR - 1) // (2 * PAIR)):
-                    turn_rows(to_quantize, b)
+            widen_next(widen_scalar, c, 2)
+            turn_channels(c - 3)
+            turn_rows(c)
+            if c + 2 == last:
+                turn_rows(c + 1)
+            empty_sums(c - 1, 1)
+            empty_products(c - 2)
+            pool_nodes(c, 0)
+            widen_next(widen_scalar, c, 3)
+            empty_channels(c - 3)
+            widen_next(widen_vector, c, 2)
+            widen_next(widen_vector, c, 3)
+            quantize_features(c - 1)
+
+        a, b = last - 1, last
+        interleave(a, 1)
+        interleave(a, 0)
+        pool_nodes(a - 1, 1)
+        empty_rows(a - 1)
+        empty_sums(a - 1, 0)
+        quantize_events(a, 1)
+        quantize_events(a, 0)
+        interleave(b, 1)
+        interleave(b, 0)
+        project(a - 2)
+        empty_sums(a - 1, 1)
+        empty_rows(a)
+        pool_nodes(a, 0)
+        empty_products(a - 2)
+        quantize_events(b, 1)
+        quantize_events(b, 0)
+        quantize_features(a - 1)
+        turn_channels(a - 3)
+        turn_rows(b)
+        empty_sums(a, 0)
+        pool_nodes(b, 0)
+        empty_channels(a - 3)
+        empty_rows(b)
+        project(a - 1)
+        quantize_features(a)
+        turn_channels(a - 2)
+        empty_sums(b, 0)
+        empty_channels(a - 2)
+        project(a)
+        empty_products(a - 1)
+        quantize_features(b)
+        rectify(a - 1)
+        project(b)
+        empty_products(a)
+        empty_products(b)
+        rectify(a)
+        rectify(b)

@@ -40,7 +40,7 @@ def scalar_planes(c):
         return range(PLANES)
     if c == 2:
         return range(6)
-    if c == 3:
+    if c % 2 == 1:
         return range(5)
     if c >= len(CHUNKS) - 2:
         return range(5)

@@ -40,11 +40,13 @@ def scalar_planes(c):
         return range(PLANES)
     if c == 2:
         return range(6)
-    if c % 2 == 1:
+    if c == 3 or c >= len(CHUNKS) - 2:
         return range(5)
-    if c >= len(CHUNKS) - 2:
-        return range(5)
-    return range(PACK)
+    return range(3 if c % 3 == 0 else 4)
+
+
+def woven(c):
+    return P if 2 <= c < len(CHUNKS) - 3 else 0
 
 
 def tile_mymodel_icdm_pa_t_w4_kernel(
@@ -77,6 +79,8 @@ def tile_mymodel_icdm_pa_t_w4_kernel(
         bias_rows = keep.tile([P, 1, OUT], BF16, name="bias_rows")
         identity = keep.tile([P, P], F32, name="identity")
         make_identity(nc, identity[:])
+        identity_bf = keep.tile([P, P], BF16, name="identity_bf")
+        make_identity(nc, identity_bf[:])
 
 
         plane_scales = keep.tile([P, GROUPS, PACK], F32, name="plane_scales")
@@ -146,6 +150,7 @@ def tile_mymodel_icdm_pa_t_w4_kernel(
 
 
         wide, h_grouped, h_codes, h_scales = {}, {}, {}, {}
+        weaves = {}
         sums, turned_rows, e_grouped, e_codes, e_scales = {}, {}, {}, {}, {}
         products, channels, turned_channels, results = {}, {}, {}, {}
 
@@ -179,21 +184,44 @@ def tile_mymodel_icdm_pa_t_w4_kernel(
                 for plane in planes[len(planes) * quarter // 4 : len(planes) * (quarter + 1) // 4]:
                     widen(c, plane)
 
+        def grouped_events(c, g):
+            if (c, g) not in h_grouped:
+                grouped = work.tile([P, CHUNKS[c], PACK], BF16, name="h_grouped", bufs=3, align_bytes=64)
+                h_grouped[c, g] = grouped
+            return h_grouped[c, g]
+
         def interleave(c, g):
             if exists(c):
-                grouped = work.tile([P, PACK * CHUNKS[c]], BF16, name="h_grouped", bufs=3, align_bytes=64)
-                h_grouped[c, g] = grouped
+                e0 = woven(c) if g == 0 else 0
                 nc.vector.tensor_copy(
-                    out=grouped[:].rearrange("p (e i t) -> p e t i", i=4, t=PACK),
-                    in_=wide[c, g][:].rearrange("p t (e i) -> p e t i", i=4),
+                    out=grouped_events(c, g)[:, e0:, :].rearrange("p (e i) t -> p e t i", i=4),
+                    in_=wide[c, g][:, :, e0:].rearrange("p t (e i) -> p e t i", i=4),
                 )
+
+        def weave(c):
+            if exists(c) and woven(c):
+                pw = psum.tile([P, woven(c), PACK], BF16, name="pw", bufs=1)
+                weaves[c] = pw
+                nc.tensor.matmul(
+                    out=pw[:].rearrange("p e t -> p t e"),
+                    lhsT=identity_bf[:],
+                    rhs=wide[c, 0][:, :, 0 : woven(c)],
+                    start=True,
+                    stop=True,
+                )
+
+        def empty_weave(c):
+            if c in weaves:
+                nc.scalar.copy(out=grouped_events(c, 0)[:, 0 : woven(c), :], in_=weaves[c][:])
 
         def quantize_events(c, g):
             if exists(c):
                 codes = work.tile([P, CHUNKS[c]], U32, name="h_codes", bufs=6, align_bytes=64)
                 scales = work.tile([P, CHUNKS[c]], U8, name="h_scales", bufs=6, align_bytes=64)
                 h_codes[c, g], h_scales[c, g] = codes, scales
-                nc.vector.quantize_mx(out=codes[:].bitcast(FP8X4), scales=scales[:], in_=h_grouped[c, g][:])
+                nc.vector.quantize_mx(
+                    out=codes[:].bitcast(FP8X4), scales=scales[:], in_=h_grouped[c, g][:].rearrange("p e t -> p (e t)")
+                )
 
         def pool_nodes(c, j):
             if exists(c, j):
@@ -216,7 +244,7 @@ def tile_mymodel_icdm_pa_t_w4_kernel(
 
         def event_features(c):
             if c not in e_grouped:
-                grouped = work.tile([P, 2, PACK * CHUNKS[c] // 2], BF16, name="e_grouped", bufs=3, align_bytes=64)
+                grouped = work.tile([P, 2, PACK * CHUNKS[c] // 2], BF16, name="e_grouped", bufs=4, align_bytes=64)
                 e_grouped[c] = grouped
             return e_grouped[c]
 
@@ -227,22 +255,24 @@ def tile_mymodel_icdm_pa_t_w4_kernel(
                     in_=sums[c, j][:].rearrange("p t n -> p n t"),
                 )
 
-        def turn_rows(c):
-            if exists(c):
-                i, e0 = place(c)
+        def turn_rows(chunks, bank):
+            if exists(chunks[0]):
+                i, e0 = place(chunks[0])
                 words = event_rows[i][:].rearrange("p r k -> p (r k)").bitcast(F32)
-                pt = psum.tile([P, CHUNKS[c] // PAIR, 2, P], F32, name="pt", bufs=2)
-                turned_rows[c] = pt
-                for j in range(CHUNKS[c] // PAIR):
+                pt = psum.tile([P, 2, 2, P], F32, name=bank, bufs=1)
+                for j in range(2):
                     w0 = e0 + HIDDEN * j
                     for u in range(2):
                         nc.tensor.transpose(pt[:, j, u, :], words[:, w0 + u : w0 + HIDDEN : 2], identity[:])
+                for c in chunks:
+                    j = (first_event[c] - first_event[chunks[0]]) // PAIR
+                    turned_rows[c] = pt[:, j : j + CHUNKS[c] // PAIR]
 
         def empty_rows(c):
             if exists(c):
                 nc.scalar.copy(
                     out=event_features(c)[:, 0, :].bitcast(F32).rearrange("p (j n u) -> p j n u", n=P, u=2),
-                    in_=turned_rows[c][:].rearrange("p j u n -> p j n u"),
+                    in_=turned_rows[c].rearrange("p j u n -> p j n u"),
                 )
 
         def quantize_features(c):
@@ -256,7 +286,8 @@ def tile_mymodel_icdm_pa_t_w4_kernel(
 
         def project(c):
             if exists(c):
-                po = psum.tile([P, CHUNKS[c] // P, OUT], F32, name="po", bufs=2)
+                bank, bufs = ("pt", 1) if c == n_chunks - 1 else ("po", 2)
+                po = psum.tile([P, CHUNKS[c] // P, OUT], F32, name=bank, bufs=bufs)
                 products[c] = po
                 for r in range(CHUNKS[c] // P):
                     j, side = divmod(r, 2)
@@ -323,8 +354,10 @@ def tile_mymodel_icdm_pa_t_w4_kernel(
         for c in range(-1, last - 1):
             interleave(c, 1)
             widen_next(widen_scalar, c, 0)
+            weave(c)
             pool_nodes(c - 1, 1)
             empty_rows(c - 1)
+            empty_weave(c)
             interleave(c, 0)
             widen_next(widen_scalar, c, 1)
             project(c - 2)
@@ -337,9 +370,9 @@ def tile_mymodel_icdm_pa_t_w4_kernel(
                 quantize_nodes()
             widen_next(widen_scalar, c, 2)
             turn_channels(c - 3)
-            turn_rows(c)
+            turn_rows((c,), "pt")
             if c + 2 == last:
-                turn_rows(c + 1)
+                turn_rows((c + 1, last), "pw")
             empty_sums(c - 1, 1)
             empty_products(c - 2)
             pool_nodes(c, 0)
@@ -360,30 +393,29 @@ def tile_mymodel_icdm_pa_t_w4_kernel(
         interleave(b, 1)
         interleave(b, 0)
         project(a - 2)
+        turn_channels(a - 3)
         empty_sums(a - 1, 1)
-        empty_rows(a)
-        pool_nodes(a, 0)
         empty_products(a - 2)
+        empty_channels(a - 3)
+        pool_nodes(a, 0)
         quantize_events(b, 1)
         quantize_events(b, 0)
         quantize_features(a - 1)
-        turn_channels(a - 3)
-        turn_rows(b)
+        empty_rows(a)
+        empty_rows(b)
         empty_sums(a, 0)
         pool_nodes(b, 0)
-        empty_channels(a - 3)
-        empty_rows(b)
         project(a - 1)
         quantize_features(a)
         turn_channels(a - 2)
         empty_sums(b, 0)
         empty_channels(a - 2)
         project(a)
-        empty_products(a - 1)
         quantize_features(b)
-        rectify(a - 1)
+        empty_products(a - 1)
         project(b)
         empty_products(a)
+        rectify(a - 1)
         empty_products(b)
         rectify(a)
         rectify(b)

@@ -27,26 +27,27 @@ BANK = 512
 PLANES = GROUPS * PACK
 
 CHUNKS = (2 * PAIR,) * 15 + (PAIR,) * 2
-LOADS = (512, 512, 1024, 1024, 1024, 2048, 2048)
+LOADS = (1024, 1024, 1024, 1024, 2048, 2048)
 DIRECT = 3
+BANKS = {"ps": 3, "po": 2, "pt": 1, "pz": 1, "pw": 1}
 
 FLOPS = 2 * NODES * EVENTS * HIDDEN + 2 * EVENTS * 2 * HIDDEN * OUT
 
 
 def scalar_planes(c):
     if c == 0:
-        return (0, PACK)
+        return ()
     if c == 1:
-        return range(PLANES)
-    if c == 2:
-        return range(6)
-    if c == 3 or c >= len(CHUNKS) - 2:
+        return range(1, PLANES, 2)
+    if c >= len(CHUNKS) - 2:
         return range(5)
-    return range(3 if c % 3 == 0 else 4)
+    return range(3 if c % 3 == 0 and c > 3 else 4)
 
 
-def woven(c):
-    return P if 2 <= c < len(CHUNKS) - 3 else 0
+def woven(c, g):
+    if g == 1 or c >= len(CHUNKS) - 3:
+        return 0
+    return CHUNKS[c] if c < 2 else P
 
 
 def tile_mymodel_icdm_pa_t_w4_kernel(
@@ -84,18 +85,20 @@ def tile_mymodel_icdm_pa_t_w4_kernel(
 
 
         plane_scales = keep.tile([P, GROUPS, PACK], F32, name="plane_scales")
-        nc.sync.dma_start(out=plane_scales[:], in_=H_A_scale.rearrange("(g p t) o -> p g (t o)", p=P, t=PACK))
+        nc.scalar.dma_start(out=plane_scales[:], in_=H_A_scale.rearrange("(g p t) o -> p g (t o)", p=P, t=PACK))
 
         event_bytes = {}
         event_rows = {}
 
-        def load_bytes(i):
+        def load_bytes(i, passes):
             events = slice(load_start[i], load_start[i] + LOADS[i])
-            for g in range(GROUPS):
+            for g in passes:
                 raw = keep.tile([P, PACK, LOADS[i]], U8, name="bytes_%d_%d" % (i, g), align_bytes=64)
                 event_bytes[i, g] = raw
                 nodes = slice(PASS * g, PASS * (g + 1))
-                nc.sync.dma_start(out=raw[:], in_=H_A_bytes[nodes, events].rearrange("(p t) e -> p t e", t=PACK))
+                source = H_A_bytes[nodes, events].rearrange("(p t) e -> p t e", t=PACK)
+                for planes in (slice(0, 2), slice(2, 4)) if i == 0 else (slice(0, 4),):
+                    nc.sync.dma_start(out=raw[:, planes, :], in_=source[:, planes, :])
 
         def load_rows(i):
             events = slice(load_start[i], load_start[i] + LOADS[i])
@@ -107,14 +110,15 @@ def tile_mymodel_icdm_pa_t_w4_kernel(
             i = max(i for i in range(len(LOADS)) if load_start[i] <= first_event[c])
             return i, first_event[c] - load_start[i]
 
-        load_bytes(0)
-        load_bytes(1)
+        def load_nodes():
+            nc.sync.dma_start(out=node_rows[:], in_=H_mean_A.rearrange("(g p j) c -> p g j c", p=P, j=PACK))
+
         node_rows = keep.tile([P, GROUPS, PACK, HIDDEN], BF16, name="node_rows", align_bytes=64)
-        nc.sync.dma_start(out=node_rows[:], in_=H_mean_A.rearrange("(g p j) c -> p g j c", p=P, j=PACK))
+        load_bytes(0, range(GROUPS))
+        load_nodes()
+        load_bytes(1, (0,))
         load_rows(0)
-        load_bytes(2)
-        load_rows(1)
-        load_bytes(3)
+        load_bytes(1, (1,))
         word_halves = wEA1_words[0].rearrange("(h p) b -> p h b", h=2).bitcast(I32)
         scale_quadrants = wEA1_scales[0].rearrange("(h r b) n -> r b h n", h=2, r=2)
         for side in range(2):
@@ -128,24 +132,25 @@ def tile_mymodel_icdm_pa_t_w4_kernel(
                 in_=scale_quadrants[r].bitcast(I32),
             )
         nc.sync.dma_start(out=bias_column[:], in_=bEA1.rearrange("(c o) -> c o", o=1))
-        load_rows(2)
-        load_rows(3)
-        for i in range(4, len(LOADS)):
-            load_bytes(i)
+        load_rows(1)
+        for i in range(2, len(LOADS)):
+            load_bytes(i, range(GROUPS))
             load_rows(i)
         nc.sync.dma_start(out=bias_rows[:, 0, :], in_=bEA1.partition_broadcast(P))
 
+        node_grouped = keep.tile([P, GROUPS, PACK, QUADS, PACK], BF16, name="node_grouped", align_bytes=64)
+
+        def group_nodes(g):
+            nc.scalar.copy(out=node_grouped[:, g], in_=node_rows[:, g].rearrange("p j (q t) -> p t q j", t=PACK))
+
         def quantize_nodes():
-            grouped = keep.tile([P, GROUPS, PACK, QUADS, PACK], BF16, name="node_grouped", align_bytes=64)
-            for g in range(GROUPS):
-                nc.vector.tensor_copy(out=grouped[:, g], in_=node_rows[:, g].rearrange("p j (q t) -> p t q j", t=PACK))
             for g in range(GROUPS):
                 for t in range(PACK):
                     c0 = (2 * (PACK * g + t) + 1) * QUADS
                     nc.vector.quantize_mx(
                         out=node_codes[:, c0 : c0 + QUADS].bitcast(FP8X4),
                         scales=node_scales[:, c0 : c0 + QUADS],
-                        in_=grouped[:, g, t].rearrange("p q j -> p (q j)"),
+                        in_=node_grouped[:, g, t].rearrange("p q j -> p (q j)"),
                     )
 
 
@@ -186,33 +191,37 @@ def tile_mymodel_icdm_pa_t_w4_kernel(
 
         def grouped_events(c, g):
             if (c, g) not in h_grouped:
-                grouped = work.tile([P, CHUNKS[c], PACK], BF16, name="h_grouped", bufs=3, align_bytes=64)
+                grouped = work.tile([P, CHUNKS[c], PACK], BF16, name="h_grouped", bufs=4, align_bytes=64)
                 h_grouped[c, g] = grouped
             return h_grouped[c, g]
 
         def interleave(c, g):
-            if exists(c):
-                e0 = woven(c) if g == 0 else 0
+            if exists(c) and woven(c, g) < CHUNKS[c]:
+                e0 = woven(c, g)
                 nc.vector.tensor_copy(
                     out=grouped_events(c, g)[:, e0:, :].rearrange("p (e i) t -> p e t i", i=4),
                     in_=wide[c, g][:, :, e0:].rearrange("p t (e i) -> p e t i", i=4),
                 )
 
-        def weave(c):
-            if exists(c) and woven(c):
-                pw = psum.tile([P, woven(c), PACK], BF16, name="pw", bufs=1)
-                weaves[c] = pw
-                nc.tensor.matmul(
-                    out=pw[:].rearrange("p e t -> p t e"),
-                    lhsT=identity_bf[:],
-                    rhs=wide[c, 0][:, :, 0 : woven(c)],
-                    start=True,
-                    stop=True,
-                )
+        def weave(c, g, j, bank):
+            if exists(c) and woven(c, g) > PAIR * j:
+                n = min(PAIR, woven(c, g) - PAIR * j)
+                pw = psum.tile([P, n, PACK], BF16, name=bank, bufs=BANKS[bank])
+                weaves[c, g, j] = pw
+                for e0 in range(0, n, P):
+                    e1 = min(n, e0 + P)
+                    nc.tensor.matmul(
+                        out=pw[:, e0:e1, :].rearrange("p e t -> p t e"),
+                        lhsT=identity_bf[:],
+                        rhs=wide[c, g][:, :, PAIR * j + e0 : PAIR * j + e1],
+                        start=True,
+                        stop=True,
+                    )
 
-        def empty_weave(c):
-            if c in weaves:
-                nc.scalar.copy(out=grouped_events(c, 0)[:, 0 : woven(c), :], in_=weaves[c][:])
+        def empty_weave(c, g, j):
+            if (c, g, j) in weaves:
+                pw = weaves[c, g, j]
+                nc.scalar.copy(out=grouped_events(c, g)[:, PAIR * j : PAIR * j + pw.shape[1], :], in_=pw[:])
 
         def quantize_events(c, g):
             if exists(c):
@@ -351,13 +360,38 @@ def tile_mymodel_icdm_pa_t_w4_kernel(
             if c + 2 == last:
                 widen_quarter(last, quarter)
 
-        for c in range(-1, last - 1):
-            interleave(c, 1)
+        for plane in range(0, PLANES, 2):
+            widen(0, plane)
+            widen(1, plane + 1)
+            widen(0, plane + 1)
+            widen(1, plane)
+            if plane == 2:
+                weave(0, 0, 0, "po")
+                weave(0, 0, 1, "po")
+        weave(1, 0, 1, "pz")
+        weave(1, 0, 0, "pw")
+        empty_weave(0, 0, 0)
+        group_nodes(0)
+        empty_weave(0, 0, 1)
+        group_nodes(1)
+        interleave(0, 1)
+        interleave(1, 1)
+        quantize_events(0, 0)
+        quantize_events(0, 1)
+        quantize_nodes()
+        empty_weave(1, 0, 1)
+        turn_rows((0,), "pt")
+        pool_nodes(0, 0)
+
+        for c in range(1, last - 1):
+            if c > 1:
+                interleave(c, 1)
             widen_next(widen_scalar, c, 0)
-            weave(c)
+            if c > 1:
+                weave(c, 0, 0, "pw")
             pool_nodes(c - 1, 1)
             empty_rows(c - 1)
-            empty_weave(c)
+            empty_weave(c, 0, 0)
             interleave(c, 0)
             widen_next(widen_scalar, c, 1)
             project(c - 2)
@@ -366,8 +400,6 @@ def tile_mymodel_icdm_pa_t_w4_kernel(
             quantize_events(c, 1)
             widen_next(widen_vector, c, 1)
             quantize_events(c, 0)
-            if c == 0:
-                quantize_nodes()
             widen_next(widen_scalar, c, 2)
             turn_channels(c - 3)
             turn_rows((c,), "pt")

@@ -26,28 +26,29 @@ QUADS = HIDDEN // PACK
 BANK = 512
 PLANES = GROUPS * PACK
 
-CHUNKS = (2 * PAIR,) * 15 + (PAIR,) * 2
-LOADS = (1024, 1024, 1024, 1024, 2048, 2048)
-DIRECT = 3
-BANKS = {"ps": 3, "po": 2, "pt": 1, "pz": 1, "pw": 1}
+CHUNKS = (4 * PAIR,) * 8
+CHUNK = 4 * PAIR
+LOAD = 4 * PAIR
+AHEAD = 3
+DIRECT = 1
+BANKS = {"ps": 3, "po": 2, "pt": 2, "pw": 1}
+SCALAR, VECTOR = 0, 1
 
 FLOPS = 2 * NODES * EVENTS * HIDDEN + 2 * EVENTS * 2 * HIDDEN * OUT
 
 
-def scalar_planes(c):
+def shares(c):
     if c == 0:
-        return ()
-    if c == 1:
-        return range(1, PLANES, 2)
-    if c >= len(CHUNKS) - 2:
-        return range(5)
-    return range(3 if c % 3 == 0 and c > 3 else 4)
+        return [(plane, 0, CHUNK) for plane in (1, 3, 5)], [(plane, 0, CHUNK) for plane in (0, 2, 4, 6, 7)]
+    split = 512 if c == 1 else 512 if c == len(CHUNKS) - 1 else 512
+    whole = [(plane, 0, CHUNK) for plane in range(PLANES)]
+    return [(4, 0, split)] + whole[:3], whole[:4:-1] + [(4, split, CHUNK), whole[3]]
 
 
 def woven(c, g):
-    if g == 1 or c >= len(CHUNKS) - 3:
+    if g == 1 or c == len(CHUNKS) - 1:
         return 0
-    return CHUNKS[c] if c < 2 else P
+    return CHUNK if c == 0 else PAIR
 
 
 def tile_mymodel_icdm_pa_t_w4_kernel(
@@ -56,14 +57,16 @@ def tile_mymodel_icdm_pa_t_w4_kernel(
     nc = tc.nc
     n_chunks = len(CHUNKS)
     first_event = [sum(CHUNKS[:c]) for c in range(n_chunks)]
-    load_start = [sum(LOADS[:i]) for i in range(len(LOADS))]
 
     with ExitStack() as ctx:
         keep = ctx.enter_context(tc.tile_pool(name="keep", bufs=1))
         work = ctx.enter_context(tc.tile_pool(name="work", bufs=2))
-        psum = ctx.enter_context(tc.psum_pool(name="psum", bufs=2))
+        psum = ctx.enter_context(tc.psum_pool(name="psum", bufs=1))
         ctx.enter_context(tc.manual_schedule())
 
+
+        plane_scales = keep.tile([P, GROUPS, PACK], F32, name="plane_scales")
+        nc.scalar.dma_start(out=plane_scales[:], in_=H_A_scale.rearrange("(g p t) o -> p g (t o)", p=P, t=PACK))
 
         n_blocks = 2 * PLANES + 1
         node_codes = keep.tile([P, n_blocks * QUADS], U32, name="node_codes", align_bytes=64)
@@ -81,44 +84,36 @@ def tile_mymodel_icdm_pa_t_w4_kernel(
         identity = keep.tile([P, P], F32, name="identity")
         make_identity(nc, identity[:])
         identity_bf = keep.tile([P, P], BF16, name="identity_bf")
-        make_identity(nc, identity_bf[:])
+        nc.scalar.activation(out=identity_bf[:], in_=identity[:], func=COPY)
 
-
-        plane_scales = keep.tile([P, GROUPS, PACK], F32, name="plane_scales")
-        nc.scalar.dma_start(out=plane_scales[:], in_=H_A_scale.rearrange("(g p t) o -> p g (t o)", p=P, t=PACK))
 
         event_bytes = {}
         event_rows = {}
 
-        def load_bytes(i, passes):
-            events = slice(load_start[i], load_start[i] + LOADS[i])
-            for g in passes:
-                raw = keep.tile([P, PACK, LOADS[i]], U8, name="bytes_%d_%d" % (i, g), align_bytes=64)
+        def load_bytes(i, g):
+            if LOAD * i < EVENTS:
+                raw = work.tile([P, PACK, LOAD], U8, name="event_bytes", bufs=2 * (AHEAD + 1), align_bytes=64)
                 event_bytes[i, g] = raw
-                nodes = slice(PASS * g, PASS * (g + 1))
-                source = H_A_bytes[nodes, events].rearrange("(p t) e -> p t e", t=PACK)
+                source = H_A_bytes[PASS * g : PASS * (g + 1), LOAD * i : LOAD * (i + 1)].rearrange("(p t) e -> p t e", t=PACK)
                 for planes in (slice(0, 2), slice(2, 4)) if i == 0 else (slice(0, 4),):
                     nc.sync.dma_start(out=raw[:, planes, :], in_=source[:, planes, :])
 
         def load_rows(i):
-            events = slice(load_start[i], load_start[i] + LOADS[i])
-            rows = keep.tile([P, LOADS[i] // P, HIDDEN], BF16, name="rows_%d" % i, align_bytes=64)
-            event_rows[i] = rows
-            nc.sync.dma_start(out=rows[:], in_=H_mean_M[events, :].rearrange("(r i) k -> i r k", i=P))
-
-        def place(c):
-            i = max(i for i in range(len(LOADS)) if load_start[i] <= first_event[c])
-            return i, first_event[c] - load_start[i]
-
-        def load_nodes():
-            nc.sync.dma_start(out=node_rows[:], in_=H_mean_A.rearrange("(g p j) c -> p g j c", p=P, j=PACK))
+            if LOAD * i < EVENTS:
+                rows = work.tile([P, LOAD // P, HIDDEN], BF16, name="event_rows", bufs=AHEAD + 1, align_bytes=64)
+                event_rows[i] = rows
+                nc.sync.dma_start(out=rows[:], in_=H_mean_M[LOAD * i : LOAD * (i + 1), :].rearrange("(r i) k -> i r k", i=P))
 
         node_rows = keep.tile([P, GROUPS, PACK, HIDDEN], BF16, name="node_rows", align_bytes=64)
-        load_bytes(0, range(GROUPS))
-        load_nodes()
-        load_bytes(1, (0,))
+        load_bytes(0, 0)
+        load_bytes(0, 1)
+        nc.sync.dma_start(out=node_rows[:], in_=H_mean_A.rearrange("(g p j) c -> p g j c", p=P, j=PACK))
+        load_bytes(1, 0)
         load_rows(0)
-        load_bytes(1, (1,))
+        load_bytes(1, 1)
+        load_rows(1)
+        load_bytes(2, 0)
+        load_bytes(2, 1)
         word_halves = wEA1_words[0].rearrange("(h p) b -> p h b", h=2).bitcast(I32)
         scale_quadrants = wEA1_scales[0].rearrange("(h r b) n -> r b h n", h=2, r=2)
         for side in range(2):
@@ -132,16 +127,14 @@ def tile_mymodel_icdm_pa_t_w4_kernel(
                 in_=scale_quadrants[r].bitcast(I32),
             )
         nc.sync.dma_start(out=bias_column[:], in_=bEA1.rearrange("(c o) -> c o", o=1))
-        load_rows(1)
-        for i in range(2, len(LOADS)):
-            load_bytes(i, range(GROUPS))
-            load_rows(i)
+        load_rows(2)
         nc.sync.dma_start(out=bias_rows[:, 0, :], in_=bEA1.partition_broadcast(P))
 
         node_grouped = keep.tile([P, GROUPS, PACK, QUADS, PACK], BF16, name="node_grouped", align_bytes=64)
 
         def group_nodes(g):
-            nc.scalar.copy(out=node_grouped[:, g], in_=node_rows[:, g].rearrange("p j (q t) -> p t q j", t=PACK))
+            copy = nc.scalar.copy if g else nc.vector.tensor_copy
+            copy(out=node_grouped[:, g], in_=node_rows[:, g].rearrange("p j (q t) -> p t q j", t=PACK))
 
         def quantize_nodes():
             for g in range(GROUPS):
@@ -154,300 +147,355 @@ def tile_mymodel_icdm_pa_t_w4_kernel(
                     )
 
 
-        wide, h_grouped, h_codes, h_scales = {}, {}, {}, {}
-        weaves = {}
+        wide, weaves, h_grouped, h_codes, h_scales = {}, {}, {}, {}, {}
         sums, turned_rows, e_grouped, e_codes, e_scales = {}, {}, {}, {}, {}
         products, channels, turned_channels, results = {}, {}, {}, {}
 
-        def exists(c, j=0):
-            return 0 <= c < n_chunks and PAIR * j < CHUNKS[c]
+        def exists(c, first=0):
+            return 0 <= c < n_chunks and first < CHUNKS[c]
 
-        def widen(c, plane):
-            g, t = divmod(plane, PACK)
-            if (c, g) not in wide:
-                planes = work.tile([P, PACK, CHUNKS[c]], BF16, name="wide", bufs=6, align_bytes=64)
-                wide[c, g] = planes
-            i, e0 = place(c)
-            values = event_bytes[i, g][:, t, e0 : e0 + CHUNKS[c]].bitcast(FP8)
-            scale = plane_scales[:, g, t : t + 1]
-            if plane in scalar_planes(c):
-                nc.scalar.activation(out=wide[c, g][:, t, :], in_=values, func=COPY, scale=scale)
-            else:
-                nc.vector.tensor_scalar(
-                    out=wide[c, g][:, t, :], in0=values, scalar1=scale, scalar2=None, op0=ALU.mult
-                )
+        def new_bank(use, shape, dtype):
+            bank = psum.tile(shape, dtype, name=use, bufs=BANKS[use])
+            return bank
 
-        def widen_scalar(c, quarter):
-            if exists(c):
-                planes = scalar_planes(c)
-                for plane in planes[len(planes) * quarter // 4 : len(planes) * (quarter + 1) // 4]:
-                    widen(c, plane)
-
-        def widen_vector(c, quarter):
-            if exists(c):
-                planes = [plane for plane in range(PLANES) if plane not in scalar_planes(c)]
-                for plane in planes[len(planes) * quarter // 4 : len(planes) * (quarter + 1) // 4]:
-                    widen(c, plane)
+        def widen(c, engine, n):
+            if exists(c) and n < len(shares(c)[engine]):
+                plane, e0, e1 = shares(c)[engine][n]
+                g, t = divmod(plane, PACK)
+                if (c, g) not in wide:
+                    planes = work.tile([P, PACK, CHUNK], BF16, name="wide", bufs=4, align_bytes=64)
+                    wide[c, g] = planes
+                values = event_bytes[c, g][:, t, e0:e1].bitcast(FP8)
+                scale = plane_scales[:, g, t : t + 1]
+                if engine == SCALAR:
+                    nc.scalar.activation(out=wide[c, g][:, t, e0:e1], in_=values, func=COPY, scale=scale)
+                else:
+                    nc.vector.tensor_scalar(
+                        out=wide[c, g][:, t, e0:e1], in0=values, scalar1=scale, scalar2=None, op0=ALU.mult
+                    )
 
         def grouped_events(c, g):
             if (c, g) not in h_grouped:
-                grouped = work.tile([P, CHUNKS[c], PACK], BF16, name="h_grouped", bufs=4, align_bytes=64)
+                grouped = work.tile([P, CHUNKS[c], PACK], BF16, name="h_grouped", bufs=3, align_bytes=64)
                 h_grouped[c, g] = grouped
             return h_grouped[c, g]
 
-        def interleave(c, g):
-            if exists(c) and woven(c, g) < CHUNKS[c]:
-                e0 = woven(c, g)
-                nc.vector.tensor_copy(
-                    out=grouped_events(c, g)[:, e0:, :].rearrange("p (e i) t -> p e t i", i=4),
-                    in_=wide[c, g][:, :, e0:].rearrange("p t (e i) -> p e t i", i=4),
-                )
+        def interleave(c, g, events, copy=nc.vector.tensor_copy):
+            copy(
+                out=grouped_events(c, g)[:, events, :].rearrange("p (e i) t -> p e t i", i=4),
+                in_=wide[c, g][:, :, events].rearrange("p t (e i) -> p e t i", i=4),
+            )
 
-        def weave(c, g, j, bank):
-            if exists(c) and woven(c, g) > PAIR * j:
-                n = min(PAIR, woven(c, g) - PAIR * j)
-                pw = psum.tile([P, n, PACK], BF16, name=bank, bufs=BANKS[bank])
-                weaves[c, g, j] = pw
+        def weave(c, j, use):
+            if exists(c) and woven(c, 0) > PAIR * j:
+                n = min(PAIR, woven(c, 0) - PAIR * j)
+                pw = new_bank(use, [P, n, PACK], BF16)
+                weaves[c, j] = pw
                 for e0 in range(0, n, P):
-                    e1 = min(n, e0 + P)
                     nc.tensor.matmul(
-                        out=pw[:, e0:e1, :].rearrange("p e t -> p t e"),
+                        out=pw[:, e0 : e0 + P, :].rearrange("p e t -> p t e"),
                         lhsT=identity_bf[:],
-                        rhs=wide[c, g][:, :, PAIR * j + e0 : PAIR * j + e1],
+                        rhs=wide[c, 0][:, :, PAIR * j + e0 : PAIR * j + e0 + P],
                         start=True,
                         stop=True,
                     )
 
-        def empty_weave(c, g, j):
-            if (c, g, j) in weaves:
-                pw = weaves[c, g, j]
-                nc.scalar.copy(out=grouped_events(c, g)[:, PAIR * j : PAIR * j + pw.shape[1], :], in_=pw[:])
+        def empty_weave(c, j):
+            if (c, j) in weaves:
+                pw = weaves[c, j]
+                nc.scalar.copy(out=grouped_events(c, 0)[:, PAIR * j : PAIR * j + pw.shape[1], :], in_=pw[:])
 
-        def quantize_events(c, g):
+        def quantize_events(c, g, events=slice(None)):
             if exists(c):
-                codes = work.tile([P, CHUNKS[c]], U32, name="h_codes", bufs=6, align_bytes=64)
-                scales = work.tile([P, CHUNKS[c]], U8, name="h_scales", bufs=6, align_bytes=64)
-                h_codes[c, g], h_scales[c, g] = codes, scales
+                if (c, g) not in h_codes:
+                    codes = work.tile([P, CHUNKS[c]], U32, name="h_codes", bufs=4, align_bytes=64)
+                    scales = work.tile([P, CHUNKS[c]], U8, name="h_scales", bufs=4, align_bytes=64)
+                    h_codes[c, g], h_scales[c, g] = codes, scales
                 nc.vector.quantize_mx(
-                    out=codes[:].bitcast(FP8X4), scales=scales[:], in_=h_grouped[c, g][:].rearrange("p e t -> p (e t)")
+                    out=h_codes[c, g][:, events].bitcast(FP8X4),
+                    scales=h_scales[c, g][:, events],
+                    in_=h_grouped[c, g][:, events, :].rearrange("p e t -> p (e t)"),
                 )
 
-        def pool_nodes(c, j):
-            if exists(c, j):
-                ps = psum.tile([P, PACK, P], F32, name="ps", bufs=3)
-                sums[c, j] = ps
-                for g in (1, 0):
-                    for t in range(PACK):
-                        for side in range(2):
-                            cols = slice(PAIR * j + P * side, PAIR * j + P * (side + 1))
-                            c0 = (2 * (PACK * g + t) + 1 - side) * QUADS
-                            nc.tensor.matmul_mx(
-                                out=ps[:, t, :],
-                                lhsT=node_codes[:, c0 : c0 + P].bitcast(FP8X4),
-                                lhsT_scale=node_scales[:, c0 : c0 + P],
-                                rhs=h_codes[c, g][:, cols].bitcast(FP8X4),
-                                rhs_scale=h_scales[c, g][:, cols],
-                                start=(g == 1 and t == 0 and side == 0),
-                                stop=(g == 0 and t == PACK - 1 and side == 1),
-                            )
+        def pool_nodes(c, j, g):
+            if exists(c, PAIR * j):
+                if g == 1:
+                    sums[c, j] = new_bank("ps", [P, PACK, P], F32)
+                for t in range(PACK):
+                    for side in range(2):
+                        cols = slice(PAIR * j + P * side, PAIR * j + P * (side + 1))
+                        c0 = (2 * (PACK * g + t) + 1 - side) * QUADS
+                        nc.tensor.matmul_mx(
+                            out=sums[c, j][:, t, :],
+                            lhsT=node_codes[:, c0 : c0 + P].bitcast(FP8X4),
+                            lhsT_scale=node_scales[:, c0 : c0 + P],
+                            rhs=h_codes[c, g][:, cols].bitcast(FP8X4),
+                            rhs_scale=h_scales[c, g][:, cols],
+                            start=(g == 1 and t == 0 and side == 0),
+                            stop=(g == 0 and t == PACK - 1 and side == 1),
+                        )
 
         def event_features(c):
             if c not in e_grouped:
-                grouped = work.tile([P, 2, PACK * CHUNKS[c] // 2], BF16, name="e_grouped", bufs=4, align_bytes=64)
+                grouped = work.tile([P, 2, PACK * CHUNKS[c] // 2], BF16, name="e_grouped", bufs=3, align_bytes=64)
                 e_grouped[c] = grouped
             return e_grouped[c]
 
         def empty_sums(c, j):
-            if exists(c, j):
+            if exists(c, PAIR * j):
                 nc.scalar.copy(
                     out=event_features(c)[:, 1, BANK * j : BANK * (j + 1)].rearrange("p (n t) -> p n t", t=PACK),
                     in_=sums[c, j][:].rearrange("p t n -> p n t"),
                 )
 
-        def turn_rows(chunks, bank):
-            if exists(chunks[0]):
-                i, e0 = place(chunks[0])
+        def turn_rows(c, b):
+            if exists(c, BANK * b):
+                i, e0 = divmod(first_event[c] + BANK * b, LOAD)
                 words = event_rows[i][:].rearrange("p r k -> p (r k)").bitcast(F32)
-                pt = psum.tile([P, 2, 2, P], F32, name=bank, bufs=1)
-                for j in range(2):
+                pt = new_bank("pt", [P, min(BANK, CHUNKS[c]) // PAIR, 2, P], F32)
+                turned_rows[c, b] = pt
+                for j in range(pt.shape[1]):
                     w0 = e0 + HIDDEN * j
                     for u in range(2):
                         nc.tensor.transpose(pt[:, j, u, :], words[:, w0 + u : w0 + HIDDEN : 2], identity[:])
-                for c in chunks:
-                    j = (first_event[c] - first_event[chunks[0]]) // PAIR
-                    turned_rows[c] = pt[:, j : j + CHUNKS[c] // PAIR]
 
-        def empty_rows(c):
-            if exists(c):
+        def empty_rows(c, b):
+            if exists(c, BANK * b):
+                pt = turned_rows[c, b]
+                words = event_features(c)[:, 0, :].bitcast(F32)[:, BANK * b : BANK * b + PAIR * pt.shape[1]]
                 nc.scalar.copy(
-                    out=event_features(c)[:, 0, :].bitcast(F32).rearrange("p (j n u) -> p j n u", n=P, u=2),
-                    in_=turned_rows[c].rearrange("p j u n -> p j n u"),
+                    out=words.rearrange("p (j n u) -> p j n u", n=P, u=2), in_=pt[:].rearrange("p j u n -> p j n u")
                 )
 
-        def quantize_features(c):
-            if exists(c):
-                codes = work.tile([P, CHUNKS[c]], U32, name="e_codes", bufs=3, align_bytes=64)
-                scales = work.tile([P, CHUNKS[c]], U8, name="e_scales", bufs=3, align_bytes=64)
+        def quantize_features(c, columns):
+            if c not in e_codes:
+                codes = work.tile([P, CHUNK], U32, name="e_codes", bufs=2, align_bytes=64)
+                scales = work.tile([P, CHUNK], U8, name="e_scales", bufs=2, align_bytes=64)
                 e_codes[c], e_scales[c] = codes, scales
-                nc.vector.quantize_mx(
-                    out=codes[:].bitcast(FP8X4), scales=scales[:], in_=e_grouped[c][:].rearrange("p h n -> p (h n)")
+            nc.vector.quantize_mx(
+                out=e_codes[c][:, columns].bitcast(FP8X4),
+                scales=e_scales[c][:, columns],
+                in_=e_grouped[c][:].rearrange("p h (n t) -> p (h n) t", t=PACK)[:, columns].rearrange("p n t -> p (n t)"),
+            )
+
+        def weight_form(side, half):
+            return weight[:, 2 * side + half, :].bitcast(FP4X4), weight_scales[:, 2 * side + half, :]
+
+        def features(c, half, first, width):
+            columns = slice(half * CHUNK // 2 + first, half * CHUNK // 2 + first + width)
+            return e_codes[c][:, columns].bitcast(FP8X4), e_scales[c][:, columns]
+
+        def project(to, still, moving):
+            for half in range(2):
+                nc.tensor.matmul_mx(
+                    out=to,
+                    lhsT=still[half][0],
+                    lhsT_scale=still[half][1],
+                    rhs=moving[half][0],
+                    rhs_scale=moving[half][1],
+                    start=(half == 0),
+                    stop=(half == 1),
                 )
 
-        def project(c):
-            if exists(c):
-                bank, bufs = ("pt", 1) if c == n_chunks - 1 else ("po", 2)
-                po = psum.tile([P, CHUNKS[c] // P, OUT], F32, name=bank, bufs=bufs)
-                products[c] = po
-                for r in range(CHUNKS[c] // P):
-                    j, side = divmod(r, 2)
-                    for half in range(2):
-                        c0 = half * CHUNKS[c] // 2 + P * j
-                        events = e_codes[c][:, c0 : c0 + P].bitcast(FP8X4), e_scales[c][:, c0 : c0 + P]
-                        form = weight[:, 2 * side + half, :].bitcast(FP4X4), weight_scales[:, 2 * side + half, :]
-                        still, moving = (events, form) if c >= n_chunks - DIRECT else (form, events)
-                        nc.tensor.matmul_mx(
-                            out=po[:, r, :],
-                            lhsT=still[0],
-                            lhsT_scale=still[1],
-                            rhs=moving[0],
-                            rhs_scale=moving[1],
-                            start=(half == 0),
-                            stop=(half == 1),
-                        )
+        def project_side(c, side):
+            po = new_bank("po", [P, BANK // P, P], F32)
+            products[c, side] = po
+            project(
+                po[:].rearrange("p j n -> p (j n)"),
+                [weight_form(side, half) for half in range(2)],
+                [features(c, half, 0, BANK) for half in range(2)],
+            )
 
-        def new_result(c):
-            result = keep.tile([P, CHUNKS[c] // P, OUT], F32, name="result_%d" % c)
-            results[c] = result
+        def project_pairs(c, pairs, use):
+            po = new_bank(use, [P, 2 * len(pairs), OUT], F32)
+            products[c, pairs] = po
+            for r in range(2 * len(pairs)):
+                project(
+                    po[:, r, :],
+                    [features(c, half, P * pairs[r // 2], P) for half in range(2)],
+                    [weight_form(r % 2, half) for half in range(2)],
+                )
+
+        def new_result(key, sets):
+            result = work.tile([P, sets, OUT], F32, name="result", bufs=5)
+            results[key] = result
             return result
 
-        def store(c):
-            events = slice(first_event[c], first_event[c] + CHUNKS[c])
-            order = "(r i) k -> i r k" if c >= n_chunks - DIRECT else "(i r) k -> i r k"
-            nc.sync.dma_start(out=out[events, :].rearrange(order, i=P), in_=results[c][:])
+        def empty_side(c, side):
+            finished = work.tile([P, BANK // P, P], F32, name="channels", bufs=3)
+            channels[c, side] = finished
+            nc.scalar.activation(out=finished[:], in_=products[c, side][:], func=RELU, bias=bias_column[:])
 
-        def empty_products(c):
-            if exists(c) and c >= n_chunks - DIRECT:
-                result = new_result(c)
-                bias = bias_rows[:].broadcast_to([P, CHUNKS[c] // P, OUT])
-                nc.vector.tensor_tensor(out=result[:], in0=products[c][:], in1=bias, op=ALU.add)
-            elif exists(c):
-                finished = work.tile([P, CHUNKS[c] // P, P], F32, name="channels", bufs=2)
-                channels[c] = finished
-                by_event = products[c][:].rearrange("p r i -> p (r i)").rearrange("p (i r) -> p r i", i=P)
-                nc.scalar.activation(out=finished[:], in_=by_event, func=RELU, bias=bias_column[:])
+        def add_bias(c, pairs):
+            bias = bias_rows[:].broadcast_to([P, 2 * len(pairs), OUT])
+            nc.vector.tensor_tensor(
+                out=new_result((c, pairs), 2 * len(pairs))[:], in0=products[c, pairs][:], in1=bias, op=ALU.add
+            )
 
-        def rectify(c):
-            nc.vector.tensor_scalar(out=results[c][:], in0=results[c][:], scalar1=0.0, scalar2=None, op0=ALU.max)
-            store(c)
+        def rectify(c, pairs):
+            result = results[c, pairs]
+            nc.vector.tensor_scalar(out=result[:], in0=result[:], scalar1=0.0, scalar2=None, op0=ALU.max)
+            rows = out[CHUNK * c + PAIR * pairs[0] : CHUNK * c + PAIR * (pairs[-1] + 1), :]
+            nc.sync.dma_start(out=rows.rearrange("(r i) k -> i r k", i=P), in_=result[:])
 
-        def turn_channels(c):
-            if c in channels:
-                pz = psum.tile([P, CHUNKS[c] // P, OUT], F32, name="pz", bufs=1)
-                turned_channels[c] = pz
-                for r in range(CHUNKS[c] // P):
-                    nc.tensor.transpose(pz[:, r, :], channels[c][:, r, :], identity[:])
+        def turn_channels(c, b):
+            if (c, b) in channels:
+                pz = new_bank("pt", [P, BANK // P, OUT], F32)
+                turned_channels[c, b] = pz
+                for r in range(BANK // P):
+                    nc.tensor.transpose(pz[:, r, :], channels[c, b][:, r, :], identity[:])
 
-        def empty_channels(c):
-            if c in turned_channels:
-                nc.scalar.copy(out=new_result(c)[:], in_=turned_channels[c][:])
-                store(c)
+        def empty_channels(c, side):
+            if (c, side) in turned_channels:
+                nc.scalar.copy(out=new_result((c, side), BANK // P)[:], in_=turned_channels[c, side][:])
+                rows = out[CHUNK * c : CHUNK * (c + 1), :].rearrange("(j side i) k -> side i j k", side=2, i=P)
+                nc.sync.dma_start(out=rows[side], in_=results[c, side][:])
 
 
         last = n_chunks - 1
 
-        def widen_next(widen_quarter, c, quarter):
-            widen_quarter(c + 1, quarter)
-            if c + 2 == last:
-                widen_quarter(last, quarter)
-
-        for plane in range(0, PLANES, 2):
-            widen(0, plane)
-            widen(1, plane + 1)
-            widen(0, plane + 1)
-            widen(1, plane)
-            if plane == 2:
-                weave(0, 0, 0, "po")
-                weave(0, 0, 1, "po")
-        weave(1, 0, 1, "pz")
-        weave(1, 0, 0, "pw")
-        empty_weave(0, 0, 0)
+        for n in range(2):
+            widen(0, VECTOR, n)
+            widen(0, SCALAR, n)
+        weave(0, 0, "po")
+        weave(0, 1, "po")
+        weave(0, 2, "pt")
+        weave(0, 3, "pw")
+        widen(0, SCALAR, 2)
+        for n in range(2, 5):
+            widen(0, VECTOR, n)
+        empty_weave(0, 0)
         group_nodes(0)
-        empty_weave(0, 0, 1)
         group_nodes(1)
-        interleave(0, 1)
-        interleave(1, 1)
-        quantize_events(0, 0)
-        quantize_events(0, 1)
+        empty_weave(0, 1)
+        interleave(0, 1, slice(0, CHUNK))
         quantize_nodes()
-        empty_weave(1, 0, 1)
-        turn_rows((0,), "pt")
-        pool_nodes(0, 0)
+        empty_weave(0, 2)
+        empty_weave(0, 3)
+        quantize_events(0, 1)
+        turn_rows(0, 0)
+        turn_rows(0, 1)
+        for j in range(3):
+            pool_nodes(0, j, 1)
+        quantize_events(0, 0)
+        widen(1, SCALAR, 0)
+        widen(1, SCALAR, 1)
+        empty_rows(0, 0)
+        empty_rows(0, 1)
+        for j in range(3):
+            pool_nodes(0, j, 0)
+        widen(1, SCALAR, 2)
+        empty_sums(0, 0)
+        widen(1, SCALAR, 3)
+        for n in range(5):
+            widen(1, VECTOR, n)
 
-        for c in range(1, last - 1):
-            if c > 1:
-                interleave(c, 1)
-            widen_next(widen_scalar, c, 0)
-            if c > 1:
-                weave(c, 0, 0, "pw")
-            pool_nodes(c - 1, 1)
-            empty_rows(c - 1)
-            empty_weave(c, 0, 0)
-            interleave(c, 0)
-            widen_next(widen_scalar, c, 1)
-            project(c - 2)
-            empty_sums(c - 1, 0)
-            widen_next(widen_vector, c, 0)
-            quantize_events(c, 1)
-            widen_next(widen_vector, c, 1)
-            quantize_events(c, 0)
-            widen_next(widen_scalar, c, 2)
-            turn_channels(c - 3)
-            turn_rows((c,), "pt")
-            if c + 2 == last:
-                turn_rows((c + 1, last), "pw")
+        for c in range(1, last):
+            load_bytes(c + AHEAD - 1, 0)
+            load_bytes(c + AHEAD - 1, 1)
+            load_rows(c + AHEAD - 1)
+            interleave(c, 1, slice(0, CHUNK))
+            pool_nodes(c - 1, 3, 1)
+            pool_nodes(c - 1, 3, 0)
             empty_sums(c - 1, 1)
-            empty_products(c - 2)
-            pool_nodes(c, 0)
-            widen_next(widen_scalar, c, 3)
-            empty_channels(c - 3)
-            widen_next(widen_vector, c, 2)
-            widen_next(widen_vector, c, 3)
-            quantize_features(c - 1)
+            empty_sums(c - 1, 2)
+            widen(c + 1, SCALAR, 0)
+            turn_channels(c - 2, 0)
+            turn_channels(c - 2, 1)
+            if c == 1:
+                turn_rows(c, 0)
+                turn_rows(c, 1)
+            weave(c, 0, "pw")
+            empty_sums(c - 1, 3)
+            widen(c + 1, VECTOR, 0)
+            quantize_events(c, 1)
+            quantize_features(c - 1, slice(0, CHUNK))
+            empty_channels(c - 2, 0)
+            empty_channels(c - 2, 1)
+            if c == 1:
+                empty_rows(c, 0)
+                empty_rows(c, 1)
+            empty_weave(c, 0)
+            for j in range(3):
+                pool_nodes(c, j, 1)
+            project_side(c - 1, 0)
+            project_side(c - 1, 1)
+            turn_rows(c + 1, 0)
+            turn_rows(c + 1, 1)
+            interleave(c, 0, slice(woven(c, 0), CHUNK))
+            widen(c + 1, VECTOR, 1)
+            quantize_events(c, 0)
+            widen(c + 1, SCALAR, 1)
+            widen(c + 1, SCALAR, 2)
+            empty_side(c - 1, 0)
+            empty_side(c - 1, 1)
+            empty_rows(c + 1, 0)
+            empty_rows(c + 1, 1)
+            for j in range(3):
+                pool_nodes(c, j, 0)
+            empty_sums(c, 0)
+            widen(c + 1, SCALAR, 3)
+            widen(c + 1, VECTOR, 2)
+            widen(c + 1, VECTOR, 3)
+            widen(c + 1, VECTOR, 4)
 
-        a, b = last - 1, last
-        interleave(a, 1)
-        interleave(a, 0)
-        pool_nodes(a - 1, 1)
-        empty_rows(a - 1)
-        empty_sums(a - 1, 0)
-        quantize_events(a, 1)
-        quantize_events(a, 0)
-        interleave(b, 1)
-        interleave(b, 0)
-        project(a - 2)
-        turn_channels(a - 3)
-        empty_sums(a - 1, 1)
-        empty_products(a - 2)
-        empty_channels(a - 3)
-        pool_nodes(a, 0)
-        quantize_events(b, 1)
-        quantize_events(b, 0)
-        quantize_features(a - 1)
-        empty_rows(a)
-        empty_rows(b)
-        empty_sums(a, 0)
-        pool_nodes(b, 0)
-        project(a - 1)
-        quantize_features(a)
-        turn_channels(a - 2)
-        empty_sums(b, 0)
-        empty_channels(a - 2)
-        project(a)
-        quantize_features(b)
-        empty_products(a - 1)
-        project(b)
-        empty_products(a)
-        rectify(a - 1)
-        empty_products(b)
-        rectify(a)
-        rectify(b)
+        c = last
+        parts = ((0, 1), (2,), (3,))
+        events = [slice(PAIR * part[0], PAIR * (part[-1] + 1)) for part in parts]
+        sum_columns = [slice(BANK + P * part[0], BANK + P * (part[-1] + 1)) for part in parts]
+
+        def pool_pair(j):
+            for g in (1, 0):
+                pool_nodes(c, j, g)
+
+        for g in (1, 0):
+            interleave(c, g, events[0])
+        for g in (1, 0):
+            quantize_events(c, g, events[0])
+        pool_nodes(c - 1, 3, 1)
+        pool_nodes(c - 1, 3, 0)
+        empty_sums(c - 1, 1)
+        empty_sums(c - 1, 2)
+        turn_channels(c - 2, 0)
+        turn_channels(c - 2, 1)
+        empty_sums(c - 1, 3)
+        quantize_features(c - 1, slice(0, CHUNK))
+        empty_channels(c - 2, 0)
+        empty_channels(c - 2, 1)
+        pool_pair(0)
+        pool_pair(1)
+        interleave(c, 1, events[1])
+        interleave(c, 0, events[1])
+        for g in (1, 0):
+            quantize_events(c, g, events[1])
+        project_side(c - 1, 0)
+        project_side(c - 1, 1)
+        empty_sums(c, 0)
+        empty_sums(c, 1)
+        empty_side(c - 1, 0)
+        empty_side(c - 1, 1)
+        pool_pair(2)
+        interleave(c, 1, events[2])
+        interleave(c, 0, events[2])
+        quantize_events(c, 1, events[2])
+        quantize_events(c, 0, events[2])
+        turn_channels(c - 1, 0)
+        turn_channels(c - 1, 1)
+        empty_sums(c, 2)
+        pool_pair(3)
+        quantize_features(c, slice(0, BANK))
+        quantize_features(c, sum_columns[0])
+        quantize_features(c, sum_columns[1])
+        empty_channels(c - 1, 0)
+        empty_channels(c - 1, 1)
+        project_pairs(c, parts[0], "po")
+        empty_sums(c, 3)
+        project_pairs(c, parts[1], "po")
+        add_bias(c, parts[0])
+        quantize_features(c, sum_columns[2])
+        rectify(c, parts[0])
+        project_pairs(c, parts[2], "pw")
+        add_bias(c, parts[1])
+        add_bias(c, parts[2])
+        rectify(c, parts[1])
+        rectify(c, parts[2])

@@ -39,8 +39,8 @@ FLOPS = 2 * NODES * EVENTS * HIDDEN + 2 * EVENTS * 2 * HIDDEN * OUT
 
 def shares(c):
     if c == 0:
-        return [(plane, 0, CHUNK) for plane in (1, 3, 5)], [(plane, 0, CHUNK) for plane in (0, 2, 4, 6, 7)]
-    split = 512 if c == 1 else 512 if c == len(CHUNKS) - 1 else 512
+        return [(plane, 0, CHUNK) for plane in (1, 5, 7)], [(plane, 0, CHUNK) for plane in (0, 2, 3, 4, 6)]
+    split = 640 if c == 1 else 256 if c == len(CHUNKS) - 1 else 256
     whole = [(plane, 0, CHUNK) for plane in range(PLANES)]
     return [(4, 0, split)] + whole[:3], whole[:4:-1] + [(4, split, CHUNK), whole[3]]
 
@@ -48,7 +48,7 @@ def shares(c):
 def woven(c, g):
     if g == 1 or c == len(CHUNKS) - 1:
         return 0
-    return CHUNK if c == 0 else PAIR
+    return CHUNK if c == 0 else 3 * P
 
 
 def tile_mymodel_icdm_pa_t_w4_kernel(
@@ -187,7 +187,7 @@ def tile_mymodel_icdm_pa_t_w4_kernel(
             )
 
         def weave(c, j, use):
-            if exists(c) and woven(c, 0) > PAIR * j:
+            if woven(c, 0) > PAIR * j:
                 n = min(PAIR, woven(c, 0) - PAIR * j)
                 pw = new_bank(use, [P, n, PACK], BF16)
                 weaves[c, j] = pw
@@ -354,16 +354,17 @@ def tile_mymodel_icdm_pa_t_w4_kernel(
 
         last = n_chunks - 1
 
-        for n in range(2):
+        widen(0, SCALAR, 0)
+        for n in range(3):
             widen(0, VECTOR, n)
-            widen(0, SCALAR, n)
         weave(0, 0, "po")
         weave(0, 1, "po")
         weave(0, 2, "pt")
         weave(0, 3, "pw")
+        widen(0, SCALAR, 1)
         widen(0, SCALAR, 2)
-        for n in range(2, 5):
-            widen(0, VECTOR, n)
+        widen(0, VECTOR, 3)
+        widen(0, VECTOR, 4)
         empty_weave(0, 0)
         group_nodes(0)
         group_nodes(1)
@@ -371,6 +372,7 @@ def tile_mymodel_icdm_pa_t_w4_kernel(
         interleave(0, 1, slice(0, CHUNK))
         quantize_nodes()
         empty_weave(0, 2)
+        widen(1, SCALAR, 1)
         empty_weave(0, 3)
         quantize_events(0, 1)
         turn_rows(0, 0)
@@ -378,13 +380,12 @@ def tile_mymodel_icdm_pa_t_w4_kernel(
         for j in range(3):
             pool_nodes(0, j, 1)
         quantize_events(0, 0)
-        widen(1, SCALAR, 0)
-        widen(1, SCALAR, 1)
+        widen(1, SCALAR, 2)
         empty_rows(0, 0)
         empty_rows(0, 1)
         for j in range(3):
             pool_nodes(0, j, 0)
-        widen(1, SCALAR, 2)
+        widen(1, SCALAR, 0)
         empty_sums(0, 0)
         widen(1, SCALAR, 3)
         for n in range(5):
@@ -406,6 +407,7 @@ def tile_mymodel_icdm_pa_t_w4_kernel(
                 turn_rows(c, 0)
                 turn_rows(c, 1)
             weave(c, 0, "pw")
+            weave(c, 1, "po")
             empty_sums(c - 1, 3)
             widen(c + 1, VECTOR, 0)
             quantize_events(c, 1)
@@ -416,6 +418,7 @@ def tile_mymodel_icdm_pa_t_w4_kernel(
                 empty_rows(c, 0)
                 empty_rows(c, 1)
             empty_weave(c, 0)
+            empty_weave(c, 1)
             for j in range(3):
                 pool_nodes(c, j, 1)
             project_side(c - 1, 0)
@@ -448,10 +451,12 @@ def tile_mymodel_icdm_pa_t_w4_kernel(
             for g in (1, 0):
                 pool_nodes(c, j, g)
 
-        for g in (1, 0):
-            interleave(c, g, events[0])
-        for g in (1, 0):
-            quantize_events(c, g, events[0])
+        pair_0, pair_1 = slice(0, PAIR), slice(PAIR, 2 * PAIR)
+        interleave(c, 1, events[0])
+        interleave(c, 0, pair_0)
+        quantize_events(c, 1, events[0])
+        quantize_events(c, 0, pair_0)
+        interleave(c, 0, pair_1)
         pool_nodes(c - 1, 3, 1)
         pool_nodes(c - 1, 3, 0)
         empty_sums(c - 1, 1)
@@ -459,12 +464,13 @@ def tile_mymodel_icdm_pa_t_w4_kernel(
         turn_channels(c - 2, 0)
         turn_channels(c - 2, 1)
         empty_sums(c - 1, 3)
+        interleave(c, 1, events[1])
+        quantize_events(c, 0, pair_1)
         quantize_features(c - 1, slice(0, CHUNK))
         empty_channels(c - 2, 0)
         empty_channels(c - 2, 1)
         pool_pair(0)
         pool_pair(1)
-        interleave(c, 1, events[1])
         interleave(c, 0, events[1])
         for g in (1, 0):
             quantize_events(c, g, events[1])

@@ -21,42 +21,43 @@ P = 128
 PACK = 4
 PASS = P * PACK
 GROUPS = NODES // PASS
+PLANES = GROUPS * PACK
 PAIR = 2 * P
 QUADS = HIDDEN // PACK
 BANK = 512
-PLANES = GROUPS * PACK
+PAIRS = 4
+CHUNK = PAIRS * PAIR
+LAST = EVENTS // CHUNK - 1
+WHOLE = slice(0, CHUNK)
 
-CHUNKS = (4 * PAIR,) * 8
-CHUNK = 4 * PAIR
-LOAD = 4 * PAIR
-AHEAD = 3
-DIRECT = 1
-BANKS = {"ps": 3, "po": 2, "pt": 2, "pw": 1}
+AHEAD = 2
+WOVEN = 352
+SPLIT = 320
+LAST_SPLIT = 384
+BANKS = {"sums": 3, "products": 2, "turned": 2, "woven": 1}
 SCALAR, VECTOR = 0, 1
 
 FLOPS = 2 * NODES * EVENTS * HIDDEN + 2 * EVENTS * 2 * HIDDEN * OUT
 
 
 def shares(c):
-    if c == 0:
-        return [(plane, 0, CHUNK) for plane in (1, 5, 7)], [(plane, 0, CHUNK) for plane in (0, 2, 3, 4, 6)]
-    split = 640 if c == 1 else 256 if c == len(CHUNKS) - 1 else 256
     whole = [(plane, 0, CHUNK) for plane in range(PLANES)]
+    if c == 0:
+        return [whole[4], whole[6]], whole[:4] + [whole[5], whole[7]]
+    if c == 1:
+        return [whole[4]] + whole[:3], whole[:4:-1] + [whole[3]]
+    split = LAST_SPLIT if c == LAST else SPLIT
     return [(4, 0, split)] + whole[:3], whole[:4:-1] + [(4, split, CHUNK), whole[3]]
 
 
-def woven(c, g):
-    if g == 1 or c == len(CHUNKS) - 1:
-        return 0
-    return CHUNK if c == 0 else 3 * P
+def woven(c):
+    return CHUNK if c == 0 else WOVEN
 
 
 def tile_mymodel_icdm_pa_t_w4_kernel(
     tc, H_A_bytes, H_A_scale, H_mean_A, H_mean_M, wEA1_words, wEA1_scales, bEA1, out
 ):
     nc = tc.nc
-    n_chunks = len(CHUNKS)
-    first_event = [sum(CHUNKS[:c]) for c in range(n_chunks)]
 
     with ExitStack() as ctx:
         keep = ctx.enter_context(tc.tile_pool(name="keep", bufs=1))
@@ -81,6 +82,7 @@ def tile_mymodel_icdm_pa_t_w4_kernel(
 
         bias_column = keep.tile([P, 1], BF16, name="bias_column")
         bias_rows = keep.tile([P, 1, OUT], BF16, name="bias_rows")
+
         identity = keep.tile([P, P], F32, name="identity")
         make_identity(nc, identity[:])
         identity_bf = keep.tile([P, P], BF16, name="identity_bf")
@@ -90,23 +92,22 @@ def tile_mymodel_icdm_pa_t_w4_kernel(
         event_bytes = {}
         event_rows = {}
 
-        def load_bytes(i, g):
-            if LOAD * i < EVENTS:
-                raw = work.tile([P, PACK, LOAD], U8, name="event_bytes", bufs=2 * (AHEAD + 1), align_bytes=64)
-                event_bytes[i, g] = raw
-                source = H_A_bytes[PASS * g : PASS * (g + 1), LOAD * i : LOAD * (i + 1)].rearrange("(p t) e -> p t e", t=PACK)
-                for planes in (slice(0, 2), slice(2, 4)) if i == 0 else (slice(0, 4),):
-                    nc.sync.dma_start(out=raw[:, planes, :], in_=source[:, planes, :])
+        def load_bytes(c, g, cuts=(0, PACK)):
+            raw = work.tile([P, PACK, CHUNK], U8, name="event_bytes", bufs=GROUPS * (AHEAD + 2), align_bytes=64)
+            event_bytes[c, g] = raw
+            source = H_A_bytes[PASS * g : PASS * (g + 1), CHUNK * c : CHUNK * (c + 1)]
+            for planes in map(slice, cuts, cuts[1:]):
+                nc.sync.dma_start(out=raw[:, planes, :], in_=source.rearrange("(p t) e -> p t e", t=PACK)[:, planes, :])
 
-        def load_rows(i):
-            if LOAD * i < EVENTS:
-                rows = work.tile([P, LOAD // P, HIDDEN], BF16, name="event_rows", bufs=AHEAD + 1, align_bytes=64)
-                event_rows[i] = rows
-                nc.sync.dma_start(out=rows[:], in_=H_mean_M[LOAD * i : LOAD * (i + 1), :].rearrange("(r i) k -> i r k", i=P))
+        def load_rows(c):
+            rows = work.tile([P, CHUNK // P, HIDDEN], BF16, name="event_rows", bufs=AHEAD + 2, align_bytes=64)
+            event_rows[c] = rows
+            source = H_mean_M[CHUNK * c : CHUNK * (c + 1), :]
+            nc.sync.dma_start(out=rows[:], in_=source.rearrange("(r i) k -> i r k", i=P))
 
+        load_bytes(0, 0, cuts=(0, 1, 2, PACK))
+        load_bytes(0, 1, cuts=(0, 2, PACK))
         node_rows = keep.tile([P, GROUPS, PACK, HIDDEN], BF16, name="node_rows", align_bytes=64)
-        load_bytes(0, 0)
-        load_bytes(0, 1)
         nc.sync.dma_start(out=node_rows[:], in_=H_mean_A.rearrange("(g p j) c -> p g j c", p=P, j=PACK))
         load_bytes(1, 0)
         load_rows(0)
@@ -130,40 +131,36 @@ def tile_mymodel_icdm_pa_t_w4_kernel(
         load_rows(2)
         nc.sync.dma_start(out=bias_rows[:, 0, :], in_=bEA1.partition_broadcast(P))
 
+
         node_grouped = keep.tile([P, GROUPS, PACK, QUADS, PACK], BF16, name="node_grouped", align_bytes=64)
 
-        def group_nodes(g):
-            copy = nc.scalar.copy if g else nc.vector.tensor_copy
+        def group_nodes(g, copy):
             copy(out=node_grouped[:, g], in_=node_rows[:, g].rearrange("p j (q t) -> p t q j", t=PACK))
 
         def quantize_nodes():
-            for g in range(GROUPS):
-                for t in range(PACK):
-                    c0 = (2 * (PACK * g + t) + 1) * QUADS
-                    nc.vector.quantize_mx(
-                        out=node_codes[:, c0 : c0 + QUADS].bitcast(FP8X4),
-                        scales=node_scales[:, c0 : c0 + QUADS],
-                        in_=node_grouped[:, g, t].rearrange("p q j -> p (q j)"),
-                    )
+            for plane in range(PLANES):
+                g, t = divmod(plane, PACK)
+                block = slice((2 * plane + 1) * QUADS, (2 * plane + 2) * QUADS)
+                nc.vector.quantize_mx(
+                    out=node_codes[:, block].bitcast(FP8X4),
+                    scales=node_scales[:, block],
+                    in_=node_grouped[:, g, t].rearrange("p q j -> p (q j)"),
+                )
 
 
         wide, weaves, h_grouped, h_codes, h_scales = {}, {}, {}, {}, {}
         sums, turned_rows, e_grouped, e_codes, e_scales = {}, {}, {}, {}, {}
         products, channels, turned_channels, results = {}, {}, {}, {}
 
-        def exists(c, first=0):
-            return 0 <= c < n_chunks and first < CHUNKS[c]
-
         def new_bank(use, shape, dtype):
             bank = psum.tile(shape, dtype, name=use, bufs=BANKS[use])
             return bank
 
-        def widen(c, engine, n):
-            if exists(c) and n < len(shares(c)[engine]):
-                plane, e0, e1 = shares(c)[engine][n]
+        def widen(c, engine, items):
+            for plane, e0, e1 in shares(c)[engine][items]:
                 g, t = divmod(plane, PACK)
                 if (c, g) not in wide:
-                    planes = work.tile([P, PACK, CHUNK], BF16, name="wide", bufs=4, align_bytes=64)
+                    planes = work.tile([P, PACK, CHUNK], BF16, name="wide", bufs=2 * GROUPS, align_bytes=64)
                     wide[c, g] = planes
                 values = event_bytes[c, g][:, t, e0:e1].bitcast(FP8)
                 scale = plane_scales[:, g, t : t + 1]
@@ -174,98 +171,103 @@ def tile_mymodel_icdm_pa_t_w4_kernel(
                         out=wide[c, g][:, t, e0:e1], in0=values, scalar1=scale, scalar2=None, op0=ALU.mult
                     )
 
+        def item(n):
+            return slice(n, n + 1)
+
         def grouped_events(c, g):
             if (c, g) not in h_grouped:
-                grouped = work.tile([P, CHUNKS[c], PACK], BF16, name="h_grouped", bufs=3, align_bytes=64)
+                grouped = work.tile([P, CHUNK, PACK], BF16, name="h_grouped", bufs=GROUPS + 1, align_bytes=64)
                 h_grouped[c, g] = grouped
             return h_grouped[c, g]
 
-        def interleave(c, g, events, copy=nc.vector.tensor_copy):
-            copy(
+        def interleave(c, g, events):
+            nc.vector.tensor_copy(
                 out=grouped_events(c, g)[:, events, :].rearrange("p (e i) t -> p e t i", i=4),
                 in_=wide[c, g][:, :, events].rearrange("p t (e i) -> p e t i", i=4),
             )
 
         def weave(c, j, use):
-            if woven(c, 0) > PAIR * j:
-                n = min(PAIR, woven(c, 0) - PAIR * j)
-                pw = new_bank(use, [P, n, PACK], BF16)
-                weaves[c, j] = pw
-                for e0 in range(0, n, P):
-                    nc.tensor.matmul(
-                        out=pw[:, e0 : e0 + P, :].rearrange("p e t -> p t e"),
-                        lhsT=identity_bf[:],
-                        rhs=wide[c, 0][:, :, PAIR * j + e0 : PAIR * j + e0 + P],
-                        start=True,
-                        stop=True,
-                    )
-
-        def empty_weave(c, j):
-            if (c, j) in weaves:
-                pw = weaves[c, j]
-                nc.scalar.copy(out=grouped_events(c, 0)[:, PAIR * j : PAIR * j + pw.shape[1], :], in_=pw[:])
-
-        def quantize_events(c, g, events=slice(None)):
-            if exists(c):
-                if (c, g) not in h_codes:
-                    codes = work.tile([P, CHUNKS[c]], U32, name="h_codes", bufs=4, align_bytes=64)
-                    scales = work.tile([P, CHUNKS[c]], U8, name="h_scales", bufs=4, align_bytes=64)
-                    h_codes[c, g], h_scales[c, g] = codes, scales
-                nc.vector.quantize_mx(
-                    out=h_codes[c, g][:, events].bitcast(FP8X4),
-                    scales=h_scales[c, g][:, events],
-                    in_=h_grouped[c, g][:, events, :].rearrange("p e t -> p (e t)"),
+            n = min(PAIR, woven(c) - PAIR * j)
+            bank = new_bank(use, [P, n, PACK], BF16)
+            weaves[c, j] = bank
+            for e0 in range(0, n, P):
+                e1 = min(n, e0 + P)
+                nc.tensor.matmul(
+                    out=bank[:, e0:e1, :].rearrange("p e t -> p t e"),
+                    lhsT=identity_bf[:],
+                    rhs=wide[c, 0][:, :, PAIR * j + e0 : PAIR * j + e1],
+                    start=True,
+                    stop=True,
                 )
 
+        def empty_weave(c, j):
+            bank = weaves[c, j]
+            nc.scalar.copy(out=grouped_events(c, 0)[:, PAIR * j : PAIR * j + bank.shape[1], :], in_=bank[:])
+
+        def quantize_events(c, g, events):
+            if (c, g) not in h_codes:
+                codes = work.tile([P, CHUNK], U32, name="h_codes", bufs=2 * GROUPS, align_bytes=64)
+                scales = work.tile([P, CHUNK], U8, name="h_scales", bufs=2 * GROUPS, align_bytes=64)
+                h_codes[c, g], h_scales[c, g] = codes, scales
+            nc.vector.quantize_mx(
+                out=h_codes[c, g][:, events].bitcast(FP8X4),
+                scales=h_scales[c, g][:, events],
+                in_=h_grouped[c, g][:, events, :].rearrange("p e t -> p (e t)"),
+            )
+
         def pool_nodes(c, j, g):
-            if exists(c, PAIR * j):
-                if g == 1:
-                    sums[c, j] = new_bank("ps", [P, PACK, P], F32)
-                for t in range(PACK):
-                    for side in range(2):
-                        cols = slice(PAIR * j + P * side, PAIR * j + P * (side + 1))
-                        c0 = (2 * (PACK * g + t) + 1 - side) * QUADS
-                        nc.tensor.matmul_mx(
-                            out=sums[c, j][:, t, :],
-                            lhsT=node_codes[:, c0 : c0 + P].bitcast(FP8X4),
-                            lhsT_scale=node_scales[:, c0 : c0 + P],
-                            rhs=h_codes[c, g][:, cols].bitcast(FP8X4),
-                            rhs_scale=h_scales[c, g][:, cols],
-                            start=(g == 1 and t == 0 and side == 0),
-                            stop=(g == 0 and t == PACK - 1 and side == 1),
-                        )
+            if g == 1:
+                sums[c, j] = new_bank("sums", [P, PACK, P], F32)
+            for t in range(PACK):
+                for side in range(2):
+                    events = slice(PAIR * j + P * side, PAIR * j + P * (side + 1))
+                    c0 = (2 * (PACK * g + t) + 1 - side) * QUADS
+                    nc.tensor.matmul_mx(
+                        out=sums[c, j][:, t, :],
+                        lhsT=node_codes[:, c0 : c0 + P].bitcast(FP8X4),
+                        lhsT_scale=node_scales[:, c0 : c0 + P],
+                        rhs=h_codes[c, g][:, events].bitcast(FP8X4),
+                        rhs_scale=h_scales[c, g][:, events],
+                        start=(g == 1 and t == 0 and side == 0),
+                        stop=(g == 0 and t == PACK - 1 and side == 1),
+                    )
+
+        def pool_pair(c, j):
+            pool_nodes(c, j, 1)
+            pool_nodes(c, j, 0)
 
         def event_features(c):
             if c not in e_grouped:
-                grouped = work.tile([P, 2, PACK * CHUNKS[c] // 2], BF16, name="e_grouped", bufs=3, align_bytes=64)
+                grouped = work.tile([P, 2, PACK * P * PAIRS], BF16, name="e_grouped", bufs=3, align_bytes=64)
                 e_grouped[c] = grouped
             return e_grouped[c]
 
         def empty_sums(c, j):
-            if exists(c, PAIR * j):
-                nc.scalar.copy(
-                    out=event_features(c)[:, 1, BANK * j : BANK * (j + 1)].rearrange("p (n t) -> p n t", t=PACK),
-                    in_=sums[c, j][:].rearrange("p t n -> p n t"),
-                )
+            nc.scalar.copy(
+                out=event_features(c)[:, 1, BANK * j : BANK * (j + 1)].rearrange("p (n t) -> p n t", t=PACK),
+                in_=sums[c, j][:].rearrange("p t n -> p n t"),
+            )
 
-        def turn_rows(c, b):
-            if exists(c, BANK * b):
-                i, e0 = divmod(first_event[c] + BANK * b, LOAD)
-                words = event_rows[i][:].rearrange("p r k -> p (r k)").bitcast(F32)
-                pt = new_bank("pt", [P, min(BANK, CHUNKS[c]) // PAIR, 2, P], F32)
-                turned_rows[c, b] = pt
-                for j in range(pt.shape[1]):
-                    w0 = e0 + HIDDEN * j
+        def turn_rows(c):
+            words = event_rows[c][:].rearrange("p r k -> p (r k)").bitcast(F32)
+            for b in range(2):
+                bank = new_bank("turned", [P, 2, 2, P], F32)
+                turned_rows[c, b] = bank
+                for j in range(2):
+                    w0 = PAIR * (2 * b + j)
                     for u in range(2):
-                        nc.tensor.transpose(pt[:, j, u, :], words[:, w0 + u : w0 + HIDDEN : 2], identity[:])
+                        nc.tensor.transpose(bank[:, j, u, :], words[:, w0 + u : w0 + PAIR : 2], identity[:])
 
-        def empty_rows(c, b):
-            if exists(c, BANK * b):
-                pt = turned_rows[c, b]
-                words = event_features(c)[:, 0, :].bitcast(F32)[:, BANK * b : BANK * b + PAIR * pt.shape[1]]
+        def empty_rows(c):
+            for b in range(2):
+                words = event_features(c)[:, 0, :].bitcast(F32)[:, BANK * b : BANK * (b + 1)]
                 nc.scalar.copy(
-                    out=words.rearrange("p (j n u) -> p j n u", n=P, u=2), in_=pt[:].rearrange("p j u n -> p j n u")
+                    out=words.rearrange("p (j n u) -> p j n u", n=P, u=2),
+                    in_=turned_rows[c, b][:].rearrange("p j u n -> p j n u"),
                 )
+
+        def feature_columns(half, pairs):
+            return slice(P * (PAIRS * half + pairs[0]), P * (PAIRS * half + pairs[-1] + 1))
 
         def quantize_features(c, columns):
             if c not in e_codes:
@@ -278,12 +280,13 @@ def tile_mymodel_icdm_pa_t_w4_kernel(
                 in_=e_grouped[c][:].rearrange("p h (n t) -> p (h n) t", t=PACK)[:, columns].rearrange("p n t -> p (n t)"),
             )
 
-        def weight_form(side, half):
-            return weight[:, 2 * side + half, :].bitcast(FP4X4), weight_scales[:, 2 * side + half, :]
+        def weight_forms(side):
+            forms = (2 * side, 2 * side + 1)
+            return [(weight[:, form, :].bitcast(FP4X4), weight_scales[:, form, :]) for form in forms]
 
-        def features(c, half, first, width):
-            columns = slice(half * CHUNK // 2 + first, half * CHUNK // 2 + first + width)
-            return e_codes[c][:, columns].bitcast(FP8X4), e_scales[c][:, columns]
+        def features(c, pairs):
+            columns = [feature_columns(half, pairs) for half in range(2)]
+            return [(e_codes[c][:, part].bitcast(FP8X4), e_scales[c][:, part]) for part in columns]
 
         def project(to, still, moving):
             for half in range(2):
@@ -297,211 +300,178 @@ def tile_mymodel_icdm_pa_t_w4_kernel(
                     stop=(half == 1),
                 )
 
-        def project_side(c, side):
-            po = new_bank("po", [P, BANK // P, P], F32)
-            products[c, side] = po
-            project(
-                po[:].rearrange("p j n -> p (j n)"),
-                [weight_form(side, half) for half in range(2)],
-                [features(c, half, 0, BANK) for half in range(2)],
-            )
-
-        def project_pairs(c, pairs, use):
-            po = new_bank(use, [P, 2 * len(pairs), OUT], F32)
-            products[c, pairs] = po
-            for r in range(2 * len(pairs)):
-                project(
-                    po[:, r, :],
-                    [features(c, half, P * pairs[r // 2], P) for half in range(2)],
-                    [weight_form(r % 2, half) for half in range(2)],
-                )
-
         def new_result(key, sets):
             result = work.tile([P, sets, OUT], F32, name="result", bufs=5)
             results[key] = result
             return result
 
-        def empty_side(c, side):
-            finished = work.tile([P, BANK // P, P], F32, name="channels", bufs=3)
-            channels[c, side] = finished
-            nc.scalar.activation(out=finished[:], in_=products[c, side][:], func=RELU, bias=bias_column[:])
 
-        def add_bias(c, pairs):
-            bias = bias_rows[:].broadcast_to([P, 2 * len(pairs), OUT])
-            nc.vector.tensor_tensor(
-                out=new_result((c, pairs), 2 * len(pairs))[:], in0=products[c, pairs][:], in1=bias, op=ALU.add
-            )
+        def project_sides(c):
+            for side in range(2):
+                bank = new_bank("products", [P, PAIRS, P], F32)
+                products[c, side] = bank
+                project(bank[:].rearrange("p j n -> p (j n)"), weight_forms(side), features(c, range(PAIRS)))
 
-        def rectify(c, pairs):
-            result = results[c, pairs]
-            nc.vector.tensor_scalar(out=result[:], in0=result[:], scalar1=0.0, scalar2=None, op0=ALU.max)
-            rows = out[CHUNK * c + PAIR * pairs[0] : CHUNK * c + PAIR * (pairs[-1] + 1), :]
-            nc.sync.dma_start(out=rows.rearrange("(r i) k -> i r k", i=P), in_=result[:])
+        def empty_sides(c):
+            for side in range(2):
+                finished = work.tile([P, PAIRS, P], F32, name="channels", bufs=3)
+                channels[c, side] = finished
+                nc.scalar.activation(out=finished[:], in_=products[c, side][:], func=RELU, bias=bias_column[:])
 
-        def turn_channels(c, b):
-            if (c, b) in channels:
-                pz = new_bank("pt", [P, BANK // P, OUT], F32)
-                turned_channels[c, b] = pz
-                for r in range(BANK // P):
-                    nc.tensor.transpose(pz[:, r, :], channels[c, b][:, r, :], identity[:])
+        def turn_channels(c):
+            for side in range(2):
+                bank = new_bank("turned", [P, PAIRS, OUT], F32)
+                turned_channels[c, side] = bank
+                for j in range(PAIRS):
+                    nc.tensor.transpose(bank[:, j, :], channels[c, side][:, j, :], identity[:])
 
-        def empty_channels(c, side):
-            if (c, side) in turned_channels:
-                nc.scalar.copy(out=new_result((c, side), BANK // P)[:], in_=turned_channels[c, side][:])
-                rows = out[CHUNK * c : CHUNK * (c + 1), :].rearrange("(j side i) k -> side i j k", side=2, i=P)
+        def empty_channels(c):
+            rows = out[CHUNK * c : CHUNK * (c + 1), :].rearrange("(j side i) k -> side i j k", side=2, i=P)
+            for side in range(2):
+                nc.scalar.copy(out=new_result((c, side), PAIRS)[:], in_=turned_channels[c, side][:])
                 nc.sync.dma_start(out=rows[side], in_=results[c, side][:])
 
 
-        last = n_chunks - 1
+        def project_pairs(pairs, use):
+            bank = new_bank(use, [P, 2 * len(pairs), OUT], F32)
+            products[pairs] = bank
+            for r in range(2 * len(pairs)):
+                j, side = divmod(r, 2)
+                project(bank[:, r, :], features(LAST, pairs[j : j + 1]), weight_forms(side))
 
-        widen(0, SCALAR, 0)
-        for n in range(3):
-            widen(0, VECTOR, n)
-        weave(0, 0, "po")
-        weave(0, 1, "po")
-        weave(0, 2, "pt")
-        weave(0, 3, "pw")
-        widen(0, SCALAR, 1)
-        widen(0, SCALAR, 2)
-        widen(0, VECTOR, 3)
-        widen(0, VECTOR, 4)
+        def add_bias(pairs):
+            sets = 2 * len(pairs)
+            bias = bias_rows[:].broadcast_to([P, sets, OUT])
+            nc.vector.tensor_tensor(out=new_result(pairs, sets)[:], in0=products[pairs][:], in1=bias, op=ALU.add)
+
+        def rectify(pairs):
+            result = results[pairs]
+            nc.vector.tensor_scalar(out=result[:], in0=result[:], scalar1=0.0, scalar2=None, op0=ALU.max)
+            rows = out[CHUNK * LAST + PAIR * pairs[0] : CHUNK * LAST + PAIR * (pairs[-1] + 1), :]
+            nc.sync.dma_start(out=rows.rearrange("(r i) k -> i r k", i=P), in_=result[:])
+
+
+        widen(0, VECTOR, slice(0, PACK))
+        for j, use in enumerate(("products", "products", "turned", "woven")):
+            weave(0, j, use)
+        for n in range(2):
+            widen(0, SCALAR, item(n))
+            widen(0, VECTOR, item(PACK + n))
         empty_weave(0, 0)
-        group_nodes(0)
-        group_nodes(1)
+        group_nodes(0, nc.vector.tensor_copy)
+        group_nodes(1, nc.scalar.copy)
         empty_weave(0, 1)
-        interleave(0, 1, slice(0, CHUNK))
+        interleave(0, 1, WHOLE)
         quantize_nodes()
         empty_weave(0, 2)
-        widen(1, SCALAR, 1)
+        widen(1, SCALAR, item(1))
         empty_weave(0, 3)
-        quantize_events(0, 1)
-        turn_rows(0, 0)
-        turn_rows(0, 1)
-        for j in range(3):
-            pool_nodes(0, j, 1)
-        quantize_events(0, 0)
-        widen(1, SCALAR, 2)
-        empty_rows(0, 0)
-        empty_rows(0, 1)
-        for j in range(3):
-            pool_nodes(0, j, 0)
-        widen(1, SCALAR, 0)
+        for half in (slice(0, 2 * PAIR), slice(2 * PAIR, CHUNK)):
+            quantize_events(0, 1, half)
+            quantize_events(0, 0, half)
+        turn_rows(0)
+        for g in (1, 0):
+            pool_nodes(0, 0, g)
+            pool_nodes(0, 1, g)
+        widen(1, SCALAR, item(2))
+        empty_rows(0)
+        pool_pair(0, 2)
+        widen(1, SCALAR, item(0))
         empty_sums(0, 0)
-        widen(1, SCALAR, 3)
-        for n in range(5):
-            widen(1, VECTOR, n)
+        widen(1, SCALAR, item(3))
+        widen(1, VECTOR, slice(None))
 
-        for c in range(1, last):
-            load_bytes(c + AHEAD - 1, 0)
-            load_bytes(c + AHEAD - 1, 1)
-            load_rows(c + AHEAD - 1)
-            interleave(c, 1, slice(0, CHUNK))
-            pool_nodes(c - 1, 3, 1)
-            pool_nodes(c - 1, 3, 0)
+
+        for c in range(1, LAST):
+            if c + AHEAD <= LAST:
+                load_bytes(c + AHEAD, 0)
+                load_bytes(c + AHEAD, 1)
+                load_rows(c + AHEAD)
+            interleave(c, 1, WHOLE)
+            pool_pair(c - 1, 3)
             empty_sums(c - 1, 1)
             empty_sums(c - 1, 2)
-            widen(c + 1, SCALAR, 0)
-            turn_channels(c - 2, 0)
-            turn_channels(c - 2, 1)
+            widen(c + 1, SCALAR, item(0))
             if c == 1:
-                turn_rows(c, 0)
-                turn_rows(c, 1)
-            weave(c, 0, "pw")
-            weave(c, 1, "po")
+                turn_rows(1)
+            else:
+                turn_channels(c - 2)
+            weave(c, 0, "woven")
+            weave(c, 1, "products")
             empty_sums(c - 1, 3)
-            widen(c + 1, VECTOR, 0)
-            quantize_events(c, 1)
-            quantize_features(c - 1, slice(0, CHUNK))
-            empty_channels(c - 2, 0)
-            empty_channels(c - 2, 1)
+            widen(c + 1, VECTOR, item(0))
+            quantize_events(c, 1, WHOLE)
+            quantize_features(c - 1, WHOLE)
             if c == 1:
-                empty_rows(c, 0)
-                empty_rows(c, 1)
+                empty_rows(1)
+            else:
+                empty_channels(c - 2)
             empty_weave(c, 0)
             empty_weave(c, 1)
-            for j in range(3):
+            for j in range(BANKS["sums"]):
                 pool_nodes(c, j, 1)
-            project_side(c - 1, 0)
-            project_side(c - 1, 1)
-            turn_rows(c + 1, 0)
-            turn_rows(c + 1, 1)
-            interleave(c, 0, slice(woven(c, 0), CHUNK))
-            widen(c + 1, VECTOR, 1)
-            quantize_events(c, 0)
-            widen(c + 1, SCALAR, 1)
-            widen(c + 1, SCALAR, 2)
-            empty_side(c - 1, 0)
-            empty_side(c - 1, 1)
-            empty_rows(c + 1, 0)
-            empty_rows(c + 1, 1)
-            for j in range(3):
+            project_sides(c - 1)
+            turn_rows(c + 1)
+            interleave(c, 0, slice(WOVEN, CHUNK))
+            widen(c + 1, VECTOR, item(1))
+            quantize_events(c, 0, WHOLE)
+            widen(c + 1, SCALAR, slice(1, 3))
+            empty_sides(c - 1)
+            empty_rows(c + 1)
+            for j in range(BANKS["sums"]):
                 pool_nodes(c, j, 0)
             empty_sums(c, 0)
-            widen(c + 1, SCALAR, 3)
-            widen(c + 1, VECTOR, 2)
-            widen(c + 1, VECTOR, 3)
-            widen(c + 1, VECTOR, 4)
+            widen(c + 1, SCALAR, item(3))
+            widen(c + 1, VECTOR, slice(2, None))
 
-        c = last
-        parts = ((0, 1), (2,), (3,))
-        events = [slice(PAIR * part[0], PAIR * (part[-1] + 1)) for part in parts]
-        sum_columns = [slice(BANK + P * part[0], BANK + P * (part[-1] + 1)) for part in parts]
 
-        def pool_pair(j):
-            for g in (1, 0):
-                pool_nodes(c, j, g)
+        def events_of(pairs):
+            return slice(PAIR * pairs[0], PAIR * (pairs[-1] + 1))
 
-        pair_0, pair_1 = slice(0, PAIR), slice(PAIR, 2 * PAIR)
-        interleave(c, 1, events[0])
-        interleave(c, 0, pair_0)
-        quantize_events(c, 1, events[0])
-        quantize_events(c, 0, pair_0)
-        interleave(c, 0, pair_1)
-        pool_nodes(c - 1, 3, 1)
-        pool_nodes(c - 1, 3, 0)
-        empty_sums(c - 1, 1)
-        empty_sums(c - 1, 2)
-        turn_channels(c - 2, 0)
-        turn_channels(c - 2, 1)
-        empty_sums(c - 1, 3)
-        interleave(c, 1, events[1])
-        quantize_events(c, 0, pair_1)
-        quantize_features(c - 1, slice(0, CHUNK))
-        empty_channels(c - 2, 0)
-        empty_channels(c - 2, 1)
-        pool_pair(0)
-        pool_pair(1)
-        interleave(c, 0, events[1])
+        first, second, third = (0, 1), (2,), (3,)
+        interleave(LAST, 1, events_of(first))
+        quantize_features(LAST, feature_columns(0, range(PAIRS)))
+        interleave(LAST, 0, events_of((0,)))
+        quantize_events(LAST, 1, events_of(first))
+        quantize_events(LAST, 0, events_of((0,)))
+        interleave(LAST, 0, events_of((1,)))
+        pool_pair(LAST - 1, 3)
+        empty_sums(LAST - 1, 1)
+        empty_sums(LAST - 1, 2)
+        turn_channels(LAST - 2)
+        empty_sums(LAST - 1, 3)
+        interleave(LAST, 1, events_of(second))
+        quantize_events(LAST, 0, events_of((1,)))
+        quantize_features(LAST - 1, WHOLE)
+        empty_channels(LAST - 2)
+        pool_pair(LAST, 0)
+        pool_pair(LAST, 1)
+        interleave(LAST, 0, events_of(second))
         for g in (1, 0):
-            quantize_events(c, g, events[1])
-        project_side(c - 1, 0)
-        project_side(c - 1, 1)
-        empty_sums(c, 0)
-        empty_sums(c, 1)
-        empty_side(c - 1, 0)
-        empty_side(c - 1, 1)
-        pool_pair(2)
-        interleave(c, 1, events[2])
-        interleave(c, 0, events[2])
-        quantize_events(c, 1, events[2])
-        quantize_events(c, 0, events[2])
-        turn_channels(c - 1, 0)
-        turn_channels(c - 1, 1)
-        empty_sums(c, 2)
-        pool_pair(3)
-        quantize_features(c, slice(0, BANK))
-        quantize_features(c, sum_columns[0])
-        quantize_features(c, sum_columns[1])
-        empty_channels(c - 1, 0)
-        empty_channels(c - 1, 1)
-        project_pairs(c, parts[0], "po")
-        empty_sums(c, 3)
-        project_pairs(c, parts[1], "po")
-        add_bias(c, parts[0])
-        quantize_features(c, sum_columns[2])
-        rectify(c, parts[0])
-        project_pairs(c, parts[2], "pw")
-        add_bias(c, parts[1])
-        add_bias(c, parts[2])
-        rectify(c, parts[1])
-        rectify(c, parts[2])
+            quantize_events(LAST, g, events_of(second))
+        project_sides(LAST - 1)
+        empty_sums(LAST, 0)
+        empty_sums(LAST, 1)
+        empty_sides(LAST - 1)
+        pool_pair(LAST, 2)
+        for g in (1, 0):
+            interleave(LAST, g, events_of(third))
+        for g in (1, 0):
+            quantize_events(LAST, g, events_of(third))
+        turn_channels(LAST - 1)
+        empty_sums(LAST, 2)
+        pool_pair(LAST, 3)
+        quantize_features(LAST, feature_columns(1, first))
+        quantize_features(LAST, feature_columns(1, second))
+        empty_channels(LAST - 1)
+        project_pairs(first, "products")
+        empty_sums(LAST, 3)
+        project_pairs(second, "products")
+        add_bias(first)
+        quantize_features(LAST, feature_columns(1, third))
+        rectify(first)
+        project_pairs(third, "woven")
+        add_bias(second)
+        add_bias(third)
+        rectify(second)
+        rectify(third)

@@ -182,8 +182,8 @@ def tile_mymodel_icdm_pa_t_w4_kernel(
 
         def interleave(c, g, events):
             nc.vector.tensor_copy(
-                out=grouped_events(c, g)[:, events, :].rearrange("p (e i) t -> p e t i", i=4),
-                in_=wide[c, g][:, :, events].rearrange("p t (e i) -> p e t i", i=4),
+                out=grouped_events(c, g)[:, events, :].rearrange("p (e i) t -> p e t i", i=8),
+                in_=wide[c, g][:, :, events].rearrange("p t (e i) -> p e t i", i=8),
             )
 
         def weave(c, j, use):
@@ -440,30 +440,31 @@ def tile_mymodel_icdm_pa_t_w4_kernel(
         empty_sums(LAST - 1, 2)
         turn_channels(LAST - 2)
         empty_sums(LAST - 1, 3)
-        interleave(LAST, 1, events_of(second))
-        quantize_events(LAST, 0, events_of((1,)))
         quantize_features(LAST - 1, WHOLE)
+        quantize_events(LAST, 0, events_of((1,)))
         empty_channels(LAST - 2)
         pool_pair(LAST, 0)
-        pool_pair(LAST, 1)
-        interleave(LAST, 0, events_of(second))
+        pool_nodes(LAST, 1, 1)
+        project_sides(LAST - 1)
+        pool_nodes(LAST, 1, 0)
+        for g in (1, 0):
+            interleave(LAST, g, events_of(second))
         for g in (1, 0):
             quantize_events(LAST, g, events_of(second))
-        project_sides(LAST - 1)
         empty_sums(LAST, 0)
-        empty_sums(LAST, 1)
         empty_sides(LAST - 1)
+        empty_sums(LAST, 1)
+        turn_channels(LAST - 1)
         pool_pair(LAST, 2)
         for g in (1, 0):
             interleave(LAST, g, events_of(third))
         for g in (1, 0):
             quantize_events(LAST, g, events_of(third))
-        turn_channels(LAST - 1)
+        empty_channels(LAST - 1)
         empty_sums(LAST, 2)
         pool_pair(LAST, 3)
         quantize_features(LAST, feature_columns(1, first))
         quantize_features(LAST, feature_columns(1, second))
-        empty_channels(LAST - 1)
         project_pairs(first, "products")
         empty_sums(LAST, 3)
         project_pairs(second, "products")

@@ -33,7 +33,6 @@ WHOLE = slice(0, CHUNK)
 AHEAD = 2
 WOVEN = 352
 SPLIT = 320
-LAST_SPLIT = 384
 BANKS = {"sums": 3, "products": 2, "turned": 2, "woven": 1}
 SCALAR, VECTOR = 0, 1
 
@@ -46,8 +45,7 @@ def shares(c):
         return [whole[4], whole[6]], whole[:4] + [whole[5], whole[7]]
     if c == 1:
         return [whole[4]] + whole[:3], whole[:4:-1] + [whole[3]]
-    split = LAST_SPLIT if c == LAST else SPLIT
-    return [(4, 0, split)] + whole[:3], whole[:4:-1] + [(4, split, CHUNK), whole[3]]
+    return [(4, 0, SPLIT)] + whole[:3], whole[:4:-1] + [(4, SPLIT, CHUNK), whole[3]]
 
 
 def woven(c):
@@ -318,9 +316,9 @@ def tile_mymodel_icdm_pa_t_w4_kernel(
                 channels[c, side] = finished
                 nc.scalar.activation(out=finished[:], in_=products[c, side][:], func=RELU, bias=bias_column[:])
 
-        def turn_channels(c):
+        def turn_channels(c, use="turned"):
             for side in range(2):
-                bank = new_bank("turned", [P, PAIRS, OUT], F32)
+                bank = new_bank(use, [P, PAIRS, OUT], F32)
                 turned_channels[c, side] = bank
                 for j in range(PAIRS):
                     nc.tensor.transpose(bank[:, j, :], channels[c, side][:, j, :], identity[:])
@@ -417,11 +415,15 @@ def tile_mymodel_icdm_pa_t_w4_kernel(
             quantize_events(c, 0, WHOLE)
             widen(c + 1, SCALAR, slice(1, 3))
             empty_sides(c - 1)
-            empty_rows(c + 1)
+            if c + 1 < LAST:
+                empty_rows(c + 1)
+            else:
+                widen(LAST, SCALAR, item(3))
             for j in range(BANKS["sums"]):
                 pool_nodes(c, j, 0)
             empty_sums(c, 0)
-            widen(c + 1, SCALAR, item(3))
+            if c + 1 < LAST:
+                widen(c + 1, SCALAR, item(3))
             widen(c + 1, VECTOR, slice(2, None))
 
 
@@ -430,7 +432,6 @@ def tile_mymodel_icdm_pa_t_w4_kernel(
 
         first, second, third = (0, 1), (2,), (3,)
         interleave(LAST, 1, events_of(first))
-        quantize_features(LAST, feature_columns(0, range(PAIRS)))
         interleave(LAST, 0, events_of((0,)))
         quantize_events(LAST, 1, events_of(first))
         quantize_events(LAST, 0, events_of((0,)))
@@ -438,11 +439,12 @@ def tile_mymodel_icdm_pa_t_w4_kernel(
         pool_pair(LAST - 1, 3)
         empty_sums(LAST - 1, 1)
         empty_sums(LAST - 1, 2)
-        turn_channels(LAST - 2)
+        turn_channels(LAST - 2, "products")
         empty_sums(LAST - 1, 3)
         quantize_features(LAST - 1, WHOLE)
         quantize_events(LAST, 0, events_of((1,)))
         empty_channels(LAST - 2)
+        empty_rows(LAST)
         pool_pair(LAST, 0)
         pool_nodes(LAST, 1, 1)
         project_sides(LAST - 1)
@@ -463,6 +465,7 @@ def tile_mymodel_icdm_pa_t_w4_kernel(
         empty_channels(LAST - 1)
         empty_sums(LAST, 2)
         pool_pair(LAST, 3)
+        quantize_features(LAST, feature_columns(0, range(PAIRS)))
         quantize_features(LAST, feature_columns(1, first))
         quantize_features(LAST, feature_columns(1, second))
         project_pairs(first, "products")

@@ -1,7 +1,6 @@
 from contextlib import ExitStack
 
 import concourse.mybir as mybir
-from concourse.masks import make_identity
 
 F32 = mybir.dt.float32
 BF16 = mybir.dt.bfloat16
@@ -31,25 +30,16 @@ LAST = EVENTS // CHUNK - 1
 WHOLE = slice(0, CHUNK)
 
 AHEAD = 2
-WOVEN = 352
-SPLIT = 320
+WOVEN = 256
+SPLIT = 448
 BANKS = {"sums": 3, "products": 2, "turned": 2, "woven": 1}
 SCALAR, VECTOR = 0, 1
 
 FLOPS = 2 * NODES * EVENTS * HIDDEN + 2 * EVENTS * 2 * HIDDEN * OUT
 
 
-def shares(c):
-    whole = [(plane, 0, CHUNK) for plane in range(PLANES)]
-    if c == 0:
-        return [whole[4], whole[6]], whole[:4] + [whole[5], whole[7]]
-    if c == 1:
-        return [whole[4]] + whole[:3], whole[:4:-1] + [whole[3]]
-    return [(4, 0, SPLIT)] + whole[:3], whole[:4:-1] + [(4, SPLIT, CHUNK), whole[3]]
-
-
-def woven(c):
-    return CHUNK if c == 0 else WOVEN
+def events_of(first, last):
+    return slice(PAIR * first, PAIR * (last + 1))
 
 
 def tile_mymodel_icdm_pa_t_w4_kernel(
@@ -67,6 +57,23 @@ def tile_mymodel_icdm_pa_t_w4_kernel(
         plane_scales = keep.tile([P, GROUPS, PACK], F32, name="plane_scales")
         nc.scalar.dma_start(out=plane_scales[:], in_=H_A_scale.rearrange("(g p t) o -> p g (t o)", p=P, t=PACK))
 
+        ones_bf = keep.tile([P, P], BF16, name="ones_bf")
+        ones = keep.tile([P, P], F32, name="ones")
+        identity_bf = keep.tile([P, P], BF16, name="identity_bf")
+        identity = keep.tile([P, P], F32, name="identity")
+        nc.vector.memset(ones_bf[:], 1.0)
+        nc.scalar.activation(out=ones[:], in_=ones_bf[:], func=COPY)
+        for diagonal, full in ((identity_bf, ones_bf), (identity, ones)):
+            nc.gpsimd.affine_select(
+                out=diagonal[:],
+                in_=full[:],
+                pattern=[[-1, P]],
+                compare_op=ALU.is_equal,
+                fill=0.0,
+                base=0,
+                channel_multiplier=1,
+            )
+
         n_blocks = 2 * PLANES + 1
         node_codes = keep.tile([P, n_blocks * QUADS], U32, name="node_codes", align_bytes=64)
         node_scales = keep.tile([P, n_blocks * QUADS], U8, name="node_scales", align_bytes=64)
@@ -81,21 +88,18 @@ def tile_mymodel_icdm_pa_t_w4_kernel(
         bias_column = keep.tile([P, 1], BF16, name="bias_column")
         bias_rows = keep.tile([P, 1, OUT], BF16, name="bias_rows")
 
-        identity = keep.tile([P, P], F32, name="identity")
-        make_identity(nc, identity[:])
-        identity_bf = keep.tile([P, P], BF16, name="identity_bf")
-        nc.scalar.activation(out=identity_bf[:], in_=identity[:], func=COPY)
-
 
         event_bytes = {}
         event_rows = {}
 
-        def load_bytes(c, g, cuts=(0, PACK)):
-            raw = work.tile([P, PACK, CHUNK], U8, name="event_bytes", bufs=GROUPS * (AHEAD + 2), align_bytes=64)
-            event_bytes[c, g] = raw
+        def load_bytes(c, g, places=slice(0, PACK)):
+            if (c, g) not in event_bytes:
+                raw = work.tile([P, PACK, CHUNK], U8, name="event_bytes", bufs=GROUPS * (AHEAD + 2), align_bytes=64)
+                event_bytes[c, g] = raw
             source = H_A_bytes[PASS * g : PASS * (g + 1), CHUNK * c : CHUNK * (c + 1)]
-            for planes in map(slice, cuts, cuts[1:]):
-                nc.sync.dma_start(out=raw[:, planes, :], in_=source.rearrange("(p t) e -> p t e", t=PACK)[:, planes, :])
+            nc.sync.dma_start(
+                out=event_bytes[c, g][:, places, :], in_=source.rearrange("(p t) e -> p t e", t=PACK)[:, places, :]
+            )
 
         def load_rows(c):
             rows = work.tile([P, CHUNK // P, HIDDEN], BF16, name="event_rows", bufs=AHEAD + 2, align_bytes=64)
@@ -103,10 +107,14 @@ def tile_mymodel_icdm_pa_t_w4_kernel(
             source = H_mean_M[CHUNK * c : CHUNK * (c + 1), :]
             nc.sync.dma_start(out=rows[:], in_=source.rearrange("(r i) k -> i r k", i=P))
 
-        load_bytes(0, 0, cuts=(0, 1, 2, PACK))
-        load_bytes(0, 1, cuts=(0, 2, PACK))
-        node_rows = keep.tile([P, GROUPS, PACK, HIDDEN], BF16, name="node_rows", align_bytes=64)
-        nc.sync.dma_start(out=node_rows[:], in_=H_mean_A.rearrange("(g p j) c -> p g j c", p=P, j=PACK))
+        for plane in (0, 4, 1, 2, 5, 3, 6, 7):
+            g, t = divmod(plane, PACK)
+            load_bytes(0, g, slice(t, t + 1))
+        node_rows = {}
+        for g in (1, 0):
+            rows = keep.tile([P, PACK, HIDDEN], BF16, name=f"node_rows_{g}", align_bytes=64)
+            node_rows[g] = rows
+            nc.sync.dma_start(out=rows[:], in_=H_mean_A.rearrange("(g p j) c -> g p j c", p=P, j=PACK)[g])
         load_bytes(1, 0)
         load_rows(0)
         load_bytes(1, 1)
@@ -133,11 +141,11 @@ def tile_mymodel_icdm_pa_t_w4_kernel(
         node_grouped = keep.tile([P, GROUPS, PACK, QUADS, PACK], BF16, name="node_grouped", align_bytes=64)
 
         def group_nodes(g, copy):
-            copy(out=node_grouped[:, g], in_=node_rows[:, g].rearrange("p j (q t) -> p t q j", t=PACK))
+            copy(out=node_grouped[:, g], in_=node_rows[g][:].rearrange("p j (q t) -> p t q j", t=PACK))
 
-        def quantize_nodes():
-            for plane in range(PLANES):
-                g, t = divmod(plane, PACK)
+        def quantize_nodes(g):
+            for t in range(PACK):
+                plane = PACK * g + t
                 block = slice((2 * plane + 1) * QUADS, (2 * plane + 2) * QUADS)
                 nc.vector.quantize_mx(
                     out=node_codes[:, block].bitcast(FP8X4),
@@ -154,23 +162,19 @@ def tile_mymodel_icdm_pa_t_w4_kernel(
             bank = psum.tile(shape, dtype, name=use, bufs=BANKS[use])
             return bank
 
-        def widen(c, engine, items):
-            for plane, e0, e1 in shares(c)[engine][items]:
-                g, t = divmod(plane, PACK)
-                if (c, g) not in wide:
-                    planes = work.tile([P, PACK, CHUNK], BF16, name="wide", bufs=2 * GROUPS, align_bytes=64)
-                    wide[c, g] = planes
-                values = event_bytes[c, g][:, t, e0:e1].bitcast(FP8)
-                scale = plane_scales[:, g, t : t + 1]
-                if engine == SCALAR:
-                    nc.scalar.activation(out=wide[c, g][:, t, e0:e1], in_=values, func=COPY, scale=scale)
-                else:
-                    nc.vector.tensor_scalar(
-                        out=wide[c, g][:, t, e0:e1], in0=values, scalar1=scale, scalar2=None, op0=ALU.mult
-                    )
-
-        def item(n):
-            return slice(n, n + 1)
+        def widen(engine, c, plane, events=WHOLE):
+            g, t = divmod(plane, PACK)
+            if (c, g) not in wide:
+                planes = work.tile([P, PACK, CHUNK], BF16, name="wide", bufs=2 * GROUPS, align_bytes=64)
+                wide[c, g] = planes
+            values = event_bytes[c, g][:, t, events].bitcast(FP8)
+            scale = plane_scales[:, g, t : t + 1]
+            if engine == SCALAR:
+                nc.scalar.activation(out=wide[c, g][:, t, events], in_=values, func=COPY, scale=scale)
+            else:
+                nc.vector.tensor_scalar(
+                    out=wide[c, g][:, t, events], in0=values, scalar1=scale, scalar2=None, op0=ALU.mult
+                )
 
         def grouped_events(c, g):
             if (c, g) not in h_grouped:
@@ -178,29 +182,29 @@ def tile_mymodel_icdm_pa_t_w4_kernel(
                 h_grouped[c, g] = grouped
             return h_grouped[c, g]
 
-        def interleave(c, g, events):
-            nc.vector.tensor_copy(
+        def interleave(c, g, events, copy=nc.vector.tensor_copy):
+            copy(
                 out=grouped_events(c, g)[:, events, :].rearrange("p (e i) t -> p e t i", i=8),
                 in_=wide[c, g][:, :, events].rearrange("p t (e i) -> p e t i", i=8),
             )
 
-        def weave(c, j, use):
-            n = min(PAIR, woven(c) - PAIR * j)
-            bank = new_bank(use, [P, n, PACK], BF16)
-            weaves[c, j] = bank
-            for e0 in range(0, n, P):
-                e1 = min(n, e0 + P)
+        def weave(c, events, use, places=slice(0, PACK)):
+            n = events.stop - events.start
+            if (c, events.start) not in weaves:
+                weaves[c, events.start] = new_bank(use, [P, n, PACK], BF16)
+            step = BANK // (places.stop - places.start)
+            for e0 in range(0, n, step):
+                e1 = min(n, e0 + step)
                 nc.tensor.matmul(
-                    out=bank[:, e0:e1, :].rearrange("p e t -> p t e"),
+                    out=weaves[c, events.start][:, e0:e1, places].rearrange("p e t -> p t e"),
                     lhsT=identity_bf[:],
-                    rhs=wide[c, 0][:, :, PAIR * j + e0 : PAIR * j + e1],
+                    rhs=wide[c, 0][:, places, events.start + e0 : events.start + e1],
                     start=True,
                     stop=True,
                 )
 
-        def empty_weave(c, j):
-            bank = weaves[c, j]
-            nc.scalar.copy(out=grouped_events(c, 0)[:, PAIR * j : PAIR * j + bank.shape[1], :], in_=bank[:])
+        def empty_weave(c, events):
+            nc.scalar.copy(out=grouped_events(c, 0)[:, events, :], in_=weaves[c, events.start][:])
 
         def quantize_events(c, g, events):
             if (c, g) not in h_codes:
@@ -213,8 +217,8 @@ def tile_mymodel_icdm_pa_t_w4_kernel(
                 in_=h_grouped[c, g][:, events, :].rearrange("p e t -> p (e t)"),
             )
 
-        def pool_nodes(c, j, g):
-            if g == 1:
+        def pool_nodes(c, j, g, opens=1):
+            if g == opens:
                 sums[c, j] = new_bank("sums", [P, PACK, P], F32)
             for t in range(PACK):
                 for side in range(2):
@@ -226,8 +230,8 @@ def tile_mymodel_icdm_pa_t_w4_kernel(
                         lhsT_scale=node_scales[:, c0 : c0 + P],
                         rhs=h_codes[c, g][:, events].bitcast(FP8X4),
                         rhs_scale=h_scales[c, g][:, events],
-                        start=(g == 1 and t == 0 and side == 0),
-                        stop=(g == 0 and t == PACK - 1 and side == 1),
+                        start=(g == opens and t == 0 and side == 0),
+                        stop=(g != opens and t == PACK - 1 and side == 1),
                     )
 
         def pool_pair(c, j):
@@ -246,10 +250,10 @@ def tile_mymodel_icdm_pa_t_w4_kernel(
                 in_=sums[c, j][:].rearrange("p t n -> p n t"),
             )
 
-        def turn_rows(c):
+        def turn_rows(c, uses=("turned", "turned")):
             words = event_rows[c][:].rearrange("p r k -> p (r k)").bitcast(F32)
             for b in range(2):
-                bank = new_bank("turned", [P, 2, 2, P], F32)
+                bank = new_bank(uses[b], [P, 2, 2, P], F32)
                 turned_rows[c, b] = bank
                 for j in range(2):
                     w0 = PAIR * (2 * b + j)
@@ -342,140 +346,176 @@ def tile_mymodel_icdm_pa_t_w4_kernel(
             bias = bias_rows[:].broadcast_to([P, sets, OUT])
             nc.vector.tensor_tensor(out=new_result(pairs, sets)[:], in0=products[pairs][:], in1=bias, op=ALU.add)
 
-        def rectify(pairs):
+        def rectify(pairs, engine=VECTOR):
             result = results[pairs]
-            nc.vector.tensor_scalar(out=result[:], in0=result[:], scalar1=0.0, scalar2=None, op0=ALU.max)
+            if engine == SCALAR:
+                nc.scalar.activation(out=result[:], in_=result[:], func=RELU)
+            else:
+                nc.vector.tensor_scalar(out=result[:], in0=result[:], scalar1=0.0, scalar2=None, op0=ALU.max)
             rows = out[CHUNK * LAST + PAIR * pairs[0] : CHUNK * LAST + PAIR * (pairs[-1] + 1), :]
             nc.sync.dma_start(out=rows.rearrange("(r i) k -> i r k", i=P), in_=result[:])
 
-
-        widen(0, VECTOR, slice(0, PACK))
-        for j, use in enumerate(("products", "products", "turned", "woven")):
-            weave(0, j, use)
-        for n in range(2):
-            widen(0, SCALAR, item(n))
-            widen(0, VECTOR, item(PACK + n))
-        empty_weave(0, 0)
-        group_nodes(0, nc.vector.tensor_copy)
-        group_nodes(1, nc.scalar.copy)
-        empty_weave(0, 1)
-        interleave(0, 1, WHOLE)
-        quantize_nodes()
-        empty_weave(0, 2)
-        widen(1, SCALAR, item(1))
-        empty_weave(0, 3)
-        for half in (slice(0, 2 * PAIR), slice(2 * PAIR, CHUNK)):
-            quantize_events(0, 1, half)
-            quantize_events(0, 0, half)
+        h0, h1 = events_of(0, 1), events_of(2, 3)
+        low, high = slice(0, 2), slice(2, 4)
+        uses = ("products", "products", "woven", "turned")
+        widen(VECTOR, 0, 0)
+        widen(SCALAR, 0, 4)
+        widen(VECTOR, 0, 1)
+        for j in range(2):
+            weave(0, events_of(j, j), uses[j], low)
+        widen(VECTOR, 0, 2)
+        widen(SCALAR, 0, 5)
+        widen(VECTOR, 0, 3)
+        for j in range(2):
+            weave(0, events_of(j, j), uses[j], high)
+        for j in range(2, 4):
+            weave(0, events_of(j, j), uses[j])
+        widen(VECTOR, 0, 6)
+        widen(SCALAR, 0, 7, h0)
+        widen(SCALAR, 0, 7, h1)
+        group_nodes(1, nc.vector.tensor_copy)
+        interleave(0, 1, h0)
+        empty_weave(0, events_of(0, 0))
+        empty_weave(0, events_of(1, 1))
+        group_nodes(0, nc.scalar.copy)
+        quantize_nodes(1)
+        quantize_events(0, 1, h0)
+        interleave(0, 1, h1)
+        empty_weave(0, events_of(2, 2))
+        empty_weave(0, events_of(3, 3))
+        quantize_events(0, 0, h0)
+        quantize_nodes(0)
+        for j in range(2):
+            pool_nodes(0, j, 1)
         turn_rows(0)
-        for g in (1, 0):
-            pool_nodes(0, 0, g)
-            pool_nodes(0, 1, g)
-        widen(1, SCALAR, item(2))
+        for j in range(2):
+            pool_nodes(0, j, 0)
+        quantize_events(0, 1, h1)
+        quantize_events(0, 0, h1)
+        widen(SCALAR, 1, 0)
+        widen(SCALAR, 1, 1)
         empty_rows(0)
-        pool_pair(0, 2)
-        widen(1, SCALAR, item(0))
         empty_sums(0, 0)
-        widen(1, SCALAR, item(3))
-        widen(1, VECTOR, slice(None))
+        pool_pair(0, 2)
+        empty_sums(0, 1)
+        pool_pair(0, 3)
+        for plane in (7, 6, 5, 4, 2, 3):
+            widen(VECTOR, 1, plane)
+        turn_rows(1)
 
-
+        woven = [slice(e0, min(e0 + PAIR, CHUNK)) for e0 in range(CHUNK - WOVEN, CHUNK, PAIR)]
         for c in range(1, LAST):
+            final = c + 1 == LAST
             if c + AHEAD <= LAST:
                 load_bytes(c + AHEAD, 0)
                 load_bytes(c + AHEAD, 1)
                 load_rows(c + AHEAD)
-            interleave(c, 1, WHOLE)
-            pool_pair(c - 1, 3)
-            empty_sums(c - 1, 1)
+            interleave(c, 1, h0)
+            interleave(c, 0, h0)
             empty_sums(c - 1, 2)
-            widen(c + 1, SCALAR, item(0))
             if c == 1:
-                turn_rows(1)
-            else:
-                turn_channels(c - 2)
-            weave(c, 0, "woven")
-            weave(c, 1, "products")
+                widen(SCALAR, c + 1, 4, slice(SPLIT, CHUNK))
             empty_sums(c - 1, 3)
-            widen(c + 1, VECTOR, item(0))
-            quantize_events(c, 1, WHOLE)
-            quantize_features(c - 1, WHOLE)
             if c == 1:
                 empty_rows(1)
             else:
                 empty_channels(c - 2)
-            empty_weave(c, 0)
-            empty_weave(c, 1)
-            for j in range(BANKS["sums"]):
+            for part, use in zip(woven, ("woven", "products")):
+                weave(c, part, use)
+            quantize_events(c, 1, h0)
+            quantize_features(c - 1, WHOLE)
+            quantize_events(c, 0, h0)
+            widen(SCALAR, c + 1, 0)
+            for part in woven:
+                empty_weave(c, part)
+            for j in range(2):
                 pool_nodes(c, j, 1)
             project_sides(c - 1)
-            turn_rows(c + 1)
-            interleave(c, 0, slice(WOVEN, CHUNK))
-            widen(c + 1, VECTOR, item(1))
-            quantize_events(c, 0, WHOLE)
-            widen(c + 1, SCALAR, slice(1, 3))
-            empty_sides(c - 1)
-            if c + 1 < LAST:
-                empty_rows(c + 1)
-            else:
-                widen(LAST, SCALAR, item(3))
-            for j in range(BANKS["sums"]):
+            for j in range(2):
                 pool_nodes(c, j, 0)
+            interleave(c, 1, h1)
+            interleave(c, 0, slice(h1.start, CHUNK - WOVEN))
+            quantize_events(c, 1, h1)
+            widen(VECTOR, c + 1, 7)
+            quantize_events(c, 0, h1)
+            widen(SCALAR, c + 1, 1)
+            empty_sides(c - 1)
             empty_sums(c, 0)
-            if c + 1 < LAST:
-                widen(c + 1, SCALAR, item(3))
-            widen(c + 1, VECTOR, slice(2, None))
+            empty_sums(c, 1)
+            turn_rows(c + 1)
+            for g in (1, 0):
+                for j in range(2, 4):
+                    pool_nodes(c, j, g)
+            if final:
+                widen(SCALAR, c + 1, 2, h0)
+                empty_rows(c + 1)
+                widen(SCALAR, c + 1, 2, h1)
+                turn_channels(c - 1)
+                for plane in (4, 6, 5, 3):
+                    widen(VECTOR, c + 1, plane, h0)
+            else:
+                widen(SCALAR, c + 1, 4, slice(0, SPLIT))
+                empty_rows(c + 1)
+                widen(SCALAR, c + 1, 2)
+                turn_channels(c - 1)
+                if c > 1:
+                    widen(VECTOR, c + 1, 4, slice(SPLIT, CHUNK))
+                for plane in (6, 5, 3):
+                    widen(VECTOR, c + 1, plane)
 
-
-        def events_of(pairs):
-            return slice(PAIR * pairs[0], PAIR * (pairs[-1] + 1))
-
-        first, second, third = (0, 1), (2,), (3,)
-        interleave(LAST, 1, events_of(first))
-        interleave(LAST, 0, events_of((0,)))
-        quantize_events(LAST, 1, events_of(first))
-        quantize_events(LAST, 0, events_of((0,)))
-        interleave(LAST, 0, events_of((1,)))
-        pool_pair(LAST - 1, 3)
-        empty_sums(LAST - 1, 1)
+        p0, p1, p2, p3 = (events_of(j, j) for j in range(PAIRS))
+        interleave(LAST, 1, p0)
+        interleave(LAST, 0, p0)
+        widen(SCALAR, LAST, 3, h1)
         empty_sums(LAST - 1, 2)
-        turn_channels(LAST - 2, "products")
         empty_sums(LAST - 1, 3)
-        quantize_features(LAST - 1, WHOLE)
-        quantize_events(LAST, 0, events_of((1,)))
         empty_channels(LAST - 2)
-        empty_rows(LAST)
+        quantize_events(LAST, 1, p0)
+        interleave(LAST, 1, p1)
+        quantize_events(LAST, 0, p0)
+        quantize_features(LAST - 1, feature_columns(0, range(PAIRS)))
+        quantize_events(LAST, 1, p1)
+        quantize_features(LAST - 1, feature_columns(1, range(PAIRS)))
+        interleave(LAST, 0, p1)
+        for plane in (4, 5):
+            widen(SCALAR, LAST, plane, h1)
+        widen(VECTOR, LAST, 6, h1)
+        quantize_events(LAST, 0, p1)
         pool_pair(LAST, 0)
         pool_nodes(LAST, 1, 1)
         project_sides(LAST - 1)
         pool_nodes(LAST, 1, 0)
-        for g in (1, 0):
-            interleave(LAST, g, events_of(second))
-        for g in (1, 0):
-            quantize_events(LAST, g, events_of(second))
-        empty_sums(LAST, 0)
         empty_sides(LAST - 1)
-        empty_sums(LAST, 1)
         turn_channels(LAST - 1)
-        pool_pair(LAST, 2)
-        for g in (1, 0):
-            interleave(LAST, g, events_of(third))
-        for g in (1, 0):
-            quantize_events(LAST, g, events_of(third))
+        empty_sums(LAST, 0)
+        empty_sums(LAST, 1)
         empty_channels(LAST - 1)
-        empty_sums(LAST, 2)
-        pool_pair(LAST, 3)
+        interleave(LAST, 0, p2)
+        interleave(LAST, 1, p2)
+        quantize_events(LAST, 0, p2)
+        interleave(LAST, 1, p3)
+        quantize_events(LAST, 1, p2)
+        interleave(LAST, 0, p3)
+        quantize_events(LAST, 1, p3)
+        quantize_features(LAST, feature_columns(1, (0, 1)))
+        quantize_events(LAST, 0, p3)
         quantize_features(LAST, feature_columns(0, range(PAIRS)))
-        quantize_features(LAST, feature_columns(1, first))
-        quantize_features(LAST, feature_columns(1, second))
-        project_pairs(first, "products")
+        pool_nodes(LAST, 2, 0, opens=0)
+        pool_nodes(LAST, 2, 1, opens=0)
+        pool_pair(LAST, 3)
+        project_pairs((0,), "products")
+        project_pairs((1,), "products")
+        empty_sums(LAST, 2)
         empty_sums(LAST, 3)
-        project_pairs(second, "products")
-        add_bias(first)
-        quantize_features(LAST, feature_columns(1, third))
-        rectify(first)
-        project_pairs(third, "woven")
-        add_bias(second)
-        add_bias(third)
-        rectify(second)
-        rectify(third)
+        quantize_features(LAST, feature_columns(1, (2,)))
+        project_pairs((2,), "turned")
+        add_bias((0,))
+        add_bias((1,))
+        quantize_features(LAST, feature_columns(1, (3,)))
+        project_pairs((3,), "woven")
+        rectify((0,), SCALAR)
+        add_bias((2,))
+        rectify((1,))
+        rectify((2,), SCALAR)
+        add_bias((3,))
+        rectify((3,))

@@ -28,11 +28,13 @@ PAIRS = 4
 CHUNK = PAIRS * PAIR
 LAST = EVENTS // CHUNK - 1
 WHOLE = slice(0, CHUNK)
+BOTH = slice(0, GROUPS)
+ONLY = [slice(g, g + 1) for g in range(GROUPS)]
 
 AHEAD = 2
-WOVEN = 256
-SPLIT = 448
-BANKS = {"sums": 3, "products": 2, "turned": 2, "woven": 1}
+WOVEN = 160
+SPLIT = 384
+BANKS = {"sums": 2, "products": 2, "turned": 2, "woven": 2}
 SCALAR, VECTOR = 0, 1
 
 FLOPS = 2 * NODES * EVENTS * HIDDEN + 2 * EVENTS * 2 * HIDDEN * OUT
@@ -120,6 +122,7 @@ def tile_mymodel_icdm_pa_t_w4_kernel(
         load_bytes(1, 1)
         load_rows(1)
         load_bytes(2, 0)
+        load_rows(2)
         load_bytes(2, 1)
         word_halves = wEA1_words[0].rearrange("(h p) b -> p h b", h=2).bitcast(I32)
         scale_quadrants = wEA1_scales[0].rearrange("(h r b) n -> r b h n", h=2, r=2)
@@ -134,7 +137,7 @@ def tile_mymodel_icdm_pa_t_w4_kernel(
                 in_=scale_quadrants[r].bitcast(I32),
             )
         nc.sync.dma_start(out=bias_column[:], in_=bEA1.rearrange("(c o) -> c o", o=1))
-        load_rows(2)
+        load_rows(3)
         nc.sync.dma_start(out=bias_rows[:, 0, :], in_=bEA1.partition_broadcast(P))
 
 
@@ -154,7 +157,7 @@ def tile_mymodel_icdm_pa_t_w4_kernel(
                 )
 
 
-        wide, weaves, h_grouped, h_codes, h_scales = {}, {}, {}, {}, {}
+        wide, weaves, parts = {}, {}, {}
         sums, turned_rows, e_grouped, e_codes, e_scales = {}, {}, {}, {}, {}
         products, channels, turned_channels, results = {}, {}, {}, {}
 
@@ -164,83 +167,87 @@ def tile_mymodel_icdm_pa_t_w4_kernel(
 
         def widen(engine, c, plane, events=WHOLE):
             g, t = divmod(plane, PACK)
-            if (c, g) not in wide:
-                planes = work.tile([P, PACK, CHUNK], BF16, name="wide", bufs=2 * GROUPS, align_bytes=64)
-                wide[c, g] = planes
+            if c not in wide:
+                planes = work.tile([P, GROUPS, PACK, CHUNK], BF16, name="wide", bufs=2, align_bytes=64)
+                wide[c] = planes
             values = event_bytes[c, g][:, t, events].bitcast(FP8)
             scale = plane_scales[:, g, t : t + 1]
             if engine == SCALAR:
-                nc.scalar.activation(out=wide[c, g][:, t, events], in_=values, func=COPY, scale=scale)
+                nc.scalar.activation(out=wide[c][:, g, t, events], in_=values, func=COPY, scale=scale)
             else:
                 nc.vector.tensor_scalar(
-                    out=wide[c, g][:, t, events], in0=values, scalar1=scale, scalar2=None, op0=ALU.mult
+                    out=wide[c][:, g, t, events], in0=values, scalar1=scale, scalar2=None, op0=ALU.mult
                 )
 
-        def grouped_events(c, g):
-            if (c, g) not in h_grouped:
-                grouped = work.tile([P, CHUNK, PACK], BF16, name="h_grouped", bufs=GROUPS + 1, align_bytes=64)
-                h_grouped[c, g] = grouped
-            return h_grouped[c, g]
+        def new_part(c, pairs):
+            n = PAIR * len(pairs)
+            grouped = work.tile([P, GROUPS, n, PACK], BF16, name="h_grouped", bufs=3, align_bytes=64)
+            codes = work.tile([P, GROUPS, n], U32, name="h_codes", bufs=3, align_bytes=64)
+            scales = work.tile([P, GROUPS, n], U8, name="h_scales", bufs=3, align_bytes=64)
+            for j in pairs:
+                parts[c, j] = (PAIR * pairs[0], grouped, codes, scales)
 
-        def interleave(c, g, events, copy=nc.vector.tensor_copy):
-            copy(
-                out=grouped_events(c, g)[:, events, :].rearrange("p (e i) t -> p e t i", i=8),
-                in_=wide[c, g][:, :, events].rearrange("p t (e i) -> p e t i", i=8),
+        def grouped_events(c, passes, events):
+            first, grouped = parts[c, events.start // PAIR][:2]
+            return grouped[:, passes, events.start - first : events.stop - first, :]
+
+        def interleave(c, passes, events):
+            nc.vector.tensor_copy(
+                out=grouped_events(c, passes, events).rearrange("p g (e i) t -> p g e t i", i=8),
+                in_=wide[c][:, passes, :, events].rearrange("p g t (e i) -> p g e t i", i=8),
             )
 
-        def weave(c, events, use, places=slice(0, PACK)):
+        def weave(c, g, events, use, places=slice(0, PACK)):
             n = events.stop - events.start
-            if (c, events.start) not in weaves:
-                weaves[c, events.start] = new_bank(use, [P, n, PACK], BF16)
+            if (c, g, events.start) not in weaves:
+                weaves[c, g, events.start] = new_bank(use, [P, n, PACK], BF16)
             step = BANK // (places.stop - places.start)
             for e0 in range(0, n, step):
                 e1 = min(n, e0 + step)
                 nc.tensor.matmul(
-                    out=weaves[c, events.start][:, e0:e1, places].rearrange("p e t -> p t e"),
+                    out=weaves[c, g, events.start][:, e0:e1, places].rearrange("p e t -> p t e"),
                     lhsT=identity_bf[:],
-                    rhs=wide[c, 0][:, places, events.start + e0 : events.start + e1],
+                    rhs=wide[c][:, g, places, events.start + e0 : events.start + e1],
                     start=True,
                     stop=True,
                 )
 
-        def empty_weave(c, events):
-            nc.scalar.copy(out=grouped_events(c, 0)[:, events, :], in_=weaves[c, events.start][:])
+        def empty_weave(c, g, events):
+            nc.scalar.copy(out=grouped_events(c, g, events), in_=weaves[c, g, events.start][:])
 
-        def quantize_events(c, g, events):
-            if (c, g) not in h_codes:
-                codes = work.tile([P, CHUNK], U32, name="h_codes", bufs=2 * GROUPS, align_bytes=64)
-                scales = work.tile([P, CHUNK], U8, name="h_scales", bufs=2 * GROUPS, align_bytes=64)
-                h_codes[c, g], h_scales[c, g] = codes, scales
+        def quantize_events(c, j, passes=BOTH):
+            grouped, codes, scales = parts[c, j][1:]
             nc.vector.quantize_mx(
-                out=h_codes[c, g][:, events].bitcast(FP8X4),
-                scales=h_scales[c, g][:, events],
-                in_=h_grouped[c, g][:, events, :].rearrange("p e t -> p (e t)"),
+                out=codes[:, passes].rearrange("p g e -> p (g e)").bitcast(FP8X4),
+                scales=scales[:, passes].rearrange("p g e -> p (g e)"),
+                in_=grouped[:, passes].rearrange("p g e t -> p (g e t)"),
             )
 
-        def pool_nodes(c, j, g, opens=1):
+        def pool_nodes(c, j, g, opens=1, use="sums"):
             if g == opens:
-                sums[c, j] = new_bank("sums", [P, PACK, P], F32)
+                sums[c, j] = new_bank(use, [P, PACK, P], F32)
+            first, codes, scales = (parts[c, j][i] for i in (0, 2, 3))
             for t in range(PACK):
                 for side in range(2):
-                    events = slice(PAIR * j + P * side, PAIR * j + P * (side + 1))
+                    e0 = PAIR * j + P * side - first
                     c0 = (2 * (PACK * g + t) + 1 - side) * QUADS
                     nc.tensor.matmul_mx(
                         out=sums[c, j][:, t, :],
                         lhsT=node_codes[:, c0 : c0 + P].bitcast(FP8X4),
                         lhsT_scale=node_scales[:, c0 : c0 + P],
-                        rhs=h_codes[c, g][:, events].bitcast(FP8X4),
-                        rhs_scale=h_scales[c, g][:, events],
+                        rhs=codes[:, g, e0 : e0 + P].bitcast(FP8X4),
+                        rhs_scale=scales[:, g, e0 : e0 + P],
                         start=(g == opens and t == 0 and side == 0),
                         stop=(g != opens and t == PACK - 1 and side == 1),
                     )
 
-        def pool_pair(c, j):
-            pool_nodes(c, j, 1)
+        def pool_pair(c, j, use="sums"):
+            pool_nodes(c, j, 1, use=use)
             pool_nodes(c, j, 0)
 
         def event_features(c):
             if c not in e_grouped:
-                grouped = work.tile([P, 2, PACK * P * PAIRS], BF16, name="e_grouped", bufs=3, align_bytes=64)
+                grouped = work.tile([P, 2, PACK * P * PAIRS], BF16, name="e_grouped", bufs=4, align_bytes=64)
                 e_grouped[c] = grouped
             return e_grouped[c]
 
@@ -356,156 +363,151 @@ def tile_mymodel_icdm_pa_t_w4_kernel(
             nc.sync.dma_start(out=rows.rearrange("(r i) k -> i r k", i=P), in_=result[:])
 
         h0, h1 = events_of(0, 1), events_of(2, 3)
+        p0, p1, p2, p3 = (events_of(j, j) for j in range(PAIRS))
         low, high = slice(0, 2), slice(2, 4)
-        uses = ("products", "products", "woven", "turned")
+        new_part(0, (0, 1))
+        new_part(0, (2, 3))
         widen(VECTOR, 0, 0)
         widen(SCALAR, 0, 4)
         widen(VECTOR, 0, 1)
-        for j in range(2):
-            weave(0, events_of(j, j), uses[j], low)
+        for pair in (p0, p1):
+            weave(0, 0, pair, "woven", low)
         widen(VECTOR, 0, 2)
         widen(SCALAR, 0, 5)
         widen(VECTOR, 0, 3)
-        for j in range(2):
-            weave(0, events_of(j, j), uses[j], high)
-        for j in range(2, 4):
-            weave(0, events_of(j, j), uses[j])
+        for pair in (p0, p1):
+            weave(0, 0, pair, "woven", high)
+        for pair in (p2, p3):
+            weave(0, 0, pair, "products")
         widen(VECTOR, 0, 6)
-        widen(SCALAR, 0, 7, h0)
-        widen(SCALAR, 0, 7, h1)
+        widen(SCALAR, 0, 7)
         group_nodes(1, nc.vector.tensor_copy)
-        interleave(0, 1, h0)
-        empty_weave(0, events_of(0, 0))
-        empty_weave(0, events_of(1, 1))
+        interleave(0, ONLY[1], h0)
+        empty_weave(0, 0, p0)
+        empty_weave(0, 0, p1)
         group_nodes(0, nc.scalar.copy)
         quantize_nodes(1)
-        quantize_events(0, 1, h0)
-        interleave(0, 1, h1)
-        empty_weave(0, events_of(2, 2))
-        empty_weave(0, events_of(3, 3))
-        quantize_events(0, 0, h0)
+        quantize_events(0, 0, ONLY[1])
+        interleave(0, ONLY[1], h1)
+        empty_weave(0, 0, p2)
+        empty_weave(0, 0, p3)
+        quantize_events(0, 0, ONLY[0])
         quantize_nodes(0)
         for j in range(2):
             pool_nodes(0, j, 1)
         turn_rows(0)
         for j in range(2):
             pool_nodes(0, j, 0)
-        quantize_events(0, 1, h1)
-        quantize_events(0, 0, h1)
+        quantize_events(0, 2)
         widen(SCALAR, 1, 0)
         widen(SCALAR, 1, 1)
-        empty_rows(0)
         empty_sums(0, 0)
-        pool_pair(0, 2)
+        empty_rows(0)
         empty_sums(0, 1)
-        pool_pair(0, 3)
-        for plane in (7, 6, 5, 4, 2, 3):
-            widen(VECTOR, 1, plane)
+        widen(SCALAR, 1, 2, h0)
+        for plane, events in ((7, WHOLE), (6, WHOLE), (5, WHOLE), (4, WHOLE), (3, WHOLE), (2, h1)):
+            widen(VECTOR, 1, plane, events)
+        pool_pair(0, 2, "products")
         turn_rows(1)
+        pool_pair(0, 3)
 
-        woven = [slice(e0, min(e0 + PAIR, CHUNK)) for e0 in range(CHUNK - WOVEN, CHUNK, PAIR)]
         for c in range(1, LAST):
             final = c + 1 == LAST
+            woven = p3 if c == 1 else slice(CHUNK - WOVEN, CHUNK)
             if c + AHEAD <= LAST:
                 load_bytes(c + AHEAD, 0)
                 load_bytes(c + AHEAD, 1)
-                load_rows(c + AHEAD)
-            interleave(c, 1, h0)
-            interleave(c, 0, h0)
+            if c + AHEAD < LAST:
+                load_rows(c + AHEAD + 1)
+            new_part(c, (0, 1))
+            interleave(c, BOTH, h0)
+            widen(SCALAR, c + 1, 0)
             empty_sums(c - 1, 2)
-            if c == 1:
-                widen(SCALAR, c + 1, 4, slice(SPLIT, CHUNK))
+            widen(SCALAR, c + 1, 4, h0 if final else slice(0, SPLIT))
             empty_sums(c - 1, 3)
             if c == 1:
                 empty_rows(1)
             else:
                 empty_channels(c - 2)
-            for part, use in zip(woven, ("woven", "products")):
-                weave(c, part, use)
-            quantize_events(c, 1, h0)
-            quantize_features(c - 1, WHOLE)
-            quantize_events(c, 0, h0)
-            widen(SCALAR, c + 1, 0)
-            for part in woven:
-                empty_weave(c, part)
-            for j in range(2):
-                pool_nodes(c, j, 1)
-            project_sides(c - 1)
-            for j in range(2):
-                pool_nodes(c, j, 0)
-            interleave(c, 1, h1)
-            interleave(c, 0, slice(h1.start, CHUNK - WOVEN))
-            quantize_events(c, 1, h1)
+            for g in range(GROUPS):
+                weave(c, g, woven, "woven")
+            if c == 1:
+                turn_rows(2, ("products", "products"))
             widen(VECTOR, c + 1, 7)
-            quantize_events(c, 0, h1)
+            widen(VECTOR, c + 1, 6, h0 if final else WHOLE)
+            quantize_events(c, 0)
+            quantize_features(c - 1, WHOLE)
+            new_part(c, (2, 3))
+            for g in range(GROUPS):
+                empty_weave(c, g, woven)
+            if c == 1:
+                empty_rows(2)
             widen(SCALAR, c + 1, 1)
-            empty_sides(c - 1)
-            empty_sums(c, 0)
-            empty_sums(c, 1)
-            turn_rows(c + 1)
-            for g in (1, 0):
-                for j in range(2, 4):
-                    pool_nodes(c, j, g)
+            pool_pair(c, 0)
+            pool_pair(c, 1)
+            if not final:
+                turn_rows(c + 2)
+            project_sides(c - 1)
+            interleave(c, BOTH, slice(h1.start, woven.start))
             if final:
-                widen(SCALAR, c + 1, 2, h0)
-                empty_rows(c + 1)
-                widen(SCALAR, c + 1, 2, h1)
-                turn_channels(c - 1)
-                for plane in (4, 6, 5, 3):
-                    widen(VECTOR, c + 1, plane, h0)
+                widen(VECTOR, c + 1, 5, h0)
+                quantize_events(c, 2)
             else:
-                widen(SCALAR, c + 1, 4, slice(0, SPLIT))
-                empty_rows(c + 1)
-                widen(SCALAR, c + 1, 2)
-                turn_channels(c - 1)
-                if c > 1:
-                    widen(VECTOR, c + 1, 4, slice(SPLIT, CHUNK))
-                for plane in (6, 5, 3):
-                    widen(VECTOR, c + 1, plane)
+                widen(VECTOR, c + 1, 5)
+                widen(VECTOR, c + 1, 3)
+                widen(VECTOR, c + 1, 4, slice(SPLIT, CHUNK))
+                quantize_events(c, 2)
+            empty_sums(c, 0)
+            widen(SCALAR, c + 1, 2, h0 if final else WHOLE)
+            if final:
+                widen(SCALAR, c + 1, 3, h0)
+            empty_sums(c, 1)
+            if not final:
+                empty_rows(c + 2)
+            empty_sides(c - 1)
+            pool_pair(c, 2)
+            pool_pair(c, 3)
+            turn_channels(c - 1)
 
-        p0, p1, p2, p3 = (events_of(j, j) for j in range(PAIRS))
-        interleave(LAST, 1, p0)
-        interleave(LAST, 0, p0)
-        widen(SCALAR, LAST, 3, h1)
+        for j in range(2):
+            new_part(LAST, (j,))
+        interleave(LAST, BOTH, p0)
+        widen(SCALAR, LAST, 2, h1)
         empty_sums(LAST - 1, 2)
+        widen(SCALAR, LAST, 3, h1)
         empty_sums(LAST - 1, 3)
+        widen(SCALAR, LAST, 4, h1)
+        widen(SCALAR, LAST, 5, h1)
         empty_channels(LAST - 2)
-        quantize_events(LAST, 1, p0)
-        interleave(LAST, 1, p1)
-        quantize_events(LAST, 0, p0)
         quantize_features(LAST - 1, feature_columns(0, range(PAIRS)))
-        quantize_events(LAST, 1, p1)
-        quantize_features(LAST - 1, feature_columns(1, range(PAIRS)))
-        interleave(LAST, 0, p1)
-        for plane in (4, 5):
-            widen(SCALAR, LAST, plane, h1)
+        quantize_events(LAST, 0)
+        interleave(LAST, BOTH, p1)
         widen(VECTOR, LAST, 6, h1)
-        quantize_events(LAST, 0, p1)
+        quantize_features(LAST - 1, feature_columns(1, range(PAIRS)))
+        quantize_events(LAST, 1)
         pool_pair(LAST, 0)
-        pool_nodes(LAST, 1, 1)
         project_sides(LAST - 1)
-        pool_nodes(LAST, 1, 0)
+        pool_pair(LAST, 1)
+        empty_sums(LAST, 0)
         empty_sides(LAST - 1)
         turn_channels(LAST - 1)
-        empty_sums(LAST, 0)
         empty_sums(LAST, 1)
         empty_channels(LAST - 1)
-        interleave(LAST, 0, p2)
-        interleave(LAST, 1, p2)
-        quantize_events(LAST, 0, p2)
-        interleave(LAST, 1, p3)
-        quantize_events(LAST, 1, p2)
-        interleave(LAST, 0, p3)
-        quantize_events(LAST, 1, p3)
+        new_part(LAST, (2,))
+        interleave(LAST, BOTH, p2)
+        new_part(LAST, (3,))
+        interleave(LAST, ONLY[1], p3)
+        quantize_events(LAST, 2)
+        interleave(LAST, ONLY[0], p3)
+        quantize_events(LAST, 3, ONLY[1])
         quantize_features(LAST, feature_columns(1, (0, 1)))
-        quantize_events(LAST, 0, p3)
+        quantize_events(LAST, 3, ONLY[0])
         quantize_features(LAST, feature_columns(0, range(PAIRS)))
-        pool_nodes(LAST, 2, 0, opens=0)
-        pool_nodes(LAST, 2, 1, opens=0)
+        pool_pair(LAST, 2)
+        empty_sums(LAST, 2)
         pool_pair(LAST, 3)
         project_pairs((0,), "products")
         project_pairs((1,), "products")
-        empty_sums(LAST, 2)
         empty_sums(LAST, 3)
         quantize_features(LAST, feature_columns(1, (2,)))
         project_pairs((2,), "turned")

@@ -33,9 +33,10 @@ ONLY = [slice(g, g + 1) for g in range(GROUPS)]
 
 AHEAD = 2
 WOVEN = 160
-SPLIT = 384
+SPLIT = 320
 BANKS = {"sums": 2, "products": 2, "turned": 2, "woven": 2}
 SCALAR, VECTOR = 0, 1
+RUN = 8
 
 FLOPS = 2 * NODES * EVENTS * HIDDEN + 2 * EVENTS * 2 * HIDDEN * OUT
 
@@ -122,8 +123,8 @@ def tile_mymodel_icdm_pa_t_w4_kernel(
         load_bytes(1, 1)
         load_rows(1)
         load_bytes(2, 0)
-        load_rows(2)
         load_bytes(2, 1)
+        load_rows(2)
         word_halves = wEA1_words[0].rearrange("(h p) b -> p h b", h=2).bitcast(I32)
         scale_quadrants = wEA1_scales[0].rearrange("(h r b) n -> r b h n", h=2, r=2)
         for side in range(2):
@@ -193,8 +194,8 @@ def tile_mymodel_icdm_pa_t_w4_kernel(
 
         def interleave(c, passes, events):
             nc.vector.tensor_copy(
-                out=grouped_events(c, passes, events).rearrange("p g (e i) t -> p g e t i", i=8),
-                in_=wide[c][:, passes, :, events].rearrange("p g t (e i) -> p g e t i", i=8),
+                out=grouped_events(c, passes, events).rearrange("p g (e i) t -> p g e t i", i=RUN),
+                in_=wide[c][:, passes, :, events].rearrange("p g t (e i) -> p g e t i", i=RUN),
             )
 
         def weave(c, g, events, use, places=slice(0, PACK)):
@@ -380,7 +381,8 @@ def tile_mymodel_icdm_pa_t_w4_kernel(
         for pair in (p2, p3):
             weave(0, 0, pair, "products")
         widen(VECTOR, 0, 6)
-        widen(SCALAR, 0, 7)
+        widen(SCALAR, 0, 7, h0)
+        widen(SCALAR, 0, 7, h1)
         group_nodes(1, nc.vector.tensor_copy)
         interleave(0, ONLY[1], h0)
         empty_weave(0, 0, p0)
@@ -401,10 +403,10 @@ def tile_mymodel_icdm_pa_t_w4_kernel(
         quantize_events(0, 2)
         widen(SCALAR, 1, 0)
         widen(SCALAR, 1, 1)
+        widen(SCALAR, 1, 2, h0)
         empty_sums(0, 0)
         empty_rows(0)
         empty_sums(0, 1)
-        widen(SCALAR, 1, 2, h0)
         for plane, events in ((7, WHOLE), (6, WHOLE), (5, WHOLE), (4, WHOLE), (3, WHOLE), (2, h1)):
             widen(VECTOR, 1, plane, events)
         pool_pair(0, 2, "products")
@@ -423,16 +425,18 @@ def tile_mymodel_icdm_pa_t_w4_kernel(
             interleave(c, BOTH, h0)
             widen(SCALAR, c + 1, 0)
             empty_sums(c - 1, 2)
-            widen(SCALAR, c + 1, 4, h0 if final else slice(0, SPLIT))
+            if final:
+                widen(SCALAR, c + 1, 4, h0)
             empty_sums(c - 1, 3)
             if c == 1:
                 empty_rows(1)
             else:
                 empty_channels(c - 2)
-            for g in range(GROUPS):
-                weave(c, g, woven, "woven")
             if c == 1:
                 turn_rows(2, ("products", "products"))
+                empty_rows(2)
+            for g in range(GROUPS):
+                weave(c, g, woven, "woven")
             widen(VECTOR, c + 1, 7)
             widen(VECTOR, c + 1, 6, h0 if final else WHOLE)
             quantize_events(c, 0)
@@ -440,8 +444,6 @@ def tile_mymodel_icdm_pa_t_w4_kernel(
             new_part(c, (2, 3))
             for g in range(GROUPS):
                 empty_weave(c, g, woven)
-            if c == 1:
-                empty_rows(2)
             widen(SCALAR, c + 1, 1)
             pool_pair(c, 0)
             pool_pair(c, 1)
@@ -455,7 +457,7 @@ def tile_mymodel_icdm_pa_t_w4_kernel(
             else:
                 widen(VECTOR, c + 1, 5)
                 widen(VECTOR, c + 1, 3)
-                widen(VECTOR, c + 1, 4, slice(SPLIT, CHUNK))
+                widen(VECTOR, c + 1, 4)
                 quantize_events(c, 2)
             empty_sums(c, 0)
             widen(SCALAR, c + 1, 2, h0 if final else WHOLE)
@@ -488,8 +490,8 @@ def tile_mymodel_icdm_pa_t_w4_kernel(
         pool_pair(LAST, 0)
         project_sides(LAST - 1)
         pool_pair(LAST, 1)
-        empty_sums(LAST, 0)
         empty_sides(LAST - 1)
+        empty_sums(LAST, 0)
         turn_channels(LAST - 1)
         empty_sums(LAST, 1)
         empty_channels(LAST - 1)
@@ -503,9 +505,9 @@ def tile_mymodel_icdm_pa_t_w4_kernel(
         quantize_features(LAST, feature_columns(1, (0, 1)))
         quantize_events(LAST, 3, ONLY[0])
         quantize_features(LAST, feature_columns(0, range(PAIRS)))
-        pool_pair(LAST, 2)
+        pool_pair(LAST, 2, "woven")
         empty_sums(LAST, 2)
-        pool_pair(LAST, 3)
+        pool_pair(LAST, 3, "woven")
         project_pairs((0,), "products")
         project_pairs((1,), "products")
         empty_sums(LAST, 3)
@@ -514,7 +516,7 @@ def tile_mymodel_icdm_pa_t_w4_kernel(
         add_bias((0,))
         add_bias((1,))
         quantize_features(LAST, feature_columns(1, (3,)))
-        project_pairs((3,), "woven")
+        project_pairs((3,), "sums")
         rectify((0,), SCALAR)
         add_bias((2,))
         rectify((1,))

@@ -33,7 +33,7 @@ ONLY = [slice(g, g + 1) for g in range(GROUPS)]
 
 AHEAD = 2
 WOVEN = 160
-SPLIT = 320
+SPLIT = 256
 BANKS = {"sums": 2, "products": 2, "turned": 2, "woven": 2}
 SCALAR, VECTOR = 0, 1
 RUN = 8
@@ -124,7 +124,6 @@ def tile_mymodel_icdm_pa_t_w4_kernel(
         load_rows(1)
         load_bytes(2, 0)
         load_bytes(2, 1)
-        load_rows(2)
         word_halves = wEA1_words[0].rearrange("(h p) b -> p h b", h=2).bitcast(I32)
         scale_quadrants = wEA1_scales[0].rearrange("(h r b) n -> r b h n", h=2, r=2)
         for side in range(2):
@@ -138,7 +137,7 @@ def tile_mymodel_icdm_pa_t_w4_kernel(
                 in_=scale_quadrants[r].bitcast(I32),
             )
         nc.sync.dma_start(out=bias_column[:], in_=bEA1.rearrange("(c o) -> c o", o=1))
-        load_rows(3)
+        load_rows(2)
         nc.sync.dma_start(out=bias_rows[:, 0, :], in_=bEA1.partition_broadcast(P))
 
 
@@ -258,22 +257,24 @@ def tile_mymodel_icdm_pa_t_w4_kernel(
                 in_=sums[c, j][:].rearrange("p t n -> p n t"),
             )
 
-        def turn_rows(c, uses=("turned", "turned")):
-            words = event_rows[c][:].rearrange("p r k -> p (r k)").bitcast(F32)
-            for b in range(2):
-                bank = new_bank(uses[b], [P, 2, 2, P], F32)
-                turned_rows[c, b] = bank
+        def turn_rows(halves, use="turned"):
+            for half in halves:
+                c, b = divmod(half, 2)
+                words = event_rows[c][:].rearrange("p r k -> p (r k)").bitcast(F32)
+                bank = new_bank(use, [P, 2, 2, P], F32)
+                turned_rows[half] = bank
                 for j in range(2):
                     w0 = PAIR * (2 * b + j)
                     for u in range(2):
                         nc.tensor.transpose(bank[:, j, u, :], words[:, w0 + u : w0 + PAIR : 2], identity[:])
 
-        def empty_rows(c):
-            for b in range(2):
+        def empty_rows(halves):
+            for half in halves:
+                c, b = divmod(half, 2)
                 words = event_features(c)[:, 0, :].bitcast(F32)[:, BANK * b : BANK * (b + 1)]
                 nc.scalar.copy(
                     out=words.rearrange("p (j n u) -> p j n u", n=P, u=2),
-                    in_=turned_rows[c, b][:].rearrange("p j u n -> p j n u"),
+                    in_=turned_rows[half][:].rearrange("p j u n -> p j n u"),
                 )
 
         def feature_columns(half, pairs):
@@ -385,9 +386,9 @@ def tile_mymodel_icdm_pa_t_w4_kernel(
         widen(SCALAR, 0, 7, h1)
         group_nodes(1, nc.vector.tensor_copy)
         interleave(0, ONLY[1], h0)
+        group_nodes(0, nc.scalar.copy)
         empty_weave(0, 0, p0)
         empty_weave(0, 0, p1)
-        group_nodes(0, nc.scalar.copy)
         quantize_nodes(1)
         quantize_events(0, 0, ONLY[1])
         interleave(0, ONLY[1], h1)
@@ -397,44 +398,46 @@ def tile_mymodel_icdm_pa_t_w4_kernel(
         quantize_nodes(0)
         for j in range(2):
             pool_nodes(0, j, 1)
-        turn_rows(0)
+        turn_rows((0, 1))
         for j in range(2):
             pool_nodes(0, j, 0)
         quantize_events(0, 2)
         widen(SCALAR, 1, 0)
         widen(SCALAR, 1, 1)
-        widen(SCALAR, 1, 2, h0)
+        widen(SCALAR, 1, 2)
         empty_sums(0, 0)
-        empty_rows(0)
+        empty_rows((0, 1))
         empty_sums(0, 1)
-        for plane, events in ((7, WHOLE), (6, WHOLE), (5, WHOLE), (4, WHOLE), (3, WHOLE), (2, h1)):
+        for plane, events in ((3, h0), (7, WHOLE), (6, WHOLE), (5, WHOLE), (4, WHOLE), (3, h1)):
             widen(VECTOR, 1, plane, events)
         pool_pair(0, 2, "products")
-        turn_rows(1)
+        turn_rows((2, 3))
         pool_pair(0, 3)
 
+        rows_done = 4
         for c in range(1, LAST):
             final = c + 1 == LAST
             woven = p3 if c == 1 else slice(CHUNK - WOVEN, CHUNK)
+            usual = range(rows_done, min(rows_done + 2, 2 * LAST + 2))
+            spare = range(usual.stop, usual.stop + (1 if c in (2, 3) else 0))
+            rows_done = spare.stop
             if c + AHEAD <= LAST:
                 load_bytes(c + AHEAD, 0)
                 load_bytes(c + AHEAD, 1)
-            if c + AHEAD < LAST:
-                load_rows(c + AHEAD + 1)
+                load_rows(c + AHEAD)
             new_part(c, (0, 1))
             interleave(c, BOTH, h0)
             widen(SCALAR, c + 1, 0)
             empty_sums(c - 1, 2)
             if final:
                 widen(SCALAR, c + 1, 4, h0)
+            elif SPLIT:
+                widen(SCALAR, c + 1, 4, slice(0, SPLIT))
             empty_sums(c - 1, 3)
             if c == 1:
-                empty_rows(1)
+                empty_rows((2, 3))
             else:
                 empty_channels(c - 2)
-            if c == 1:
-                turn_rows(2, ("products", "products"))
-                empty_rows(2)
             for g in range(GROUPS):
                 weave(c, g, woven, "woven")
             widen(VECTOR, c + 1, 7)
@@ -447,28 +450,34 @@ def tile_mymodel_icdm_pa_t_w4_kernel(
             widen(SCALAR, c + 1, 1)
             pool_pair(c, 0)
             pool_pair(c, 1)
-            if not final:
-                turn_rows(c + 2)
+            turn_rows(usual)
             project_sides(c - 1)
+            turn_rows(spare, "woven")
             interleave(c, BOTH, slice(h1.start, woven.start))
             if final:
                 widen(VECTOR, c + 1, 5, h0)
-                quantize_events(c, 2)
+                quantize_events(c, 2, ONLY[1])
+                quantize_events(c, 2, ONLY[0])
             else:
                 widen(VECTOR, c + 1, 5)
                 widen(VECTOR, c + 1, 3)
-                widen(VECTOR, c + 1, 4)
+                widen(VECTOR, c + 1, 4, slice(SPLIT, CHUNK))
                 quantize_events(c, 2)
             empty_sums(c, 0)
             widen(SCALAR, c + 1, 2, h0 if final else WHOLE)
             if final:
                 widen(SCALAR, c + 1, 3, h0)
             empty_sums(c, 1)
-            if not final:
-                empty_rows(c + 2)
+            empty_rows(usual)
             empty_sides(c - 1)
-            pool_pair(c, 2)
-            pool_pair(c, 3)
+            empty_rows(spare)
+            if final:
+                for g in (1, 0):
+                    pool_nodes(c, 2, g)
+                    pool_nodes(c, 3, g, use="woven")
+            else:
+                pool_pair(c, 2)
+                pool_pair(c, 3)
             turn_channels(c - 1)
 
         for j in range(2):

@@ -33,7 +33,7 @@ ONLY = [slice(g, g + 1) for g in range(GROUPS)]
 
 AHEAD = 2
 WOVEN = 160
-SPLIT = 256
+SPLIT = 0
 BANKS = {"sums": 2, "products": 2, "turned": 2, "woven": 2}
 SCALAR, VECTOR = 0, 1
 RUN = 8

@@ -97,7 +97,7 @@ def tile_mymodel_icdm_pa_t_w4_kernel(
 
         def load_bytes(c, g, places=slice(0, PACK)):
             if (c, g) not in event_bytes:
-                raw = work.tile([P, PACK, CHUNK], U8, name="event_bytes", bufs=GROUPS * (AHEAD + 2), align_bytes=64)
+                raw = work.tile([P, PACK, CHUNK], U8, name="event_bytes", bufs=GROUPS * (AHEAD + 2) - 1, align_bytes=64)
                 event_bytes[c, g] = raw
             source = H_A_bytes[PASS * g : PASS * (g + 1), CHUNK * c : CHUNK * (c + 1)]
             nc.sync.dma_start(
@@ -168,7 +168,7 @@ def tile_mymodel_icdm_pa_t_w4_kernel(
         def widen(engine, c, plane, events=WHOLE):
             g, t = divmod(plane, PACK)
             if c not in wide:
-                planes = work.tile([P, GROUPS, PACK, CHUNK], BF16, name="wide", bufs=2, align_bytes=64)
+                planes = work.tile([P, GROUPS, PACK, CHUNK], BF16, name="wide", bufs=3, align_bytes=64)
                 wide[c] = planes
             values = event_bytes[c, g][:, t, events].bitcast(FP8)
             scale = plane_scales[:, g, t : t + 1]
@@ -312,7 +312,7 @@ def tile_mymodel_icdm_pa_t_w4_kernel(
                 )
 
         def new_result(key, sets):
-            result = work.tile([P, sets, OUT], F32, name="result", bufs=5)
+            result = work.tile([P, sets, OUT], F32, name="result", bufs=14)
             results[key] = result
             return result
 
@@ -411,8 +411,8 @@ def tile_mymodel_icdm_pa_t_w4_kernel(
         for plane, events in ((3, h0), (7, WHOLE), (6, WHOLE), (5, WHOLE), (4, WHOLE), (3, h1)):
             widen(VECTOR, 1, plane, events)
         pool_pair(0, 2, "products")
+        pool_pair(0, 3, "products")
         turn_rows((2, 3))
-        pool_pair(0, 3)
 
         rows_done = 4
         for c in range(1, LAST):
@@ -443,6 +443,8 @@ def tile_mymodel_icdm_pa_t_w4_kernel(
             widen(VECTOR, c + 1, 7)
             widen(VECTOR, c + 1, 6, h0 if final else WHOLE)
             quantize_events(c, 0)
+            if not final:
+                widen(VECTOR, c + 1, 5)
             quantize_features(c - 1, WHOLE)
             new_part(c, (2, 3))
             for g in range(GROUPS):
@@ -459,7 +461,6 @@ def tile_mymodel_icdm_pa_t_w4_kernel(
                 quantize_events(c, 2, ONLY[1])
                 quantize_events(c, 2, ONLY[0])
             else:
-                widen(VECTOR, c + 1, 5)
                 widen(VECTOR, c + 1, 3)
                 widen(VECTOR, c + 1, 4, slice(SPLIT, CHUNK))
                 quantize_events(c, 2)
@@ -483,12 +484,12 @@ def tile_mymodel_icdm_pa_t_w4_kernel(
         for j in range(2):
             new_part(LAST, (j,))
         interleave(LAST, BOTH, p0)
-        widen(SCALAR, LAST, 2, h1)
-        empty_sums(LAST - 1, 2)
-        widen(SCALAR, LAST, 3, h1)
-        empty_sums(LAST - 1, 3)
         widen(SCALAR, LAST, 4, h1)
+        empty_sums(LAST - 1, 2)
         widen(SCALAR, LAST, 5, h1)
+        empty_sums(LAST - 1, 3)
+        widen(SCALAR, LAST, 2, h1)
+        widen(SCALAR, LAST, 3, h1)
         empty_channels(LAST - 2)
         quantize_features(LAST - 1, feature_columns(0, range(PAIRS)))
         quantize_events(LAST, 0)
@@ -501,34 +502,39 @@ def tile_mymodel_icdm_pa_t_w4_kernel(
         pool_pair(LAST, 1)
         empty_sides(LAST - 1)
         empty_sums(LAST, 0)
-        turn_channels(LAST - 1)
         empty_sums(LAST, 1)
-        empty_channels(LAST - 1)
         new_part(LAST, (2,))
-        interleave(LAST, BOTH, p2)
         new_part(LAST, (3,))
+        interleave(LAST, ONLY[1], p2)
         interleave(LAST, ONLY[1], p3)
-        quantize_events(LAST, 2)
-        interleave(LAST, ONLY[0], p3)
+        quantize_events(LAST, 2, ONLY[1])
+        interleave(LAST, ONLY[0], p2)
         quantize_events(LAST, 3, ONLY[1])
-        quantize_features(LAST, feature_columns(1, (0, 1)))
+        interleave(LAST, ONLY[0], p3)
+        quantize_events(LAST, 2, ONLY[0])
+        quantize_features(LAST, feature_columns(0, (0, 1)))
         quantize_events(LAST, 3, ONLY[0])
-        quantize_features(LAST, feature_columns(0, range(PAIRS)))
-        pool_pair(LAST, 2, "woven")
+        quantize_features(LAST, feature_columns(1, (0, 1)))
+        quantize_features(LAST, feature_columns(0, (2, 3)))
+        turn_channels(LAST - 1)
+        pool_nodes(LAST, 2, 1, use="woven")
+        pool_nodes(LAST, 3, 1, use="woven")
+        pool_nodes(LAST, 2, 0)
+        pool_nodes(LAST, 3, 0)
+        empty_channels(LAST - 1)
         empty_sums(LAST, 2)
-        pool_pair(LAST, 3, "woven")
+        empty_sums(LAST, 3)
         project_pairs((0,), "products")
         project_pairs((1,), "products")
-        empty_sums(LAST, 3)
         quantize_features(LAST, feature_columns(1, (2,)))
-        project_pairs((2,), "turned")
+        project_pairs((2,), "sums")
         add_bias((0,))
-        add_bias((1,))
         quantize_features(LAST, feature_columns(1, (3,)))
+        add_bias((1,))
         project_pairs((3,), "sums")
         rectify((0,), SCALAR)
         add_bias((2,))
-        rectify((1,))
-        rectify((2,), SCALAR)
+        rectify((1,), SCALAR)
         add_bias((3,))
+        rectify((2,), SCALAR)
         rectify((3,))

@@ -32,8 +32,8 @@ BOTH = slice(0, GROUPS)
 ONLY = [slice(g, g + 1) for g in range(GROUPS)]
 
 AHEAD = 2
-WOVEN = 160
-SPLIT = 0
+WOVEN = 144
+SPLIT = 512
 BANKS = {"sums": 2, "products": 2, "turned": 2, "woven": 2}
 SCALAR, VECTOR = 0, 1
 RUN = 8
@@ -393,6 +393,7 @@ def tile_mymodel_icdm_pa_t_w4_kernel(
         quantize_events(0, 0, ONLY[1])
         interleave(0, ONLY[1], h1)
         empty_weave(0, 0, p2)
+        widen(SCALAR, 1, 0, h0)
         empty_weave(0, 0, p3)
         quantize_events(0, 0, ONLY[0])
         quantize_nodes(0)
@@ -401,14 +402,15 @@ def tile_mymodel_icdm_pa_t_w4_kernel(
         turn_rows((0, 1))
         for j in range(2):
             pool_nodes(0, j, 0)
+        widen(VECTOR, 1, 3, h0)
         quantize_events(0, 2)
-        widen(SCALAR, 1, 0)
+        widen(SCALAR, 1, 0, h1)
         widen(SCALAR, 1, 1)
         widen(SCALAR, 1, 2)
         empty_sums(0, 0)
         empty_rows((0, 1))
         empty_sums(0, 1)
-        for plane, events in ((3, h0), (7, WHOLE), (6, WHOLE), (5, WHOLE), (4, WHOLE), (3, h1)):
+        for plane, events in ((7, WHOLE), (6, WHOLE), (5, WHOLE), (4, WHOLE), (3, h1)):
             widen(VECTOR, 1, plane, events)
         pool_pair(0, 2, "products")
         pool_pair(0, 3, "products")
@@ -431,7 +433,7 @@ def tile_mymodel_icdm_pa_t_w4_kernel(
             empty_sums(c - 1, 2)
             if final:
                 widen(SCALAR, c + 1, 4, h0)
-            elif SPLIT:
+            elif c not in (2, 3):
                 widen(SCALAR, c + 1, 4, slice(0, SPLIT))
             empty_sums(c - 1, 3)
             if c == 1:
@@ -462,7 +464,7 @@ def tile_mymodel_icdm_pa_t_w4_kernel(
                 quantize_events(c, 2, ONLY[0])
             else:
                 widen(VECTOR, c + 1, 3)
-                widen(VECTOR, c + 1, 4, slice(SPLIT, CHUNK))
+                widen(VECTOR, c + 1, 4, slice(SPLIT if c not in (2, 3) else 0, CHUNK))
                 quantize_events(c, 2)
             empty_sums(c, 0)
             widen(SCALAR, c + 1, 2, h0 if final else WHOLE)

@@ -32,8 +32,9 @@ BOTH = slice(0, GROUPS)
 ONLY = [slice(g, g + 1) for g in range(GROUPS)]
 
 AHEAD = 2
-WOVEN = 144
-SPLIT = 512
+WOVEN = 384
+WOVEN_BESIDE_ROWS = 320
+SPLIT = 256
 BANKS = {"sums": 2, "products": 2, "turned": 2, "woven": 2}
 SCALAR, VECTOR = 0, 1
 RUN = 8
@@ -181,11 +182,10 @@ def tile_mymodel_icdm_pa_t_w4_kernel(
 
         def new_part(c, pairs):
             n = PAIR * len(pairs)
-            grouped = work.tile([P, GROUPS, n, PACK], BF16, name="h_grouped", bufs=3, align_bytes=64)
-            codes = work.tile([P, GROUPS, n], U32, name="h_codes", bufs=3, align_bytes=64)
-            scales = work.tile([P, GROUPS, n], U8, name="h_scales", bufs=3, align_bytes=64)
+            grouped = work.tile([P, GROUPS, n, PACK], BF16, name="h_grouped", bufs=4, align_bytes=64)
+            part = [PAIR * pairs[0], grouped]
             for j in pairs:
-                parts[c, j] = (PAIR * pairs[0], grouped, codes, scales)
+                parts[c, j] = part
 
         def grouped_events(c, passes, events):
             first, grouped = parts[c, events.start // PAIR][:2]
@@ -216,7 +216,13 @@ def tile_mymodel_icdm_pa_t_w4_kernel(
             nc.scalar.copy(out=grouped_events(c, g, events), in_=weaves[c, g, events.start][:])
 
         def quantize_events(c, j, passes=BOTH):
-            grouped, codes, scales = parts[c, j][1:]
+            part = parts[c, j]
+            if len(part) == 2:
+                n = part[1].shape[2]
+                codes = work.tile([P, GROUPS, n], U32, name="h_codes", bufs=3, align_bytes=64)
+                scales = work.tile([P, GROUPS, n], U8, name="h_scales", bufs=3, align_bytes=64)
+                part.extend((codes, scales))
+            grouped, codes, scales = part[1:]
             nc.vector.quantize_mx(
                 out=codes[:, passes].rearrange("p g e -> p (g e)").bitcast(FP8X4),
                 scales=scales[:, passes].rearrange("p g e -> p (g e)"),
@@ -251,8 +257,8 @@ def tile_mymodel_icdm_pa_t_w4_kernel(
                 e_grouped[c] = grouped
             return e_grouped[c]
 
-        def empty_sums(c, j):
-            nc.scalar.copy(
+        def empty_sums(c, j, copy=nc.scalar.copy):
+            copy(
                 out=event_features(c)[:, 1, BANK * j : BANK * (j + 1)].rearrange("p (n t) -> p n t", t=PACK),
                 in_=sums[c, j][:].rearrange("p t n -> p n t"),
             )
@@ -269,7 +275,7 @@ def tile_mymodel_icdm_pa_t_w4_kernel(
                         nc.tensor.transpose(bank[:, j, u, :], words[:, w0 + u : w0 + PAIR : 2], identity[:])
 
         def empty_rows(halves):
-            for half in halves:
+            for half in reversed(halves):
                 c, b = divmod(half, 2)
                 words = event_features(c)[:, 0, :].bitcast(F32)[:, BANK * b : BANK * (b + 1)]
                 nc.scalar.copy(
@@ -312,7 +318,10 @@ def tile_mymodel_icdm_pa_t_w4_kernel(
                 )
 
         def new_result(key, sets):
-            result = work.tile([P, sets, OUT], F32, name="result", bufs=14)
+            if sets == PAIRS:
+                result = work.tile([P, sets, OUT], F32, name="result", bufs=14)
+            else:
+                result = work.tile([P, sets, OUT], F32, name="last_result", bufs=PAIRS + 1)
             results[key] = result
             return result
 
@@ -323,8 +332,8 @@ def tile_mymodel_icdm_pa_t_w4_kernel(
                 products[c, side] = bank
                 project(bank[:].rearrange("p j n -> p (j n)"), weight_forms(side), features(c, range(PAIRS)))
 
-        def empty_sides(c):
-            for side in range(2):
+        def empty_sides(c, sides=(1, 0)):
+            for side in sides:
                 finished = work.tile([P, PAIRS, P], F32, name="channels", bufs=3)
                 channels[c, side] = finished
                 nc.scalar.activation(out=finished[:], in_=products[c, side][:], func=RELU, bias=bias_column[:])
@@ -336,32 +345,31 @@ def tile_mymodel_icdm_pa_t_w4_kernel(
                 for j in range(PAIRS):
                     nc.tensor.transpose(bank[:, j, :], channels[c, side][:, j, :], identity[:])
 
-        def empty_channels(c):
+        def empty_channels(c, sides=(1, 0)):
             rows = out[CHUNK * c : CHUNK * (c + 1), :].rearrange("(j side i) k -> side i j k", side=2, i=P)
-            for side in range(2):
+            for side in sides:
                 nc.scalar.copy(out=new_result((c, side), PAIRS)[:], in_=turned_channels[c, side][:])
                 nc.sync.dma_start(out=rows[side], in_=results[c, side][:])
 
 
-        def project_pairs(pairs, use):
-            bank = new_bank(use, [P, 2 * len(pairs), OUT], F32)
-            products[pairs] = bank
-            for r in range(2 * len(pairs)):
+        def project_sets(sets, use):
+            bank = new_bank(use, [P, len(sets), OUT], F32)
+            products[sets] = bank
+            for i, r in enumerate(sets):
                 j, side = divmod(r, 2)
-                project(bank[:, r, :], features(LAST, pairs[j : j + 1]), weight_forms(side))
+                project(bank[:, i, :], features(LAST, (j,)), weight_forms(side))
 
-        def add_bias(pairs):
-            sets = 2 * len(pairs)
-            bias = bias_rows[:].broadcast_to([P, sets, OUT])
-            nc.vector.tensor_tensor(out=new_result(pairs, sets)[:], in0=products[pairs][:], in1=bias, op=ALU.add)
+        def add_bias(sets):
+            bias = bias_rows[:].broadcast_to([P, len(sets), OUT])
+            nc.vector.tensor_tensor(out=new_result(sets, len(sets))[:], in0=products[sets][:], in1=bias, op=ALU.add)
 
-        def rectify(pairs, engine=VECTOR):
-            result = results[pairs]
+        def rectify(sets, engine=VECTOR):
+            result = results[sets]
             if engine == SCALAR:
                 nc.scalar.activation(out=result[:], in_=result[:], func=RELU)
             else:
                 nc.vector.tensor_scalar(out=result[:], in0=result[:], scalar1=0.0, scalar2=None, op0=ALU.max)
-            rows = out[CHUNK * LAST + PAIR * pairs[0] : CHUNK * LAST + PAIR * (pairs[-1] + 1), :]
+            rows = out[CHUNK * LAST + P * sets[0] : CHUNK * LAST + P * (sets[-1] + 1), :]
             nc.sync.dma_start(out=rows.rearrange("(r i) k -> i r k", i=P), in_=result[:])
 
         h0, h1 = events_of(0, 1), events_of(2, 3)
@@ -417,96 +425,131 @@ def tile_mymodel_icdm_pa_t_w4_kernel(
         turn_rows((2, 3))
 
         rows_done = 4
-        for c in range(1, LAST):
-            final = c + 1 == LAST
-            woven = p3 if c == 1 else slice(CHUNK - WOVEN, CHUNK)
+        woven = p3
+        pending, pending_spare = range(2, 4), range(0)
+        new_part(1, (0, 1))
+        new_part(1, (2, 3))
+        for c in range(1, LAST - 1):
+            extra_rows = c in (2, 3)
+            split = CHUNK if c == 1 else SPLIT
             usual = range(rows_done, min(rows_done + 2, 2 * LAST + 2))
-            spare = range(usual.stop, usual.stop + (1 if c in (2, 3) else 0))
+            spare = range(usual.stop, usual.stop + (1 if extra_rows else 0))
             rows_done = spare.stop
             if c + AHEAD <= LAST:
                 load_bytes(c + AHEAD, 0)
                 load_bytes(c + AHEAD, 1)
                 load_rows(c + AHEAD)
-            new_part(c, (0, 1))
             interleave(c, BOTH, h0)
-            widen(SCALAR, c + 1, 0)
-            empty_sums(c - 1, 2)
-            if final:
-                widen(SCALAR, c + 1, 4, h0)
-            elif c not in (2, 3):
-                widen(SCALAR, c + 1, 4, slice(0, SPLIT))
-            empty_sums(c - 1, 3)
             if c == 1:
-                empty_rows((2, 3))
+                widen(SCALAR, c + 1, 0)
+                empty_sums(c - 1, 2)
+                empty_sums(c - 1, 3)
+                empty_rows(pending)
+                for g in range(GROUPS):
+                    weave(c, g, p3, "woven")
+                for g in range(GROUPS):
+                    empty_weave(c, g, p3)
             else:
+                empty_rows(pending)
+                empty_rows(pending_spare)
+                empty_sides(c - 2)
+                turn_channels(c - 2)
+                empty_sums(c - 1, 2)
+                widen(SCALAR, c + 1, 0)
                 empty_channels(c - 2)
-            for g in range(GROUPS):
-                weave(c, g, woven, "woven")
+                empty_sums(c - 1, 3)
             widen(VECTOR, c + 1, 7)
-            widen(VECTOR, c + 1, 6, h0 if final else WHOLE)
+            widen(VECTOR, c + 1, 6)
             quantize_events(c, 0)
-            if not final:
-                widen(VECTOR, c + 1, 5)
-            quantize_features(c - 1, WHOLE)
-            new_part(c, (2, 3))
-            for g in range(GROUPS):
-                empty_weave(c, g, woven)
+            widen(VECTOR, c + 1, 5)
+            widen(VECTOR, c + 1, 4)
+            if split < CHUNK:
+                widen(VECTOR, c + 1, 3, WHOLE if extra_rows else slice(split, CHUNK))
             widen(SCALAR, c + 1, 1)
             pool_pair(c, 0)
+            empty_sums(c, 0)
+            widen(SCALAR, c + 1, 2)
+            if not extra_rows:
+                widen(SCALAR, c + 1, 3, slice(0, split))
+            new_part(c + 1, (2, 3))
+            ahead = slice(CHUNK - (WOVEN_BESIDE_ROWS if extra_rows else WOVEN), CHUNK)
+            woven_banks = [slice(e, min(e + PAIR, CHUNK)) for e in range(ahead.start, CHUNK, PAIR)]
+            for events in woven_banks:
+                weave(c + 1, 1, events, "woven")
+            for events in reversed(woven_banks):
+                empty_weave(c + 1, 1, events)
             pool_pair(c, 1)
+            empty_sums(c, 1)
             turn_rows(usual)
+            if c == 1:
+                interleave(c, BOTH, p2)
+            else:
+                interleave(c, BOTH, slice(h1.start, woven.start))
+                interleave(c, ONLY[0], woven)
+            quantize_features(c - 1, WHOLE)
             project_sides(c - 1)
             turn_rows(spare, "woven")
-            interleave(c, BOTH, slice(h1.start, woven.start))
-            if final:
-                widen(VECTOR, c + 1, 5, h0)
-                quantize_events(c, 2, ONLY[1])
-                quantize_events(c, 2, ONLY[0])
-            else:
-                widen(VECTOR, c + 1, 3)
-                widen(VECTOR, c + 1, 4, slice(SPLIT if c not in (2, 3) else 0, CHUNK))
-                quantize_events(c, 2)
-            empty_sums(c, 0)
-            widen(SCALAR, c + 1, 2, h0 if final else WHOLE)
-            if final:
-                widen(SCALAR, c + 1, 3, h0)
-            empty_sums(c, 1)
-            empty_rows(usual)
-            empty_sides(c - 1)
-            empty_rows(spare)
-            if final:
-                for g in (1, 0):
-                    pool_nodes(c, 2, g)
-                    pool_nodes(c, 3, g, use="woven")
-            else:
-                pool_pair(c, 2)
-                pool_pair(c, 3)
-            turn_channels(c - 1)
+            pending, pending_spare, woven = usual, spare, ahead
+            quantize_events(c, 2)
+            new_part(c + 1, (0, 1))
+            pool_pair(c, 2)
+            pool_pair(c, 3)
 
-        for j in range(2):
+        c = LAST - 1
+        interleave(c, BOTH, h0)
+        widen(SCALAR, LAST, 0, h0)
+        empty_sides(c - 2)
+        turn_channels(c - 2, "woven")
+        empty_sums(c - 1, 2)
+        widen(SCALAR, LAST, 0, h1)
+        empty_sums(c - 1, 3)
+        widen(VECTOR, LAST, 7)
+        widen(VECTOR, LAST, 6)
+        quantize_events(c, 0)
+        interleave(c, BOTH, slice(h1.start, woven.start))
+        quantize_features(c - 1, WHOLE)
+        widen(VECTOR, LAST, 5)
+        interleave(c, ONLY[0], woven)
+        widen(SCALAR, LAST, 1, h0)
+        empty_channels(c - 2)
+        pool_pair(c, 0)
+        pool_pair(c, 1)
+        project_sides(c - 1)
+        widen(SCALAR, LAST, 2, h0)
+        empty_sums(c, 0)
+        widen(SCALAR, LAST, 3, h0)
+        widen(SCALAR, LAST, 4, h0)
+        empty_sums(c, 1)
+        quantize_events(c, 2, ONLY[1])
+        quantize_events(c, 2, ONLY[0])
+        empty_sides(c - 1)
+        for g in (1, 0):
+            pool_nodes(c, 2, g)
+            pool_nodes(c, 3, g)
+        turn_channels(c - 1, "woven")
+
+        for j in range(PAIRS):
             new_part(LAST, (j,))
         interleave(LAST, BOTH, p0)
         widen(SCALAR, LAST, 4, h1)
-        empty_sums(LAST - 1, 2)
-        widen(SCALAR, LAST, 5, h1)
-        empty_sums(LAST - 1, 3)
+        empty_sums(c, 2)
+        empty_sums(c, 3)
+        widen(SCALAR, LAST, 1, h1)
         widen(SCALAR, LAST, 2, h1)
-        widen(SCALAR, LAST, 3, h1)
-        empty_channels(LAST - 2)
-        quantize_features(LAST - 1, feature_columns(0, range(PAIRS)))
+        quantize_features(c, feature_columns(0, range(PAIRS)))
         quantize_events(LAST, 0)
         interleave(LAST, BOTH, p1)
-        widen(VECTOR, LAST, 6, h1)
-        quantize_features(LAST - 1, feature_columns(1, range(PAIRS)))
+        quantize_features(c, feature_columns(1, range(PAIRS)))
         quantize_events(LAST, 1)
+        empty_rows(pending)
         pool_pair(LAST, 0)
-        project_sides(LAST - 1)
+        project_sides(c)
+        empty_sides(c, (0, 1))
+        empty_channels(c - 1)
         pool_pair(LAST, 1)
-        empty_sides(LAST - 1)
-        empty_sums(LAST, 0)
         empty_sums(LAST, 1)
-        new_part(LAST, (2,))
-        new_part(LAST, (3,))
+        empty_sums(LAST, 0)
+        widen(VECTOR, LAST, 3, h1)
         interleave(LAST, ONLY[1], p2)
         interleave(LAST, ONLY[1], p3)
         quantize_events(LAST, 2, ONLY[1])
@@ -514,29 +557,31 @@ def tile_mymodel_icdm_pa_t_w4_kernel(
         quantize_events(LAST, 3, ONLY[1])
         interleave(LAST, ONLY[0], p3)
         quantize_events(LAST, 2, ONLY[0])
-        quantize_features(LAST, feature_columns(0, (0, 1)))
         quantize_events(LAST, 3, ONLY[0])
+        quantize_features(LAST, feature_columns(0, range(PAIRS)))
         quantize_features(LAST, feature_columns(1, (0, 1)))
-        quantize_features(LAST, feature_columns(0, (2, 3)))
-        turn_channels(LAST - 1)
-        pool_nodes(LAST, 2, 1, use="woven")
-        pool_nodes(LAST, 3, 1, use="woven")
+        turn_channels(c)
+        pool_nodes(LAST, 2, 1, use="products")
+        pool_nodes(LAST, 3, 1, use="products")
         pool_nodes(LAST, 2, 0)
         pool_nodes(LAST, 3, 0)
-        empty_channels(LAST - 1)
+        empty_channels(c)
         empty_sums(LAST, 2)
         empty_sums(LAST, 3)
-        project_pairs((0,), "products")
-        project_pairs((1,), "products")
+        project_sets((0, 1), "woven")
+        project_sets((2, 3), "woven")
+        add_bias((0, 1))
         quantize_features(LAST, feature_columns(1, (2,)))
-        project_pairs((2,), "sums")
-        add_bias((0,))
+        project_sets((4, 5), "sums")
         quantize_features(LAST, feature_columns(1, (3,)))
-        add_bias((1,))
-        project_pairs((3,), "sums")
-        rectify((0,), SCALAR)
-        add_bias((2,))
-        rectify((1,), SCALAR)
-        add_bias((3,))
-        rectify((2,), SCALAR)
-        rectify((3,))
+        add_bias((2, 3))
+        project_sets((6,), "sums")
+        project_sets((7,), "turned")
+        rectify((0, 1), SCALAR)
+        add_bias((4, 5))
+        rectify((2, 3), SCALAR)
+        add_bias((6,))
+        add_bias((7,))
+        rectify((4, 5), SCALAR)
+        rectify((6,))
+        rectify((7,))

@@ -35,7 +35,9 @@ AHEAD = 2
 WOVEN = 384
 WOVEN_BESIDE_ROWS = 320
 SPLIT = 256
-BANKS = {"sums": 2, "products": 2, "turned": 2, "woven": 2}
+SPLIT_BESIDE_ROWS = 0
+FIRST = 256
+BANKS = 8
 SCALAR, VECTOR = 0, 1
 RUN = 8
 
@@ -61,33 +63,31 @@ def tile_mymodel_icdm_pa_t_w4_kernel(
         plane_scales = keep.tile([P, GROUPS, PACK], F32, name="plane_scales")
         nc.scalar.dma_start(out=plane_scales[:], in_=H_A_scale.rearrange("(g p t) o -> p g (t o)", p=P, t=PACK))
 
-        ones_bf = keep.tile([P, P], BF16, name="ones_bf")
         ones = keep.tile([P, P], F32, name="ones")
         identity_bf = keep.tile([P, P], BF16, name="identity_bf")
         identity = keep.tile([P, P], F32, name="identity")
-        nc.vector.memset(ones_bf[:], 1.0)
-        nc.scalar.activation(out=ones[:], in_=ones_bf[:], func=COPY)
-        for diagonal, full in ((identity_bf, ones_bf), (identity, ones)):
-            nc.gpsimd.affine_select(
-                out=diagonal[:],
-                in_=full[:],
-                pattern=[[-1, P]],
-                compare_op=ALU.is_equal,
-                fill=0.0,
-                base=0,
-                channel_multiplier=1,
-            )
+        nc.gpsimd.memset(ones[:], 1.0)
+        nc.gpsimd.affine_select(
+            out=identity[:],
+            in_=ones[:],
+            pattern=[[-1, P]],
+            compare_op=ALU.is_equal,
+            fill=0.0,
+            base=0,
+            channel_multiplier=1,
+        )
+        nc.scalar.activation(out=identity_bf[:], in_=identity[:], func=COPY)
 
         n_blocks = 2 * PLANES + 1
         node_codes = keep.tile([P, n_blocks * QUADS], U32, name="node_codes", align_bytes=64)
         node_scales = keep.tile([P, n_blocks * QUADS], U8, name="node_scales", align_bytes=64)
-        nc.vector.memset(node_codes[:], 0)
-        nc.vector.memset(node_scales[:].bitcast(I32), 0)
 
         weight = keep.tile([P, 4, 2 * OUT], U8, name="weight", align_bytes=64)
         weight_scales = keep.tile([P, 4, OUT], U8, name="weight_scales", align_bytes=64)
         nc.vector.memset(weight[:].rearrange("p v b -> p (v b)").bitcast(I32), 0)
         nc.vector.memset(weight_scales[:].rearrange("p v n -> p (v n)").bitcast(I32), 0)
+        nc.vector.memset(node_scales[:].bitcast(I32), 0)
+        nc.vector.memset(node_codes[:], 0)
 
         bias_column = keep.tile([P, 1], BF16, name="bias_column")
         bias_rows = keep.tile([P, 1, OUT], BF16, name="bias_rows")
@@ -162,9 +162,17 @@ def tile_mymodel_icdm_pa_t_w4_kernel(
         sums, turned_rows, e_grouped, e_codes, e_scales = {}, {}, {}, {}, {}
         products, channels, turned_channels, results = {}, {}, {}, {}
 
-        def new_bank(use, shape, dtype):
-            bank = psum.tile(shape, dtype, name=use, bufs=BANKS[use])
+        free_banks, bank_numbers = list(range(BANKS)), {}
+
+        def new_bank(key, shape, dtype, skip=0):
+            number = free_banks[skip]
+            free_banks.remove(number)
+            bank_numbers[key] = number
+            bank = psum.tile(shape, dtype, name=f"bank_{number}")
             return bank
+
+        def emptied(key):
+            free_banks.append(bank_numbers[key])
 
         def widen(engine, c, plane, events=WHOLE):
             g, t = divmod(plane, PACK)
@@ -197,10 +205,10 @@ def tile_mymodel_icdm_pa_t_w4_kernel(
                 in_=wide[c][:, passes, :, events].rearrange("p g t (e i) -> p g e t i", i=RUN),
             )
 
-        def weave(c, g, events, use, places=slice(0, PACK)):
+        def weave(c, g, events, places=slice(0, PACK)):
             n = events.stop - events.start
             if (c, g, events.start) not in weaves:
-                weaves[c, g, events.start] = new_bank(use, [P, n, PACK], BF16)
+                weaves[c, g, events.start] = new_bank(("woven", c, g, events.start), [P, n, PACK], BF16)
             step = BANK // (places.stop - places.start)
             for e0 in range(0, n, step):
                 e1 = min(n, e0 + step)
@@ -214,6 +222,7 @@ def tile_mymodel_icdm_pa_t_w4_kernel(
 
         def empty_weave(c, g, events):
             nc.scalar.copy(out=grouped_events(c, g, events), in_=weaves[c, g, events.start][:])
+            emptied(("woven", c, g, events.start))
 
         def quantize_events(c, j, passes=BOTH):
             part = parts[c, j]
@@ -229,9 +238,9 @@ def tile_mymodel_icdm_pa_t_w4_kernel(
                 in_=grouped[:, passes].rearrange("p g e t -> p (g e t)"),
             )
 
-        def pool_nodes(c, j, g, opens=1, use="sums"):
+        def pool_nodes(c, j, g, opens=1, skip=0):
             if g == opens:
-                sums[c, j] = new_bank(use, [P, PACK, P], F32)
+                sums[c, j] = new_bank(("sums", c, j), [P, PACK, P], F32, skip)
             first, codes, scales = (parts[c, j][i] for i in (0, 2, 3))
             for t in range(PACK):
                 for side in range(2):
@@ -247,8 +256,8 @@ def tile_mymodel_icdm_pa_t_w4_kernel(
                         stop=(g != opens and t == PACK - 1 and side == 1),
                     )
 
-        def pool_pair(c, j, use="sums"):
-            pool_nodes(c, j, 1, use=use)
+        def pool_pair(c, j, skip=0):
+            pool_nodes(c, j, 1, skip=skip)
             pool_nodes(c, j, 0)
 
         def event_features(c):
@@ -262,12 +271,13 @@ def tile_mymodel_icdm_pa_t_w4_kernel(
                 out=event_features(c)[:, 1, BANK * j : BANK * (j + 1)].rearrange("p (n t) -> p n t", t=PACK),
                 in_=sums[c, j][:].rearrange("p t n -> p n t"),
             )
+            emptied(("sums", c, j))
 
-        def turn_rows(halves, use="turned"):
+        def turn_rows(halves):
             for half in halves:
                 c, b = divmod(half, 2)
                 words = event_rows[c][:].rearrange("p r k -> p (r k)").bitcast(F32)
-                bank = new_bank(use, [P, 2, 2, P], F32)
+                bank = new_bank(("rows", half), [P, 2, 2, P], F32, halves[-1] - half)
                 turned_rows[half] = bank
                 for j in range(2):
                     w0 = PAIR * (2 * b + j)
@@ -282,6 +292,7 @@ def tile_mymodel_icdm_pa_t_w4_kernel(
                     out=words.rearrange("p (j n u) -> p j n u", n=P, u=2),
                     in_=turned_rows[half][:].rearrange("p j u n -> p j n u"),
                 )
+                emptied(("rows", half))
 
         def feature_columns(half, pairs):
             return slice(P * (PAIRS * half + pairs[0]), P * (PAIRS * half + pairs[-1] + 1))
@@ -328,7 +339,7 @@ def tile_mymodel_icdm_pa_t_w4_kernel(
 
         def project_sides(c):
             for side in range(2):
-                bank = new_bank("products", [P, PAIRS, P], F32)
+                bank = new_bank(("products", c, side), [P, PAIRS, P], F32)
                 products[c, side] = bank
                 project(bank[:].rearrange("p j n -> p (j n)"), weight_forms(side), features(c, range(PAIRS)))
 
@@ -337,23 +348,25 @@ def tile_mymodel_icdm_pa_t_w4_kernel(
                 finished = work.tile([P, PAIRS, P], F32, name="channels", bufs=3)
                 channels[c, side] = finished
                 nc.scalar.activation(out=finished[:], in_=products[c, side][:], func=RELU, bias=bias_column[:])
+                emptied(("products", c, side))
 
-        def turn_channels(c, use="turned"):
-            for side in range(2):
-                bank = new_bank(use, [P, PAIRS, OUT], F32)
+        def turn_channels(c, sides=(0, 1)):
+            for side in sides:
+                bank = new_bank(("channels", c, side), [P, PAIRS, OUT], F32)
                 turned_channels[c, side] = bank
                 for j in range(PAIRS):
                     nc.tensor.transpose(bank[:, j, :], channels[c, side][:, j, :], identity[:])
 
-        def empty_channels(c, sides=(1, 0)):
+        def empty_channels(c, sides=(1, 0), copy=nc.scalar.copy):
             rows = out[CHUNK * c : CHUNK * (c + 1), :].rearrange("(j side i) k -> side i j k", side=2, i=P)
             for side in sides:
-                nc.scalar.copy(out=new_result((c, side), PAIRS)[:], in_=turned_channels[c, side][:])
+                copy(out=new_result((c, side), PAIRS)[:], in_=turned_channels[c, side][:])
+                emptied(("channels", c, side))
                 nc.sync.dma_start(out=rows[side], in_=results[c, side][:])
 
 
-        def project_sets(sets, use):
-            bank = new_bank(use, [P, len(sets), OUT], F32)
+        def project_sets(sets):
+            bank = new_bank(sets, [P, len(sets), OUT], F32)
             products[sets] = bank
             for i, r in enumerate(sets):
                 j, side = divmod(r, 2)
@@ -362,6 +375,7 @@ def tile_mymodel_icdm_pa_t_w4_kernel(
         def add_bias(sets):
             bias = bias_rows[:].broadcast_to([P, len(sets), OUT])
             nc.vector.tensor_tensor(out=new_result(sets, len(sets))[:], in0=products[sets][:], in1=bias, op=ALU.add)
+            emptied(sets)
 
         def rectify(sets, engine=VECTOR):
             result = results[sets]
@@ -381,14 +395,14 @@ def tile_mymodel_icdm_pa_t_w4_kernel(
         widen(SCALAR, 0, 4)
         widen(VECTOR, 0, 1)
         for pair in (p0, p1):
-            weave(0, 0, pair, "woven", low)
+            weave(0, 0, pair, low)
         widen(VECTOR, 0, 2)
         widen(SCALAR, 0, 5)
         widen(VECTOR, 0, 3)
         for pair in (p0, p1):
-            weave(0, 0, pair, "woven", high)
+            weave(0, 0, pair, high)
         for pair in (p2, p3):
-            weave(0, 0, pair, "products")
+            weave(0, 0, pair)
         widen(VECTOR, 0, 6)
         widen(SCALAR, 0, 7, h0)
         widen(SCALAR, 0, 7, h1)
@@ -420,9 +434,9 @@ def tile_mymodel_icdm_pa_t_w4_kernel(
         empty_sums(0, 1)
         for plane, events in ((7, WHOLE), (6, WHOLE), (5, WHOLE), (4, WHOLE), (3, h1)):
             widen(VECTOR, 1, plane, events)
-        pool_pair(0, 2, "products")
-        pool_pair(0, 3, "products")
+        pool_pair(0, 2)
         turn_rows((2, 3))
+        pool_pair(0, 3)
 
         rows_done = 4
         woven = p3
@@ -431,7 +445,7 @@ def tile_mymodel_icdm_pa_t_w4_kernel(
         new_part(1, (2, 3))
         for c in range(1, LAST - 1):
             extra_rows = c in (2, 3)
-            split = CHUNK if c == 1 else SPLIT
+            split = CHUNK if c == 1 else SPLIT_BESIDE_ROWS if extra_rows else SPLIT
             usual = range(rows_done, min(rows_done + 2, 2 * LAST + 2))
             spare = range(usual.stop, usual.stop + (1 if extra_rows else 0))
             rows_done = spare.stop
@@ -446,7 +460,7 @@ def tile_mymodel_icdm_pa_t_w4_kernel(
                 empty_sums(c - 1, 3)
                 empty_rows(pending)
                 for g in range(GROUPS):
-                    weave(c, g, p3, "woven")
+                    weave(c, g, p3)
                 for g in range(GROUPS):
                     empty_weave(c, g, p3)
             else:
@@ -462,24 +476,26 @@ def tile_mymodel_icdm_pa_t_w4_kernel(
             widen(VECTOR, c + 1, 6)
             quantize_events(c, 0)
             widen(VECTOR, c + 1, 5)
-            widen(VECTOR, c + 1, 4)
+            widen(VECTOR, c + 1, 4, slice(FIRST if c == 1 else 0, CHUNK))
             if split < CHUNK:
-                widen(VECTOR, c + 1, 3, WHOLE if extra_rows else slice(split, CHUNK))
+                widen(VECTOR, c + 1, 3, slice(split, CHUNK))
             widen(SCALAR, c + 1, 1)
             pool_pair(c, 0)
-            empty_sums(c, 0)
             widen(SCALAR, c + 1, 2)
-            if not extra_rows:
+            if split:
                 widen(SCALAR, c + 1, 3, slice(0, split))
+            if c == 1 and FIRST:
+                widen(SCALAR, c + 1, 4, slice(0, FIRST))
             new_part(c + 1, (2, 3))
             ahead = slice(CHUNK - (WOVEN_BESIDE_ROWS if extra_rows else WOVEN), CHUNK)
             woven_banks = [slice(e, min(e + PAIR, CHUNK)) for e in range(ahead.start, CHUNK, PAIR)]
             for events in woven_banks:
-                weave(c + 1, 1, events, "woven")
-            for events in reversed(woven_banks):
-                empty_weave(c + 1, 1, events)
+                weave(c + 1, 1, events)
             pool_pair(c, 1)
             empty_sums(c, 1)
+            empty_sums(c, 0)
+            for events in woven_banks:
+                empty_weave(c + 1, 1, events)
             turn_rows(usual)
             if c == 1:
                 interleave(c, BOTH, p2)
@@ -488,18 +504,18 @@ def tile_mymodel_icdm_pa_t_w4_kernel(
                 interleave(c, ONLY[0], woven)
             quantize_features(c - 1, WHOLE)
             project_sides(c - 1)
-            turn_rows(spare, "woven")
+            turn_rows(spare)
             pending, pending_spare, woven = usual, spare, ahead
             quantize_events(c, 2)
             new_part(c + 1, (0, 1))
-            pool_pair(c, 2)
+            pool_pair(c, 2, skip=1)
             pool_pair(c, 3)
 
         c = LAST - 1
         interleave(c, BOTH, h0)
         widen(SCALAR, LAST, 0, h0)
         empty_sides(c - 2)
-        turn_channels(c - 2, "woven")
+        turn_channels(c - 2)
         empty_sums(c - 1, 2)
         widen(SCALAR, LAST, 0, h1)
         empty_sums(c - 1, 3)
@@ -526,7 +542,7 @@ def tile_mymodel_icdm_pa_t_w4_kernel(
         for g in (1, 0):
             pool_nodes(c, 2, g)
             pool_nodes(c, 3, g)
-        turn_channels(c - 1, "woven")
+        turn_channels(c - 1)
 
         for j in range(PAIRS):
             new_part(LAST, (j,))
@@ -561,22 +577,23 @@ def tile_mymodel_icdm_pa_t_w4_kernel(
         quantize_features(LAST, feature_columns(0, range(PAIRS)))
         quantize_features(LAST, feature_columns(1, (0, 1)))
         turn_channels(c)
-        pool_nodes(LAST, 2, 1, use="products")
-        pool_nodes(LAST, 3, 1, use="products")
+        pool_nodes(LAST, 2, 1)
+        pool_nodes(LAST, 3, 1)
         pool_nodes(LAST, 2, 0)
         pool_nodes(LAST, 3, 0)
-        empty_channels(c)
+        empty_channels(c, (1,))
+        empty_channels(c, (0,), nc.vector.tensor_copy)
         empty_sums(LAST, 2)
         empty_sums(LAST, 3)
-        project_sets((0, 1), "woven")
-        project_sets((2, 3), "woven")
+        project_sets((0, 1))
+        project_sets((2, 3))
         add_bias((0, 1))
         quantize_features(LAST, feature_columns(1, (2,)))
-        project_sets((4, 5), "sums")
+        project_sets((4, 5))
         quantize_features(LAST, feature_columns(1, (3,)))
         add_bias((2, 3))
-        project_sets((6,), "sums")
-        project_sets((7,), "turned")
+        project_sets((6,))
+        project_sets((7,))
         rectify((0, 1), SCALAR)
         add_bias((4, 5))
         rectify((2, 3), SCALAR)

@@ -63,20 +63,22 @@ def tile_mymodel_icdm_pa_t_w4_kernel(
         plane_scales = keep.tile([P, GROUPS, PACK], F32, name="plane_scales")
         nc.scalar.dma_start(out=plane_scales[:], in_=H_A_scale.rearrange("(g p t) o -> p g (t o)", p=P, t=PACK))
 
+        ones_bf = keep.tile([P, P], BF16, name="ones_bf")
         ones = keep.tile([P, P], F32, name="ones")
         identity_bf = keep.tile([P, P], BF16, name="identity_bf")
         identity = keep.tile([P, P], F32, name="identity")
-        nc.gpsimd.memset(ones[:], 1.0)
-        nc.gpsimd.affine_select(
-            out=identity[:],
-            in_=ones[:],
-            pattern=[[-1, P]],
-            compare_op=ALU.is_equal,
-            fill=0.0,
-            base=0,
-            channel_multiplier=1,
-        )
-        nc.scalar.activation(out=identity_bf[:], in_=identity[:], func=COPY)
+        nc.vector.memset(ones_bf[:], 1.0)
+        nc.scalar.activation(out=ones[:], in_=ones_bf[:], func=COPY)
+        for diagonal, full in ((identity_bf, ones_bf), (identity, ones)):
+            nc.gpsimd.affine_select(
+                out=diagonal[:],
+                in_=full[:],
+                pattern=[[-1, P]],
+                compare_op=ALU.is_equal,
+                fill=0.0,
+                base=0,
+                channel_multiplier=1,
+            )
 
         n_blocks = 2 * PLANES + 1
         node_codes = keep.tile([P, n_blocks * QUADS], U32, name="node_codes", align_bytes=64)

@@ -437,8 +437,8 @@ def tile_mymodel_icdm_pa_t_w4_kernel(
         for plane, events in ((7, WHOLE), (6, WHOLE), (5, WHOLE), (4, WHOLE), (3, h1)):
             widen(VECTOR, 1, plane, events)
         pool_pair(0, 2)
-        turn_rows((2, 3))
         pool_pair(0, 3)
+        turn_rows((2, 3))
 
         rows_done = 4
         woven = p3
@@ -475,8 +475,8 @@ def tile_mymodel_icdm_pa_t_w4_kernel(
                 empty_channels(c - 2)
                 empty_sums(c - 1, 3)
             widen(VECTOR, c + 1, 7)
-            widen(VECTOR, c + 1, 6)
             quantize_events(c, 0)
+            widen(VECTOR, c + 1, 6)
             widen(VECTOR, c + 1, 5)
             widen(VECTOR, c + 1, 4, slice(FIRST if c == 1 else 0, CHUNK))
             if split < CHUNK:
@@ -522,8 +522,8 @@ def tile_mymodel_icdm_pa_t_w4_kernel(
         widen(SCALAR, LAST, 0, h1)
         empty_sums(c - 1, 3)
         widen(VECTOR, LAST, 7)
-        widen(VECTOR, LAST, 6)
         quantize_events(c, 0)
+        widen(VECTOR, LAST, 6)
         interleave(c, BOTH, slice(h1.start, woven.start))
         quantize_features(c - 1, WHOLE)
         widen(VECTOR, LAST, 5)

@@ -32,11 +32,11 @@ BOTH = slice(0, GROUPS)
 ONLY = [slice(g, g + 1) for g in range(GROUPS)]
 
 AHEAD = 2
-WOVEN = 384
-WOVEN_BESIDE_ROWS = 320
-SPLIT = 256
+WOVEN = 400
+WOVEN_BESIDE_ROWS = 352
+SPLIT = 192
 SPLIT_BESIDE_ROWS = 0
-FIRST = 256
+FIRST = 384
 BANKS = 8
 SCALAR, VECTOR = 0, 1
 RUN = 8
@@ -559,41 +559,39 @@ def tile_mymodel_icdm_pa_t_w4_kernel(
         interleave(LAST, BOTH, p1)
         quantize_features(c, feature_columns(1, range(PAIRS)))
         quantize_events(LAST, 1)
-        empty_rows(pending)
+        empty_channels(c - 1)
         pool_pair(LAST, 0)
         project_sides(c)
         empty_sides(c, (0, 1))
-        empty_channels(c - 1)
+        empty_rows(pending)
         pool_pair(LAST, 1)
         empty_sums(LAST, 1)
         empty_sums(LAST, 0)
         widen(VECTOR, LAST, 3, h1)
         interleave(LAST, ONLY[1], p2)
-        interleave(LAST, ONLY[1], p3)
-        quantize_events(LAST, 2, ONLY[1])
         interleave(LAST, ONLY[0], p2)
-        quantize_events(LAST, 3, ONLY[1])
-        interleave(LAST, ONLY[0], p3)
+        quantize_events(LAST, 2, ONLY[1])
+        interleave(LAST, ONLY[1], p3)
         quantize_events(LAST, 2, ONLY[0])
+        interleave(LAST, ONLY[0], p3)
+        quantize_events(LAST, 3, ONLY[1])
         quantize_events(LAST, 3, ONLY[0])
         quantize_features(LAST, feature_columns(0, range(PAIRS)))
         quantize_features(LAST, feature_columns(1, (0, 1)))
         turn_channels(c)
-        pool_nodes(LAST, 2, 1)
-        pool_nodes(LAST, 3, 1)
-        pool_nodes(LAST, 2, 0)
-        pool_nodes(LAST, 3, 0)
+        pool_pair(LAST, 2)
+        pool_pair(LAST, 3)
         empty_channels(c, (1,))
-        empty_channels(c, (0,), nc.vector.tensor_copy)
         empty_sums(LAST, 2)
+        empty_channels(c, (0,))
         empty_sums(LAST, 3)
         project_sets((0, 1))
         project_sets((2, 3))
-        add_bias((0, 1))
         quantize_features(LAST, feature_columns(1, (2,)))
+        add_bias((0, 1))
         project_sets((4, 5))
-        quantize_features(LAST, feature_columns(1, (3,)))
         add_bias((2, 3))
+        quantize_features(LAST, feature_columns(1, (3,)))
         project_sets((6,))
         project_sets((7,))
         rectify((0, 1), SCALAR)

@@ -37,6 +37,7 @@ WOVEN_BESIDE_ROWS = 352
 SPLIT = 192
 SPLIT_BESIDE_ROWS = 0
 FIRST = 384
+CUT = 240
 BANKS = 8
 SCALAR, VECTOR = 0, 1
 RUN = 8
@@ -203,8 +204,8 @@ def tile_mymodel_icdm_pa_t_w4_kernel(
 
         def interleave(c, passes, events):
             nc.vector.tensor_copy(
-                out=grouped_events(c, passes, events).rearrange("p g (e i) t -> p g e t i", i=RUN),
-                in_=wide[c][:, passes, :, events].rearrange("p g t (e i) -> p g e t i", i=RUN),
+                out=grouped_events(c, passes, events).rearrange("p g (e i) t -> p e g t i", i=RUN),
+                in_=wide[c][:, passes, :, events].rearrange("p g t (e i) -> p e g t i", i=RUN),
             )
 
         def weave(c, g, events, places=slice(0, PACK)):
@@ -455,7 +456,8 @@ def tile_mymodel_icdm_pa_t_w4_kernel(
                 load_bytes(c + AHEAD, 0)
                 load_bytes(c + AHEAD, 1)
                 load_rows(c + AHEAD)
-            interleave(c, BOTH, h0)
+            interleave(c, BOTH, slice(0, CUT))
+            interleave(c, BOTH, slice(CUT, h0.stop))
             if c == 1:
                 widen(SCALAR, c + 1, 0)
                 empty_sums(c - 1, 2)
@@ -514,7 +516,8 @@ def tile_mymodel_icdm_pa_t_w4_kernel(
             pool_pair(c, 3)
 
         c = LAST - 1
-        interleave(c, BOTH, h0)
+        interleave(c, BOTH, slice(0, CUT))
+        interleave(c, BOTH, slice(CUT, h0.stop))
         widen(SCALAR, LAST, 0, h0)
         empty_sides(c - 2)
         turn_channels(c - 2)

from contextlib import ExitStack

import concourse.mybir as mybir

F32 = mybir.dt.float32
BF16 = mybir.dt.bfloat16
U32 = mybir.dt.uint32
I32 = mybir.dt.int32
U8 = mybir.dt.uint8
FP8 = mybir.dt.float8_e4m3fn
FP8X4 = mybir.dt.float8_e4m3fn_x4
FP4X4 = mybir.dt.float4_e2m1fn_x4
ALU = mybir.AluOpType
COPY = mybir.ActivationFunctionType.Copy
RELU = mybir.ActivationFunctionType.Relu

NODES, EVENTS, HIDDEN, OUT = 1024, 8192, 256, 128

P = 128
PACK = 4
PASS = P * PACK
GROUPS = NODES // PASS
PLANES = GROUPS * PACK
PAIR = 2 * P
QUADS = HIDDEN // PACK
BANK = 512
PAIRS = 4
CHUNK = PAIRS * PAIR
LAST = EVENTS // CHUNK - 1
WHOLE = slice(0, CHUNK)
BOTH = slice(0, GROUPS)
ONLY = [slice(g, g + 1) for g in range(GROUPS)]

AHEAD = 2
WOVEN = 400
WOVEN_BESIDE_ROWS = 352
SPLIT = 192
SPLIT_BESIDE_ROWS = 0
FIRST = 384
CUT = 240
BANKS = 8
SCALAR, VECTOR = 0, 1
RUN = 8

FLOPS = 2 * NODES * EVENTS * HIDDEN + 2 * EVENTS * 2 * HIDDEN * OUT


def events_of(first, last):
    return slice(PAIR * first, PAIR * (last + 1))


def tile_mymodel_icdm_pa_t_w4_kernel(
    tc, H_A_bytes, H_A_scale, H_mean_A, H_mean_M, wEA1_words, wEA1_scales, bEA1, out
):
    nc = tc.nc

    with ExitStack() as ctx:
        keep = ctx.enter_context(tc.tile_pool(name="keep", bufs=1))
        work = ctx.enter_context(tc.tile_pool(name="work", bufs=2))
        psum = ctx.enter_context(tc.psum_pool(name="psum", bufs=1))
        ctx.enter_context(tc.manual_schedule())


        plane_scales = keep.tile([P, GROUPS, PACK], F32, name="plane_scales")
        nc.scalar.dma_start(out=plane_scales[:], in_=H_A_scale.rearrange("(g p t) o -> p g (t o)", p=P, t=PACK))

        ones_bf = keep.tile([P, P], BF16, name="ones_bf")
        ones = keep.tile([P, P], F32, name="ones")
        identity_bf = keep.tile([P, P], BF16, name="identity_bf")
        identity = keep.tile([P, P], F32, name="identity")
        nc.vector.memset(ones_bf[:], 1.0)
        nc.scalar.activation(out=ones[:], in_=ones_bf[:], func=COPY)
        for diagonal, full in ((identity_bf, ones_bf), (identity, ones)):
            nc.gpsimd.affine_select(
                out=diagonal[:],
                in_=full[:],
                pattern=[[-1, P]],
                compare_op=ALU.is_equal,
                fill=0.0,
                base=0,
                channel_multiplier=1,
            )

        n_blocks = 2 * PLANES + 1
        node_codes = keep.tile([P, n_blocks * QUADS], U32, name="node_codes", align_bytes=64)
        node_scales = keep.tile([P, n_blocks * QUADS], U8, name="node_scales", align_bytes=64)

        weight = keep.tile([P, 4, 2 * OUT], U8, name="weight", align_bytes=64)
        weight_scales = keep.tile([P, 4, OUT], U8, name="weight_scales", align_bytes=64)
        nc.vector.memset(weight[:].rearrange("p v b -> p (v b)").bitcast(I32), 0)
        nc.vector.memset(weight_scales[:].rearrange("p v n -> p (v n)").bitcast(I32), 0)
        nc.vector.memset(node_scales[:].bitcast(I32), 0)
        nc.vector.memset(node_codes[:], 0)

        bias_column = keep.tile([P, 1], BF16, name="bias_column")
        bias_rows = keep.tile([P, 1, OUT], BF16, name="bias_rows")


        event_bytes = {}
        event_rows = {}

        def load_bytes(c, g, places=slice(0, PACK)):
            if (c, g) not in event_bytes:
                raw = work.tile([P, PACK, CHUNK], U8, name="event_bytes", bufs=GROUPS * (AHEAD + 2) - 1, align_bytes=64)
                event_bytes[c, g] = raw
            source = H_A_bytes[PASS * g : PASS * (g + 1), CHUNK * c : CHUNK * (c + 1)]
            nc.sync.dma_start(
                out=event_bytes[c, g][:, places, :], in_=source.rearrange("(p t) e -> p t e", t=PACK)[:, places, :]
            )

        def load_rows(c):
            rows = work.tile([P, CHUNK // P, HIDDEN], BF16, name="event_rows", bufs=AHEAD + 2, align_bytes=64)
            event_rows[c] = rows
            source = H_mean_M[CHUNK * c : CHUNK * (c + 1), :]
            nc.sync.dma_start(out=rows[:], in_=source.rearrange("(r i) k -> i r k", i=P))

        for plane in (0, 4, 1, 2, 5, 3, 6, 7):
            g, t = divmod(plane, PACK)
            load_bytes(0, g, slice(t, t + 1))
        node_rows = {}
        for g in (1, 0):
            rows = keep.tile([P, PACK, HIDDEN], BF16, name=f"node_rows_{g}", align_bytes=64)
            node_rows[g] = rows
            nc.sync.dma_start(out=rows[:], in_=H_mean_A.rearrange("(g p j) c -> g p j c", p=P, j=PACK)[g])
        load_bytes(1, 0)
        load_rows(0)
        load_bytes(1, 1)
        load_rows(1)
        load_bytes(2, 0)
        load_bytes(2, 1)
        word_halves = wEA1_words[0].rearrange("(h p) b -> p h b", h=2).bitcast(I32)
        scale_quadrants = wEA1_scales[0].rearrange("(h r b) n -> r b h n", h=2, r=2)
        for side in range(2):
            forms = slice(2 * side, 2 * side + 2)
            nc.sync.dma_start(out=weight[QUADS * side : QUADS * (side + 1), forms, :].bitcast(I32), in_=word_halves)
        for quadrant in range(4):
            side, r = divmod(quadrant, 2)
            forms = slice(2 * side, 2 * side + 2)
            nc.sync.dma_start(
                out=weight_scales[32 * quadrant : 32 * quadrant + 4, forms, :].bitcast(I32),
                in_=scale_quadrants[r].bitcast(I32),
            )
        nc.sync.dma_start(out=bias_column[:], in_=bEA1.rearrange("(c o) -> c o", o=1))
        load_rows(2)
        nc.sync.dma_start(out=bias_rows[:, 0, :], in_=bEA1.partition_broadcast(P))


        node_grouped = keep.tile([P, GROUPS, PACK, QUADS, PACK], BF16, name="node_grouped", align_bytes=64)

        def group_nodes(g, copy):
            copy(out=node_grouped[:, g], in_=node_rows[g][:].rearrange("p j (q t) -> p t q j", t=PACK))

        def quantize_nodes(g):
            for t in range(PACK):
                plane = PACK * g + t
                block = slice((2 * plane + 1) * QUADS, (2 * plane + 2) * QUADS)
                nc.vector.quantize_mx(
                    out=node_codes[:, block].bitcast(FP8X4),
                    scales=node_scales[:, block],
                    in_=node_grouped[:, g, t].rearrange("p q j -> p (q j)"),
                )


        wide, weaves, parts = {}, {}, {}
        sums, turned_rows, e_grouped, e_codes, e_scales = {}, {}, {}, {}, {}
        products, channels, turned_channels, results = {}, {}, {}, {}

        free_banks, bank_numbers = list(range(BANKS)), {}

        def new_bank(key, shape, dtype, skip=0):
            number = free_banks[skip]
            free_banks.remove(number)
            bank_numbers[key] = number
            bank = psum.tile(shape, dtype, name=f"bank_{number}")
            return bank

        def emptied(key):
            free_banks.append(bank_numbers[key])

        def widen(engine, c, plane, events=WHOLE):
            g, t = divmod(plane, PACK)
            if c not in wide:
                planes = work.tile([P, GROUPS, PACK, CHUNK], BF16, name="wide", bufs=3, align_bytes=64)
                wide[c] = planes
            values = event_bytes[c, g][:, t, events].bitcast(FP8)
            scale = plane_scales[:, g, t : t + 1]
            if engine == SCALAR:
                nc.scalar.activation(out=wide[c][:, g, t, events], in_=values, func=COPY, scale=scale)
            else:
                nc.vector.tensor_scalar(
                    out=wide[c][:, g, t, events], in0=values, scalar1=scale, scalar2=None, op0=ALU.mult
                )

        def new_part(c, pairs):
            n = PAIR * len(pairs)
            grouped = work.tile([P, GROUPS, n, PACK], BF16, name="h_grouped", bufs=4, align_bytes=64)
            part = [PAIR * pairs[0], grouped]
            for j in pairs:
                parts[c, j] = part

        def grouped_events(c, passes, events):
            first, grouped = parts[c, events.start // PAIR][:2]
            return grouped[:, passes, events.start - first : events.stop - first, :]

        def interleave(c, passes, events):
            nc.vector.tensor_copy(
                out=grouped_events(c, passes, events).rearrange("p g (e i) t -> p e g t i", i=RUN),
                in_=wide[c][:, passes, :, events].rearrange("p g t (e i) -> p e g t i", i=RUN),
            )

        def weave(c, g, events, places=slice(0, PACK)):
            n = events.stop - events.start
            if (c, g, events.start) not in weaves:
                weaves[c, g, events.start] = new_bank(("woven", c, g, events.start), [P, n, PACK], BF16)
            step = BANK // (places.stop - places.start)
            for e0 in range(0, n, step):
                e1 = min(n, e0 + step)
                nc.tensor.matmul(
                    out=weaves[c, g, events.start][:, e0:e1, places].rearrange("p e t -> p t e"),
                    lhsT=identity_bf[:],
                    rhs=wide[c][:, g, places, events.start + e0 : events.start + e1],
                    start=True,
                    stop=True,
                )

        def empty_weave(c, g, events):
            nc.scalar.copy(out=grouped_events(c, g, events), in_=weaves[c, g, events.start][:])
            emptied(("woven", c, g, events.start))

        def quantize_events(c, j, passes=BOTH):
            part = parts[c, j]
            if len(part) == 2:
                n = part[1].shape[2]
                codes = work.tile([P, GROUPS, n], U32, name="h_codes", bufs=3, align_bytes=64)
                scales = work.tile([P, GROUPS, n], U8, name="h_scales", bufs=3, align_bytes=64)
                part.extend((codes, scales))
            grouped, codes, scales = part[1:]
            nc.vector.quantize_mx(
                out=codes[:, passes].rearrange("p g e -> p (g e)").bitcast(FP8X4),
                scales=scales[:, passes].rearrange("p g e -> p (g e)"),
                in_=grouped[:, passes].rearrange("p g e t -> p (g e t)"),
            )

        def pool_nodes(c, j, g, opens=1, skip=0):
            if g == opens:
                sums[c, j] = new_bank(("sums", c, j), [P, PACK, P], F32, skip)
            first, codes, scales = (parts[c, j][i] for i in (0, 2, 3))
            for t in range(PACK):
                for side in range(2):
                    e0 = PAIR * j + P * side - first
                    c0 = (2 * (PACK * g + t) + 1 - side) * QUADS
                    nc.tensor.matmul_mx(
                        out=sums[c, j][:, t, :],
                        lhsT=node_codes[:, c0 : c0 + P].bitcast(FP8X4),
                        lhsT_scale=node_scales[:, c0 : c0 + P],
                        rhs=codes[:, g, e0 : e0 + P].bitcast(FP8X4),
                        rhs_scale=scales[:, g, e0 : e0 + P],
                        start=(g == opens and t == 0 and side == 0),
                        stop=(g != opens and t == PACK - 1 and side == 1),
                    )

        def pool_pair(c, j, skip=0):
            pool_nodes(c, j, 1, skip=skip)
            pool_nodes(c, j, 0)

        def event_features(c):
            if c not in e_grouped:
                grouped = work.tile([P, 2, PACK * P * PAIRS], BF16, name="e_grouped", bufs=4, align_bytes=64)
                e_grouped[c] = grouped
            return e_grouped[c]

        def empty_sums(c, j, copy=nc.scalar.copy):
            copy(
                out=event_features(c)[:, 1, BANK * j : BANK * (j + 1)].rearrange("p (n t) -> p n t", t=PACK),
                in_=sums[c, j][:].rearrange("p t n -> p n t"),
            )
            emptied(("sums", c, j))

        def turn_rows(halves):
            for half in halves:
                c, b = divmod(half, 2)
                words = event_rows[c][:].rearrange("p r k -> p (r k)").bitcast(F32)
                bank = new_bank(("rows", half), [P, 2, 2, P], F32, halves[-1] - half)
                turned_rows[half] = bank
                for j in range(2):
                    w0 = PAIR * (2 * b + j)
                    for u in range(2):
                        nc.tensor.transpose(bank[:, j, u, :], words[:, w0 + u : w0 + PAIR : 2], identity[:])

        def empty_rows(halves):
            for half in reversed(halves):
                c, b = divmod(half, 2)
                words = event_features(c)[:, 0, :].bitcast(F32)[:, BANK * b : BANK * (b + 1)]
                nc.scalar.copy(
                    out=words.rearrange("p (j n u) -> p j n u", n=P, u=2),
                    in_=turned_rows[half][:].rearrange("p j u n -> p j n u"),
                )
                emptied(("rows", half))

        def feature_columns(half, pairs):
            return slice(P * (PAIRS * half + pairs[0]), P * (PAIRS * half + pairs[-1] + 1))

        def quantize_features(c, columns):
            if c not in e_codes:
                codes = work.tile([P, CHUNK], U32, name="e_codes", bufs=2, align_bytes=64)
                scales = work.tile([P, CHUNK], U8, name="e_scales", bufs=2, align_bytes=64)
                e_codes[c], e_scales[c] = codes, scales
            nc.vector.quantize_mx(
                out=e_codes[c][:, columns].bitcast(FP8X4),
                scales=e_scales[c][:, columns],
                in_=e_grouped[c][:].rearrange("p h (n t) -> p (h n) t", t=PACK)[:, columns].rearrange("p n t -> p (n t)"),
            )

        def weight_forms(side):
            forms = (2 * side, 2 * side + 1)
            return [(weight[:, form, :].bitcast(FP4X4), weight_scales[:, form, :]) for form in forms]

        def features(c, pairs):
            columns = [feature_columns(half, pairs) for half in range(2)]
            return [(e_codes[c][:, part].bitcast(FP8X4), e_scales[c][:, part]) for part in columns]

        def project(to, still, moving):
            for half in range(2):
                nc.tensor.matmul_mx(
                    out=to,
                    lhsT=still[half][0],
                    lhsT_scale=still[half][1],
                    rhs=moving[half][0],
                    rhs_scale=moving[half][1],
                    start=(half == 0),
                    stop=(half == 1),
                )

        def new_result(key, sets):
            if sets == PAIRS:
                result = work.tile([P, sets, OUT], F32, name="result", bufs=14)
            else:
                result = work.tile([P, sets, OUT], F32, name="last_result", bufs=PAIRS + 1)
            results[key] = result
            return result


        def project_sides(c):
            for side in range(2):
                bank = new_bank(("products", c, side), [P, PAIRS, P], F32)
                products[c, side] = bank
                project(bank[:].rearrange("p j n -> p (j n)"), weight_forms(side), features(c, range(PAIRS)))

        def empty_sides(c, sides=(1, 0)):
            for side in sides:
                finished = work.tile([P, PAIRS, P], F32, name="channels", bufs=3)
                channels[c, side] = finished
                nc.scalar.activation(out=finished[:], in_=products[c, side][:], func=RELU, bias=bias_column[:])
                emptied(("products", c, side))

        def turn_channels(c, sides=(0, 1)):
            for side in sides:
                bank = new_bank(("channels", c, side), [P, PAIRS, OUT], F32)
                turned_channels[c, side] = bank
                for j in range(PAIRS):
                    nc.tensor.transpose(bank[:, j, :], channels[c, side][:, j, :], identity[:])

        def empty_channels(c, sides=(1, 0), copy=nc.scalar.copy):
            rows = out[CHUNK * c : CHUNK * (c + 1), :].rearrange("(j side i) k -> side i j k", side=2, i=P)
            for side in sides:
                copy(out=new_result((c, side), PAIRS)[:], in_=turned_channels[c, side][:])
                emptied(("channels", c, side))
                nc.sync.dma_start(out=rows[side], in_=results[c, side][:])


        def project_sets(sets):
            bank = new_bank(sets, [P, len(sets), OUT], F32)
            products[sets] = bank
            for i, r in enumerate(sets):
                j, side = divmod(r, 2)
                project(bank[:, i, :], features(LAST, (j,)), weight_forms(side))

        def add_bias(sets):
            bias = bias_rows[:].broadcast_to([P, len(sets), OUT])
            nc.vector.tensor_tensor(out=new_result(sets, len(sets))[:], in0=products[sets][:], in1=bias, op=ALU.add)
            emptied(sets)

        def rectify(sets, engine=VECTOR):
            result = results[sets]
            if engine == SCALAR:
                nc.scalar.activation(out=result[:], in_=result[:], func=RELU)
            else:
                nc.vector.tensor_scalar(out=result[:], in0=result[:], scalar1=0.0, scalar2=None, op0=ALU.max)
            rows = out[CHUNK * LAST + P * sets[0] : CHUNK * LAST + P * (sets[-1] + 1), :]
            nc.sync.dma_start(out=rows.rearrange("(r i) k -> i r k", i=P), in_=result[:])

        h0, h1 = events_of(0, 1), events_of(2, 3)
        p0, p1, p2, p3 = (events_of(j, j) for j in range(PAIRS))
        low, high = slice(0, 2), slice(2, 4)
        new_part(0, (0, 1))
        new_part(0, (2, 3))
        widen(VECTOR, 0, 0)
        widen(SCALAR, 0, 4)
        widen(VECTOR, 0, 1)
        for pair in (p0, p1):
            weave(0, 0, pair, low)
        widen(VECTOR, 0, 2)
        widen(SCALAR, 0, 5)
        widen(VECTOR, 0, 3)
        for pair in (p0, p1):
            weave(0, 0, pair, high)
        for pair in (p2, p3):
            weave(0, 0, pair)
        widen(VECTOR, 0, 6)
        widen(SCALAR, 0, 7, h0)
        widen(SCALAR, 0, 7, h1)
        group_nodes(1, nc.vector.tensor_copy)
        interleave(0, ONLY[1], h0)
        group_nodes(0, nc.scalar.copy)
        empty_weave(0, 0, p0)
        empty_weave(0, 0, p1)
        quantize_nodes(1)
        quantize_events(0, 0, ONLY[1])
        interleave(0, ONLY[1], h1)
        empty_weave(0, 0, p2)
        widen(SCALAR, 1, 0, h0)
        empty_weave(0, 0, p3)
        quantize_events(0, 0, ONLY[0])
        quantize_nodes(0)
        for j in range(2):
            pool_nodes(0, j, 1)
        turn_rows((0, 1))
        for j in range(2):
            pool_nodes(0, j, 0)
        widen(VECTOR, 1, 3, h0)
        quantize_events(0, 2)
        widen(SCALAR, 1, 0, h1)
        widen(SCALAR, 1, 1)
        widen(SCALAR, 1, 2)
        empty_sums(0, 0)
        empty_rows((0, 1))
        empty_sums(0, 1)
        for plane, events in ((7, WHOLE), (6, WHOLE), (5, WHOLE), (4, WHOLE), (3, h1)):
            widen(VECTOR, 1, plane, events)
        pool_pair(0, 2)
        pool_pair(0, 3)
        turn_rows((2, 3))

        rows_done = 4
        woven = p3
        pending, pending_spare = range(2, 4), range(0)
        new_part(1, (0, 1))
        new_part(1, (2, 3))
        for c in range(1, LAST - 1):
            extra_rows = c in (2, 3)
            split = CHUNK if c == 1 else SPLIT_BESIDE_ROWS if extra_rows else SPLIT
            usual = range(rows_done, min(rows_done + 2, 2 * LAST + 2))
            spare = range(usual.stop, usual.stop + (1 if extra_rows else 0))
            rows_done = spare.stop
            if c + AHEAD <= LAST:
                load_bytes(c + AHEAD, 0)
                load_bytes(c + AHEAD, 1)
                load_rows(c + AHEAD)
            interleave(c, BOTH, slice(0, CUT))
            interleave(c, BOTH, slice(CUT, h0.stop))
            if c == 1:
                widen(SCALAR, c + 1, 0)
                empty_sums(c - 1, 2)
                empty_sums(c - 1, 3)
                empty_rows(pending)
                for g in range(GROUPS):
                    weave(c, g, p3)
                for g in range(GROUPS):
                    empty_weave(c, g, p3)
            else:
                empty_rows(pending)
                empty_rows(pending_spare)
                empty_sides(c - 2)
                turn_channels(c - 2)
                empty_sums(c - 1, 2)
                widen(SCALAR, c + 1, 0)
                empty_channels(c - 2)
                empty_sums(c - 1, 3)
            widen(VECTOR, c + 1, 7)
            quantize_events(c, 0)
            widen(VECTOR, c + 1, 6)
            widen(VECTOR, c + 1, 5)
            widen(VECTOR, c + 1, 4, slice(FIRST if c == 1 else 0, CHUNK))
            if split < CHUNK:
                widen(VECTOR, c + 1, 3, slice(split, CHUNK))
            widen(SCALAR, c + 1, 1)
            pool_pair(c, 0)
            widen(SCALAR, c + 1, 2)
            if split:
                widen(SCALAR, c + 1, 3, slice(0, split))
            if c == 1 and FIRST:
                widen(SCALAR, c + 1, 4, slice(0, FIRST))
            new_part(c + 1, (2, 3))
            ahead = slice(CHUNK - (WOVEN_BESIDE_ROWS if extra_rows else WOVEN), CHUNK)
            woven_banks = [slice(e, min(e + PAIR, CHUNK)) for e in range(ahead.start, CHUNK, PAIR)]
            for events in woven_banks:
                weave(c + 1, 1, events)
            pool_pair(c, 1)
            empty_sums(c, 1)
            empty_sums(c, 0)
            for events in woven_banks:
                empty_weave(c + 1, 1, events)
            turn_rows(usual)
            if c == 1:
                interleave(c, BOTH, p2)
            else:
                interleave(c, BOTH, slice(h1.start, woven.start))
                interleave(c, ONLY[0], woven)
            quantize_features(c - 1, WHOLE)
            project_sides(c - 1)
            turn_rows(spare)
            pending, pending_spare, woven = usual, spare, ahead
            quantize_events(c, 2)
            new_part(c + 1, (0, 1))
            pool_pair(c, 2, skip=1)
            pool_pair(c, 3)

        c = LAST - 1
        interleave(c, BOTH, slice(0, CUT))
        interleave(c, BOTH, slice(CUT, h0.stop))
        widen(SCALAR, LAST, 0, h0)
        empty_sides(c - 2)
        turn_channels(c - 2)
        empty_sums(c - 1, 2)
        widen(SCALAR, LAST, 0, h1)
        empty_sums(c - 1, 3)
        widen(VECTOR, LAST, 7)
        quantize_events(c, 0)
        widen(VECTOR, LAST, 6)
        interleave(c, BOTH, slice(h1.start, woven.start))
        quantize_features(c - 1, WHOLE)
        widen(VECTOR, LAST, 5)
        interleave(c, ONLY[0], woven)
        widen(SCALAR, LAST, 1, h0)
        empty_channels(c - 2)
        pool_pair(c, 0)
        pool_pair(c, 1)
        project_sides(c - 1)
        widen(SCALAR, LAST, 2, h0)
        empty_sums(c, 0)
        widen(SCALAR, LAST, 3, h0)
        widen(SCALAR, LAST, 4, h0)
        empty_sums(c, 1)
        quantize_events(c, 2, ONLY[1])
        quantize_events(c, 2, ONLY[0])
        empty_sides(c - 1)
        for g in (1, 0):
            pool_nodes(c, 2, g)
            pool_nodes(c, 3, g)
        turn_channels(c - 1)

        for j in range(PAIRS):
            new_part(LAST, (j,))
        interleave(LAST, BOTH, p0)
        widen(SCALAR, LAST, 4, h1)
        empty_sums(c, 2)
        empty_sums(c, 3)
        widen(SCALAR, LAST, 1, h1)
        widen(SCALAR, LAST, 2, h1)
        quantize_features(c, feature_columns(0, range(PAIRS)))
        quantize_events(LAST, 0)
        interleave(LAST, BOTH, p1)
        quantize_features(c, feature_columns(1, range(PAIRS)))
        quantize_events(LAST, 1)
        empty_channels(c - 1)
        pool_pair(LAST, 0)
        project_sides(c)
        empty_sides(c, (0, 1))
        empty_rows(pending)
        pool_pair(LAST, 1)
        empty_sums(LAST, 1)
        empty_sums(LAST, 0)
        widen(VECTOR, LAST, 3, h1)
        interleave(LAST, ONLY[1], p2)
        interleave(LAST, ONLY[0], p2)
        quantize_events(LAST, 2, ONLY[1])
        interleave(LAST, ONLY[1], p3)
        quantize_events(LAST, 2, ONLY[0])
        interleave(LAST, ONLY[0], p3)
        quantize_events(LAST, 3, ONLY[1])
        quantize_events(LAST, 3, ONLY[0])
        quantize_features(LAST, feature_columns(0, range(PAIRS)))
        quantize_features(LAST, feature_columns(1, (0, 1)))
        turn_channels(c)
        pool_pair(LAST, 2)
        pool_pair(LAST, 3)
        empty_channels(c, (1,))
        empty_sums(LAST, 2)
        empty_channels(c, (0,))
        empty_sums(LAST, 3)
        project_sets((0, 1))
        project_sets((2, 3))
        quantize_features(LAST, feature_columns(1, (2,)))
        add_bias((0, 1))
        project_sets((4, 5))
        add_bias((2, 3))
        quantize_features(LAST, feature_columns(1, (3,)))
        project_sets((6,))
        project_sets((7,))
        rectify((0, 1), SCALAR)
        add_bias((4, 5))
        rectify((2, 3), SCALAR)
        add_bias((6,))
        add_bias((7,))
        rectify((4, 5), SCALAR)
        rectify((6,))
        rectify((7,))
